import numpy as np
import ml_dtypes


def mxq(x, axis, fmt="e4m3"):
    dtype, down = {"e4m3": (ml_dtypes.float8_e4m3fn, 7), "e5m2": (ml_dtypes.float8_e5m2, 14)}[fmt]
    v = np.moveaxis(np.asarray(x, np.float32).astype(ml_dtypes.bfloat16).astype(np.float64), axis, -1)
    blocks = v.reshape(v.shape[:-1] + (-1, 32))
    amax = np.abs(blocks).max(-1, keepdims=True)
    byte = np.maximum(np.where(amax > 0, np.frexp(amax)[1] - 1 + 127, 0) - down, 1)
    scale = np.exp2(byte - 127.0)
    codes = (blocks / scale).astype(np.float32).astype(dtype).astype(np.float64)
    return np.moveaxis((codes * scale).reshape(v.shape), -1, axis)


WIDE = False


def mx_kscale(k):
    if not WIDE:
        return np.ones(k)
    levels = np.array([10, -10, 5, -5, 0])
    a = np.random.permutation(np.resize(levels, k // 512 * 4)).reshape(k // 512, 4)
    idx = np.arange(k)
    return np.exp2(a[idx // 512, idx % 128 // 32])


BF16 = ml_dtypes.bfloat16


def bf(x):
    return np.asarray(x, np.float32).astype(BF16)


def f64(x):
    return np.asarray(x).astype(np.float64)


B, T, C, H = 1, 2048, 512, 2
D = C // H


def softmax(a):
    e = np.exp(a - a.max(-1, keepdims=True))
    return e / e.sum(-1, keepdims=True)


def heads(a):
    return a.reshape(B, T, H, D).transpose(0, 2, 1, 3)


def setup_inputs():
    u = np.array(mx_kscale(T), dtype=np.float64)
    u[:D] = u.min()
    u = u / u.min()
    q = np.random.standard_normal((B, T, C)) * 1.5
    k = np.random.standard_normal((B, T, C)) * 1.5
    v = np.random.standard_normal((B, T, C)) * u[None, :, None]
    q[:, :, ::D] = np.sqrt(D)
    k[:, :, ::D] -= np.log(u)[None, :, None]
    return {"q": bf(q), "k": bf(k), "v": bf(v),
            "alpha": bf((1.0 + 0.1 * np.random.standard_normal(1)) / u.max()),
            "beta": bf(1.0 + 0.1 * np.random.standard_normal(1)),
            "gamma": bf((1.0 + 0.1 * np.random.standard_normal(1)) / u.max())}


def reference(q, k, v, alpha, beta, gamma):
    qh, kh, vh = heads(f64(q)), heads(f64(k)), heads(f64(v))
    att = (qh @ kh.transpose(0, 1, 3, 2)) * (1.0 / np.sqrt(D))
    causal = np.tril(np.ones((T, T), dtype=bool))
    att = np.where(causal, att, -1e20)
    att = f64(beta) * softmax(att)
    eye = np.eye(T)
    M = np.triu(np.ones((T, T)), k=1)
    MC = softmax(1e20 * M)
    att = att + f64(alpha) * eye - f64(gamma) * MC
    y = mxq(att, 3, "e4m3") @ mxq(vh, 2, "e4m3")
    return y.transpose(0, 2, 1, 3).reshape(B, T, C)

@@ -1,0 +1,411 @@
+from contextlib import ExitStack
+
+import concourse.mybir as mybir
+from concourse.masks import make_identity
+
+F32 = mybir.dt.float32
+BF16 = mybir.dt.bfloat16
+I32 = mybir.dt.int32
+U32 = mybir.dt.uint32
+U8 = mybir.dt.uint8
+FP8X4 = mybir.dt.float8_e4m3fn_x4
+ALU = mybir.AluOpType
+ACT = mybir.ActivationFunctionType
+AXIS = mybir.AxisListType
+
+P = 128
+T = 2048
+HEADS = 2
+D = 256
+C = HEADS * D
+TILES = T // P
+PACK = 4
+K_PASS = P * PACK
+PASSES = T // K_PASS
+TILES_PER_PASS = K_PASS // P
+HALF = T // 2
+TILE_COLS = P // 2
+PASS_COLS = K_PASS // 2
+D_BLOCKS = C // P
+MASKED = -1.0e30
+U_TILES = TILES - TILES_PER_PASS
+
+FLOPS = 2 * 2 * T * T * D * HEADS
+
+
+def tile_causalshapedattention_pa_kernel(tc, q, k, v, alpha, beta, gamma, out):
+    nc = tc.nc
+    q_rows = q.flatten_outer_dims()
+    k_rows = k.flatten_outer_dims()
+    v_rows = v.flatten_outer_dims()
+    out_rows = out.flatten_outer_dims()
+
+    with ExitStack() as ctx:
+        keep = ctx.enter_context(tc.tile_pool(name="keep", bufs=1))
+        wide = ctx.enter_context(tc.tile_pool(name="wide", bufs=2))
+        stats = ctx.enter_context(tc.tile_pool(name="stats", bufs=6))
+        score_pool = ctx.enter_context(tc.tile_pool(name="scores", bufs=5))
+        a_pool = ctx.enter_context(tc.tile_pool(name="a", bufs=3))
+        grouped_pool = ctx.enter_context(tc.tile_pool(name="grouped", bufs=4))
+        code_pool = ctx.enter_context(tc.tile_pool(name="codes", bufs=10))
+        out_pool = ctx.enter_context(tc.tile_pool(name="out", bufs=3))
+        psum_scores = ctx.enter_context(tc.psum_pool(name="psum_scores", bufs=3))
+        psum_turn = ctx.enter_context(tc.psum_pool(name="psum_turn", bufs=3))
+        psum_out = ctx.enter_context(tc.psum_pool(name="psum_out", bufs=2))
+
+        q_sb = keep.tile([P, TILES, C], BF16)
+        k_sb = keep.tile([P, TILES, C], BF16)
+        q_view = q_rows.rearrange("(t p) c -> p t c", p=P)
+        k_view = k_rows.rearrange("(t p) c -> p t c", p=P)
+        v_raw = keep.tile([P, PASSES, PACK, C], BF16)
+
+        alpha_bf = keep.tile([P, 1], BF16)
+        beta_bf = keep.tile([P, 1], BF16)
+        gamma_bf = keep.tile([P, 1], BF16)
+        nc.scalar.dma_start(out=gamma_bf[:], in_=gamma.partition_broadcast(P))
+        nc.scalar.dma_start(out=alpha_bf[:], in_=alpha.partition_broadcast(P))
+        nc.scalar.dma_start(out=beta_bf[:], in_=beta.partition_broadcast(P))
+
+        def load_tiles(dst, src, first):
+            tiles = slice(first, first + TILES_PER_PASS)
+            nc.sync.dma_start(out=dst[:, tiles, :], in_=src[:, tiles, :])
+
+        load_tiles(q_sb, q_view, TILES - TILES_PER_PASS)
+        for g in range(PASSES):
+            load_tiles(k_sb, k_view, g * TILES_PER_PASS)
+        nc.sync.dma_start(
+            out=v_raw[:].rearrange("p g t c -> p g (t c)"),
+            in_=v_rows.rearrange("(g p t) c -> p g (t c)", p=P, t=PACK),
+        )
+        for g in range(PASSES - 2, -1, -1):
+            load_tiles(q_sb, q_view, g * TILES_PER_PASS)
+
+        ident_bf = keep.tile([P, P], BF16)
+        make_identity(nc, ident_bf[:])
+        ident_f = keep.tile([P, P], F32)
+        make_identity(nc, ident_f[:])
+        above = keep.tile([P, P], F32)
+        nc.gpsimd.memset(above[:], 0.0)
+        nc.gpsimd.affine_select(
+            out=above[:],
+            in_=above[:],
+            compare_op=ALU.is_ge,
+            fill=1.0,
+            base=0,
+            pattern=[[-1, P]],
+            channel_multiplier=1,
+        )
+        left_i = keep.tile([P, TILES], I32)
+        nc.gpsimd.iota(left_i[:], pattern=[[-P, TILES]], base=T - 1, channel_multiplier=-1)
+        ones_bf = keep.tile([P, 2 * HEADS, PASS_COLS - TILE_COLS], BF16)
+        nc.gpsimd.memset(ones_bf[:], 1.0)
+
+        def halves(square):
+            return square.rearrange("p (m u e) -> p u m e", u=2, e=2)
+
+        def in_halves(square):
+            return square.rearrange("p (u m e) -> p u m e", u=2, e=2)
+
+        ident_halves_f = keep.tile([P, P], F32)
+        nc.vector.tensor_copy(out=in_halves(ident_halves_f[:]), in_=halves(ident_f[:]))
+        ident_halves_bf = keep.tile([P, P], BF16)
+        nc.vector.tensor_copy(out=ident_halves_bf[:], in_=ident_halves_f[:])
+        above_halves = keep.tile([P, P], F32)
+        nc.vector.tensor_copy(out=in_halves(above_halves[:]), in_=halves(above[:]))
+        masked_bf = keep.tile([P, P], BF16)
+        nc.vector.tensor_scalar(
+            out=masked_bf[:], in0=above_halves[:], scalar1=MASKED, scalar2=None, op0=ALU.mult
+        )
+
+        alpha_f = keep.tile([P, 1], F32)
+        beta_f = keep.tile([P, 1], F32)
+        gamma_f = keep.tile([P, 1], F32)
+        nc.vector.tensor_copy(out=gamma_f[:], in_=gamma_bf[:])
+        nc.vector.tensor_copy(out=alpha_f[:], in_=alpha_bf[:])
+        nc.vector.tensor_copy(out=beta_f[:], in_=beta_bf[:])
+
+        left = keep.tile([P, TILES], F32)
+        nc.vector.tensor_copy(out=left[:], in_=left_i[:])
+        is_last = keep.tile([P, TILES], F32)
+        nc.vector.tensor_scalar(
+            out=is_last[:], in0=left[:], scalar1=0.0, scalar2=None, op0=ALU.is_equal
+        )
+        count = keep.tile([P, TILES], F32)
+        nc.vector.scalar_tensor_tensor(
+            out=count[:], in0=is_last[:], scalar=float(T), in1=left[:], op0=ALU.mult, op1=ALU.add
+        )
+        share = keep.tile([P, TILES], F32)
+        nc.vector.reciprocal(out=share[:], in_=count[:])
+        mc_above = keep.tile([P, TILES], F32)
+        nc.vector.tensor_scalar(
+            out=mc_above[:],
+            in0=share[:],
+            scalar1=gamma_f[:, 0:1],
+            scalar2=-1.0,
+            op0=ALU.mult,
+            op1=ALU.mult,
+        )
+        mc_below = keep.tile([P, TILES], F32)
+        nc.vector.tensor_tensor(out=mc_below[:], in0=mc_above[:], in1=is_last[:], op=ALU.mult)
+
+        alpha_eye = keep.tile([P, P], F32)
+        nc.vector.tensor_scalar(
+            out=alpha_eye[:], in0=ident_halves_f[:], scalar1=alpha_f[:, 0:1], scalar2=None, op0=ALU.mult
+        )
+        diag_add = keep.tile([P, TILES, P], F32)
+        nc.vector.tensor_tensor(
+            out=diag_add[:],
+            in0=above_halves[:].unsqueeze(1).to_broadcast([P, TILES, P]),
+            in1=mc_above[:].unsqueeze(2).to_broadcast([P, TILES, P]),
+            op=ALU.mult,
+        )
+        nc.vector.tensor_tensor(
+            out=diag_add[:],
+            in0=diag_add[:],
+            in1=alpha_eye[:].unsqueeze(1).to_broadcast([P, TILES, P]),
+            op=ALU.add,
+        )
+        nc.vector.tensor_scalar(
+            out=diag_add[:, TILES - 1, :],
+            in0=diag_add[:, TILES - 1, :],
+            scalar1=mc_below[:, TILES - 1 : TILES],
+            scalar2=None,
+            op0=ALU.add,
+        )
+
+        q_t = keep.tile([P, D_BLOCKS, T], BF16)
+        k_t = keep.tile([P, D_BLOCKS, 2, HALF], BF16)
+
+        def turn_q(t):
+            turned = psum_turn.tile([P, D_BLOCKS, P], BF16, tag="turn")
+            for b in range(D_BLOCKS):
+                nc.tensor.transpose(turned[:, b, :], q_sb[:, t, b * P : (b + 1) * P], ident_bf[:])
+            nc.scalar.copy(out=q_t[:, :, t * P : (t + 1) * P], in_=turned[:])
+
+        def turn_k(t):
+            turned = psum_turn.tile([P, D_BLOCKS, P], BF16, tag="turn")
+            for b in range(D_BLOCKS):
+                nc.tensor.transpose(
+                    turned[:, b, :], k_sb[:, t, b * P : (b + 1) * P], ident_halves_bf[:]
+                )
+            nc.scalar.copy(
+                out=k_t[:, :, :, t * TILE_COLS : (t + 1) * TILE_COLS],
+                in_=turned[:].rearrange("p b (u x) -> p b u x", u=2),
+            )
+
+        turn_q(TILES - 1)
+        for t in range(TILES):
+            turn_k(t)
+
+        v_codes = keep.tile([P, PASSES, C], U32, align_bytes=64)
+        v_scales = keep.tile([P, PASSES, C], U8, align_bytes=64)
+        for g in range(PASSES):
+            v_grouped = wide.tile([P, C, PACK], BF16, tag="wide", align_bytes=64)
+            nc.gpsimd.tensor_scalar(
+                out=v_grouped[:],
+                in0=v_raw[:, g].rearrange("p t c -> p c t"),
+                scalar1=1.0,
+                scalar2=0.0,
+                op0=ALU.mult,
+                op1=ALU.add,
+            )
+            nc.vector.quantize_mx(
+                out=v_codes[:, g, :].bitcast(FP8X4),
+                scales=v_scales[:, g, :],
+                in_=v_grouped[:].rearrange("p c t -> p (c t)"),
+            )
+
+        mc_above_bf = keep.tile([P, TILES], BF16)
+        nc.vector.tensor_copy(out=mc_above_bf[:], in_=mc_above[:])
+        u_codes = keep.tile([P, U_TILES * P], U32, align_bytes=64)
+        u_scales = keep.tile([P, U_TILES * P], U8, align_bytes=64)
+        for first in range(0, U_TILES, TILES_PER_PASS):
+            spread = psum_scores.tile([P, K_PASS], F32, tag="scores")
+            for j in range(TILES_PER_PASS):
+                nc.tensor.matmul(
+                    out=spread[:, j * P : (j + 1) * P],
+                    lhsT=mc_above_bf[:, first + j : first + j + 1].to_broadcast([P, P]),
+                    rhs=ident_bf[:],
+                    start=True,
+                    stop=True,
+                )
+            u_grouped = wide.tile([P, K_PASS, PACK], BF16, tag="wide", align_bytes=64)
+            nc.scalar.copy(
+                out=u_grouped[:], in_=spread[:].unsqueeze(2).to_broadcast([P, K_PASS, PACK])
+            )
+            cols = slice(first * P, first * P + K_PASS)
+            nc.vector.quantize_mx(
+                out=u_codes[:, cols].bitcast(FP8X4),
+                scales=u_scales[:, cols],
+                in_=u_grouped[:].rearrange("p q t -> p (q t)"),
+            )
+
+        exps = {}
+        sums = {}
+        a_tiles = {}
+        a_codes = {}
+
+        def scores(qi):
+            last_pass = qi // TILES_PER_PASS
+            before = (qi % TILES_PER_PASS) * TILE_COLS
+            q_cols = slice(qi * P, (qi + 1) * P)
+            row_sum = stats.tile([P, HEADS], F32, tag="row_sum")
+            neg_max = stats.tile([P, HEADS], F32, tag="neg_max")
+            sums[qi] = row_sum
+            for h in range(HEADS):
+                e = score_pool.tile([P, 2, HALF], F32, tag="e")
+                exps[(qi, h)] = e
+                pass_max = stats.tile([P, PASSES], F32, tag="pass_max")
+                for g in range(last_pass + 1):
+                    s_ps = psum_scores.tile([P, 2, PASS_COLS], F32, tag="scores")
+                    first = g * PASS_COLS
+                    width = PASS_COLS if g < last_pass else before
+                    if width > 0:
+                        for b in range(2):
+                            nc.tensor.matmul(
+                                out=s_ps[:, :, :width],
+                                lhsT=q_t[:, 2 * h + b, q_cols],
+                                rhs=k_t[:, 2 * h + b, :, first : first + width],
+                                start=(b == 0),
+                                stop=(b == 1),
+                            )
+                    if g == last_pass:
+                        diag = slice(before, before + TILE_COLS)
+                        for b in range(2):
+                            nc.tensor.matmul(
+                                out=s_ps[:, :, diag],
+                                lhsT=q_t[:, 2 * h + b, q_cols],
+                                rhs=k_t[:, 2 * h + b, :, qi * TILE_COLS : (qi + 1) * TILE_COLS],
+                                start=(b == 0),
+                                stop=False,
+                            )
+                        nc.tensor.matmul(
+                            out=s_ps[:, :, diag],
+                            lhsT=ident_bf[:],
+                            rhs=masked_bf[:].rearrange("p (u x) -> p u x", u=2),
+                            start=False,
+                            stop=True,
+                        )
+                        width = before + TILE_COLS
+                    nc.vector.tensor_scalar(
+                        out=e[:, :, first : first + width],
+                        in0=s_ps[:, :, :width],
+                        scalar1=1.0 / 16.0,
+                        scalar2=None,
+                        op0=ALU.mult,
+                        op1=ALU.max,
+                        accum_out=pass_max[:, g : g + 1],
+                    )
+                nc.vector.tensor_reduce(
+                    out=neg_max[:, h : h + 1],
+                    in_=pass_max[:, : last_pass + 1],
+                    axis=AXIS.X,
+                    op=ALU.max,
+                    negate=True,
+                )
+                seen = (qi + 1) * TILE_COLS
+                nc.scalar.activation(
+                    out=e[:, :, :seen],
+                    in_=e[:, :, :seen],
+                    func=ACT.Exp,
+                    bias=neg_max[:, h : h + 1],
+                    scale=1.0,
+                    accum_out=row_sum[:, h : h + 1],
+                )
+
+        def weights(qi):
+            below = qi * TILE_COLS
+            seen = below + TILE_COLS
+            end = (qi // TILES_PER_PASS + 1) * PASS_COLS
+            inv_sum = stats.tile([P, HEADS], F32, tag="inv_sum")
+            nc.vector.reciprocal(out=inv_sum[:], in_=sums[qi][:])
+            gain = stats.tile([P, HEADS], F32, tag="gain")
+            nc.vector.tensor_scalar(
+                out=gain[:], in0=inv_sum[:], scalar1=beta_f[:, 0:1], scalar2=None, op0=ALU.mult
+            )
+            a = a_pool.tile([P, 2 * HEADS, HALF], BF16, tag="a", align_bytes=64)
+            a_tiles[qi] = a
+            for h in range(HEADS):
+                e = exps[(qi, h)]
+                if below > 0:
+                    nc.scalar.activation(
+                        out=a[:, 2 * h : 2 * h + 2, :below],
+                        in_=e[:, :, :below],
+                        func=ACT.Identity,
+                        bias=mc_below[:, qi : qi + 1],
+                        scale=gain[:, h : h + 1],
+                    )
+                nc.vector.scalar_tensor_tensor(
+                    out=a[:, 2 * h : 2 * h + 2, below:seen],
+                    in0=e[:, :, below:seen],
+                    scalar=gain[:, h : h + 1],
+                    in1=diag_add[:, qi, :].rearrange("p (u x) -> p u x", u=2),
+                    op0=ALU.mult,
+                    op1=ALU.add,
+                )
+            if end > seen:
+                nc.gpsimd.tensor_scalar(
+                    out=a[:, :, seen:end],
+                    in0=ones_bf[:, :, : end - seen],
+                    scalar1=mc_above[:, qi : qi + 1],
+                    scalar2=0.0,
+                    op0=ALU.mult,
+                    op1=ALU.add,
+                )
+
+        def turn_and_quantise(qi):
+            a_words = a_tiles[qi][:].bitcast(F32)
+            a_codes[qi] = []
+            for g in range(qi // TILES_PER_PASS + 1):
+                turned = psum_turn.tile([P, HEADS, 2, P], F32, tag="turn")
+                for h in range(HEADS):
+                    for u in range(2):
+                        nc.tensor.transpose(
+                            turned[:, h, u, :], a_words[:, 2 * h + u, g * P : (g + 1) * P], ident_f[:]
+                        )
+                grouped = grouped_pool.tile([P, HEADS * P * PACK], BF16, tag="grouped", align_bytes=64)
+                nc.vector.tensor_copy(
+                    out=grouped[:].bitcast(F32).rearrange("p (h x u) -> p h x u", h=HEADS, u=2),
+                    in_=turned[:].rearrange("p h u x -> p h x u"),
+                )
+                codes = code_pool.tile([P, HEADS * P], U32, tag="codes", align_bytes=64)
+                scales = code_pool.tile([P, HEADS * P], U8, tag="scales", align_bytes=64)
+                nc.vector.quantize_mx(out=codes[:].bitcast(FP8X4), scales=scales[:], in_=grouped[:])
+                a_codes[qi].append((codes, scales))
+
+        def attend(qi):
+            o_ps = psum_out.tile([P, HEADS, D], F32, tag="o")
+            for h in range(HEADS):
+                for g in range(PASSES):
+                    if g < len(a_codes[qi]):
+                        codes, scales = a_codes[qi][g]
+                        lhs_codes = codes[:, h * P : (h + 1) * P]
+                        lhs_scales = scales[:, h * P : (h + 1) * P]
+                    else:
+                        lhs_codes = u_codes[:, qi * P : (qi + 1) * P]
+                        lhs_scales = u_scales[:, qi * P : (qi + 1) * P]
+                    nc.tensor.matmul_mx(
+                        out=o_ps[:, h, :],
+                        lhsT=lhs_codes.bitcast(FP8X4),
+                        lhsT_scale=lhs_scales,
+                        rhs=v_codes[:, g, h * D : (h + 1) * D].bitcast(FP8X4),
+                        rhs_scale=v_scales[:, g, h * D : (h + 1) * D],
+                        start=(g == 0),
+                        stop=(g == PASSES - 1),
+                    )
+            o_sb = out_pool.tile([P, C], F32, tag="o_sb")
+            nc.scalar.copy(out=o_sb[:], in_=o_ps[:].rearrange("p h d -> p (h d)"))
+            nc.sync.dma_start(out=out_rows[qi * P : (qi + 1) * P, :], in_=o_sb[:])
+
+        order = list(range(TILES - 1, -1, -1))
+        for step in range(TILES + 3):
+            if step + 1 < TILES:
+                turn_q(order[step + 1])
+            if step < TILES:
+                scores(order[step])
+            if 0 <= step - 1 < TILES:
+                weights(order[step - 1])
+            if 0 <= step - 2 < TILES:
+                turn_and_quantise(order[step - 2])
+            if 0 <= step - 3 < TILES:
+                attend(order[step - 3])

@@ -29,6 +29,7 @@ PASS_COLS = K_PASS // 2
 D_BLOCKS = C // P
 MASKED = -1.0e30
 U_TILES = TILES - TILES_PER_PASS
+VECTOR_SHARE = 4
 
 FLOPS = 2 * 2 * T * T * D * HEADS
 
@@ -46,12 +47,12 @@ def tile_causalshapedattention_pa_kernel(tc, q, k, v, alpha, beta, gamma, out):
         stats = ctx.enter_context(tc.tile_pool(name="stats", bufs=6))
         score_pool = ctx.enter_context(tc.tile_pool(name="scores", bufs=5))
         a_pool = ctx.enter_context(tc.tile_pool(name="a", bufs=3))
-        grouped_pool = ctx.enter_context(tc.tile_pool(name="grouped", bufs=4))
+        grouped_pool = ctx.enter_context(tc.tile_pool(name="grouped", bufs=3))
         code_pool = ctx.enter_context(tc.tile_pool(name="codes", bufs=10))
         out_pool = ctx.enter_context(tc.tile_pool(name="out", bufs=3))
         psum_scores = ctx.enter_context(tc.psum_pool(name="psum_scores", bufs=3))
-        psum_turn = ctx.enter_context(tc.psum_pool(name="psum_turn", bufs=3))
-        psum_out = ctx.enter_context(tc.psum_pool(name="psum_out", bufs=2))
+        psum_turn = ctx.enter_context(tc.psum_pool(name="psum_turn", bufs=4))
+        psum_out = ctx.enter_context(tc.psum_pool(name="psum_out", bufs=1))
 
         q_sb = keep.tile([P, TILES, C], BF16)
         k_sb = keep.tile([P, TILES, C], BF16)
@@ -80,6 +81,10 @@ def tile_causalshapedattention_pa_kernel(tc, q, k, v, alpha, beta, gamma, out):
         for g in range(PASSES - 2, -1, -1):
             load_tiles(q_sb, q_view, g * TILES_PER_PASS)
 
+        warm = keep.tile([P, 1], F32)
+        nc.vector.memset(warm[:], 0.0)
+        nc.scalar.activation(out=warm[:], in_=warm[:], func=ACT.Exp)
+
         ident_bf = keep.tile([P, P], BF16)
         make_identity(nc, ident_bf[:])
         ident_f = keep.tile([P, P], F32)
@@ -100,29 +105,22 @@ def tile_causalshapedattention_pa_kernel(tc, q, k, v, alpha, beta, gamma, out):
         ones_bf = keep.tile([P, 2 * HEADS, PASS_COLS - TILE_COLS], BF16)
         nc.gpsimd.memset(ones_bf[:], 1.0)
 
-        def halves(square):
+        def natural(square):
             return square.rearrange("p (m u e) -> p u m e", u=2, e=2)
 
         def in_halves(square):
             return square.rearrange("p (u m e) -> p u m e", u=2, e=2)
 
         ident_halves_f = keep.tile([P, P], F32)
-        nc.vector.tensor_copy(out=in_halves(ident_halves_f[:]), in_=halves(ident_f[:]))
+        nc.vector.tensor_copy(out=in_halves(ident_halves_f[:]), in_=natural(ident_f[:]))
         ident_halves_bf = keep.tile([P, P], BF16)
         nc.vector.tensor_copy(out=ident_halves_bf[:], in_=ident_halves_f[:])
         above_halves = keep.tile([P, P], F32)
-        nc.vector.tensor_copy(out=in_halves(above_halves[:]), in_=halves(above[:]))
+        nc.vector.tensor_copy(out=in_halves(above_halves[:]), in_=natural(above[:]))
         masked_bf = keep.tile([P, P], BF16)
         nc.vector.tensor_scalar(
             out=masked_bf[:], in0=above_halves[:], scalar1=MASKED, scalar2=None, op0=ALU.mult
         )
-
-        alpha_f = keep.tile([P, 1], F32)
-        beta_f = keep.tile([P, 1], F32)
-        gamma_f = keep.tile([P, 1], F32)
-        nc.vector.tensor_copy(out=gamma_f[:], in_=gamma_bf[:])
-        nc.vector.tensor_copy(out=alpha_f[:], in_=alpha_bf[:])
-        nc.vector.tensor_copy(out=beta_f[:], in_=beta_bf[:])
 
         left = keep.tile([P, TILES], F32)
         nc.vector.tensor_copy(out=left[:], in_=left_i[:])
@@ -136,6 +134,10 @@ def tile_causalshapedattention_pa_kernel(tc, q, k, v, alpha, beta, gamma, out):
         )
         share = keep.tile([P, TILES], F32)
         nc.vector.reciprocal(out=share[:], in_=count[:])
+        alpha_f = keep.tile([P, 1], F32)
+        beta_f = keep.tile([P, 1], F32)
+        gamma_f = keep.tile([P, 1], F32)
+        nc.vector.tensor_copy(out=gamma_f[:], in_=gamma_bf[:])
         mc_above = keep.tile([P, TILES], F32)
         nc.vector.tensor_scalar(
             out=mc_above[:],
@@ -145,32 +147,37 @@ def tile_causalshapedattention_pa_kernel(tc, q, k, v, alpha, beta, gamma, out):
             op0=ALU.mult,
             op1=ALU.mult,
         )
-        mc_below = keep.tile([P, TILES], F32)
-        nc.vector.tensor_tensor(out=mc_below[:], in0=mc_above[:], in1=is_last[:], op=ALU.mult)
-
+        nc.vector.tensor_copy(out=alpha_f[:], in_=alpha_bf[:])
         alpha_eye = keep.tile([P, P], F32)
         nc.vector.tensor_scalar(
             out=alpha_eye[:], in0=ident_halves_f[:], scalar1=alpha_f[:, 0:1], scalar2=None, op0=ALU.mult
         )
+        mc_below = keep.tile([P, TILES], F32)
+        nc.vector.tensor_tensor(out=mc_below[:], in0=mc_above[:], in1=is_last[:], op=ALU.mult)
+        mc_above_bf = keep.tile([P, TILES], BF16)
+        nc.vector.tensor_copy(out=mc_above_bf[:], in_=mc_above[:])
+        nc.vector.tensor_copy(out=beta_f[:], in_=beta_bf[:])
+
         diag_add = keep.tile([P, TILES, P], F32)
-        nc.vector.tensor_tensor(
+        nc.gpsimd.tensor_tensor(
             out=diag_add[:],
             in0=above_halves[:].unsqueeze(1).to_broadcast([P, TILES, P]),
             in1=mc_above[:].unsqueeze(2).to_broadcast([P, TILES, P]),
             op=ALU.mult,
         )
-        nc.vector.tensor_tensor(
+        nc.gpsimd.tensor_tensor(
             out=diag_add[:],
             in0=diag_add[:],
             in1=alpha_eye[:].unsqueeze(1).to_broadcast([P, TILES, P]),
             op=ALU.add,
         )
-        nc.vector.tensor_scalar(
+        nc.gpsimd.tensor_scalar(
             out=diag_add[:, TILES - 1, :],
             in0=diag_add[:, TILES - 1, :],
-            scalar1=mc_below[:, TILES - 1 : TILES],
-            scalar2=None,
-            op0=ALU.add,
+            scalar1=1.0,
+            scalar2=mc_below[:, TILES - 1 : TILES],
+            op0=ALU.mult,
+            op1=ALU.add,
         )
 
         q_t = keep.tile([P, D_BLOCKS, T], BF16)
@@ -188,164 +195,164 @@ def tile_causalshapedattention_pa_kernel(tc, q, k, v, alpha, beta, gamma, out):
                 nc.tensor.transpose(
                     turned[:, b, :], k_sb[:, t, b * P : (b + 1) * P], ident_halves_bf[:]
                 )
-            nc.scalar.copy(
+            copy_out = nc.scalar.copy if t % 2 == 0 else nc.vector.tensor_copy
+            copy_out(
                 out=k_t[:, :, :, t * TILE_COLS : (t + 1) * TILE_COLS],
                 in_=turned[:].rearrange("p b (u x) -> p b u x", u=2),
             )
 
-        turn_q(TILES - 1)
-        for t in range(TILES):
-            turn_k(t)
-
         v_codes = keep.tile([P, PASSES, C], U32, align_bytes=64)
         v_scales = keep.tile([P, PASSES, C], U8, align_bytes=64)
-        for g in range(PASSES):
-            v_grouped = wide.tile([P, C, PACK], BF16, tag="wide", align_bytes=64)
-            nc.gpsimd.tensor_scalar(
-                out=v_grouped[:],
-                in0=v_raw[:, g].rearrange("p t c -> p c t"),
-                scalar1=1.0,
-                scalar2=0.0,
-                op0=ALU.mult,
-                op1=ALU.add,
-            )
+        v_grouped = {}
+
+        def regroup_v(g):
+            v_grouped[g] = wide.tile([P, C, PACK], BF16, tag="wide", name="v_grouped", align_bytes=64)
+            nc.vector.tensor_copy(out=v_grouped[g][:], in_=v_raw[:, g].rearrange("p t c -> p c t"))
+
+        def quantise_v(g):
             nc.vector.quantize_mx(
                 out=v_codes[:, g, :].bitcast(FP8X4),
                 scales=v_scales[:, g, :],
-                in_=v_grouped[:].rearrange("p c t -> p (c t)"),
-            )
-
-        mc_above_bf = keep.tile([P, TILES], BF16)
-        nc.vector.tensor_copy(out=mc_above_bf[:], in_=mc_above[:])
-        u_codes = keep.tile([P, U_TILES * P], U32, align_bytes=64)
-        u_scales = keep.tile([P, U_TILES * P], U8, align_bytes=64)
-        for first in range(0, U_TILES, TILES_PER_PASS):
-            spread = psum_scores.tile([P, K_PASS], F32, tag="scores")
-            for j in range(TILES_PER_PASS):
-                nc.tensor.matmul(
-                    out=spread[:, j * P : (j + 1) * P],
-                    lhsT=mc_above_bf[:, first + j : first + j + 1].to_broadcast([P, P]),
-                    rhs=ident_bf[:],
-                    start=True,
-                    stop=True,
-                )
-            u_grouped = wide.tile([P, K_PASS, PACK], BF16, tag="wide", align_bytes=64)
-            nc.scalar.copy(
-                out=u_grouped[:], in_=spread[:].unsqueeze(2).to_broadcast([P, K_PASS, PACK])
-            )
-            cols = slice(first * P, first * P + K_PASS)
-            nc.vector.quantize_mx(
-                out=u_codes[:, cols].bitcast(FP8X4),
-                scales=u_scales[:, cols],
-                in_=u_grouped[:].rearrange("p q t -> p (q t)"),
+                in_=v_grouped[g][:].rearrange("p c t -> p (c t)"),
             )
 
         exps = {}
-        sums = {}
+        pass_maxes = {}
+        neg_maxes = {}
+        row_sums = {}
+        gains = {}
         a_tiles = {}
+        turned_a = {}
+        grouped_a = {}
         a_codes = {}
+        above_grouped = {}
+        o_tiles = {}
+        above_codes = keep.tile([P, U_TILES * P], U32, align_bytes=64)
+        above_scales = keep.tile([P, U_TILES * P], U8, align_bytes=64)
 
-        def scores(qi):
+        def own_passes(qi):
+            return range(qi // TILES_PER_PASS + 1)
+
+        def score_pass(qi, h, g):
+            if g == 0:
+                exps[(qi, h)] = score_pool.tile([P, 2, HALF], F32, tag="e", name="e")
+                pass_maxes[(qi, h)] = stats.tile([P, PASSES], F32, tag="pass_max", name="pass_max")
             last_pass = qi // TILES_PER_PASS
             before = (qi % TILES_PER_PASS) * TILE_COLS
             q_cols = slice(qi * P, (qi + 1) * P)
-            row_sum = stats.tile([P, HEADS], F32, tag="row_sum")
-            neg_max = stats.tile([P, HEADS], F32, tag="neg_max")
-            sums[qi] = row_sum
-            for h in range(HEADS):
-                e = score_pool.tile([P, 2, HALF], F32, tag="e")
-                exps[(qi, h)] = e
-                pass_max = stats.tile([P, PASSES], F32, tag="pass_max")
-                for g in range(last_pass + 1):
-                    s_ps = psum_scores.tile([P, 2, PASS_COLS], F32, tag="scores")
-                    first = g * PASS_COLS
-                    width = PASS_COLS if g < last_pass else before
-                    if width > 0:
-                        for b in range(2):
-                            nc.tensor.matmul(
-                                out=s_ps[:, :, :width],
-                                lhsT=q_t[:, 2 * h + b, q_cols],
-                                rhs=k_t[:, 2 * h + b, :, first : first + width],
-                                start=(b == 0),
-                                stop=(b == 1),
-                            )
-                    if g == last_pass:
-                        diag = slice(before, before + TILE_COLS)
-                        for b in range(2):
-                            nc.tensor.matmul(
-                                out=s_ps[:, :, diag],
-                                lhsT=q_t[:, 2 * h + b, q_cols],
-                                rhs=k_t[:, 2 * h + b, :, qi * TILE_COLS : (qi + 1) * TILE_COLS],
-                                start=(b == 0),
-                                stop=False,
-                            )
-                        nc.tensor.matmul(
-                            out=s_ps[:, :, diag],
-                            lhsT=ident_bf[:],
-                            rhs=masked_bf[:].rearrange("p (u x) -> p u x", u=2),
-                            start=False,
-                            stop=True,
-                        )
-                        width = before + TILE_COLS
-                    nc.vector.tensor_scalar(
-                        out=e[:, :, first : first + width],
-                        in0=s_ps[:, :, :width],
-                        scalar1=1.0 / 16.0,
-                        scalar2=None,
-                        op0=ALU.mult,
-                        op1=ALU.max,
-                        accum_out=pass_max[:, g : g + 1],
+            s_ps = psum_scores.tile([P, 2, PASS_COLS], F32, tag="scores")
+            first = g * PASS_COLS
+            width = PASS_COLS if g < last_pass else before
+            if width > 0:
+                for b in range(2):
+                    nc.tensor.matmul(
+                        out=s_ps[:, :, :width],
+                        lhsT=q_t[:, 2 * h + b, q_cols],
+                        rhs=k_t[:, 2 * h + b, :, first : first + width],
+                        start=(b == 0),
+                        stop=(b == 1),
                     )
-                nc.vector.tensor_reduce(
-                    out=neg_max[:, h : h + 1],
-                    in_=pass_max[:, : last_pass + 1],
-                    axis=AXIS.X,
-                    op=ALU.max,
-                    negate=True,
+            if g == last_pass:
+                diag = slice(before, before + TILE_COLS)
+                for b in range(2):
+                    nc.tensor.matmul(
+                        out=s_ps[:, :, diag],
+                        lhsT=q_t[:, 2 * h + b, q_cols],
+                        rhs=k_t[:, 2 * h + b, :, qi * TILE_COLS : (qi + 1) * TILE_COLS],
+                        start=(b == 0),
+                        stop=False,
+                    )
+                nc.tensor.matmul(
+                    out=s_ps[:, :, diag],
+                    lhsT=ident_bf[:],
+                    rhs=masked_bf[:].rearrange("p (u x) -> p u x", u=2),
+                    start=False,
+                    stop=True,
                 )
-                seen = (qi + 1) * TILE_COLS
+                width = before + TILE_COLS
+            nc.vector.tensor_scalar(
+                out=exps[(qi, h)][:, :, first : first + width],
+                in0=s_ps[:, :, :width],
+                scalar1=1.0 / 16.0,
+                scalar2=None,
+                op0=ALU.mult,
+                op1=ALU.max,
+                accum_out=pass_maxes[(qi, h)][:, g : g + 1],
+            )
+
+        def row_max(qi, h):
+            neg_maxes[(qi, h)] = stats.tile([P, 1], F32, tag="neg_max", name="neg_max")
+            nc.vector.tensor_reduce(
+                out=neg_maxes[(qi, h)][:],
+                in_=pass_maxes[(qi, h)][:, : qi // TILES_PER_PASS + 1],
+                axis=AXIS.X,
+                op=ALU.max,
+                negate=True,
+            )
+
+        def exponent(qi, h):
+            row_sums[(qi, h)] = stats.tile([P, 1], F32, tag="row_sum", name="row_sum")
+            seen = (qi + 1) * TILE_COLS
+            nc.scalar.activation(
+                out=exps[(qi, h)][:, :, :seen],
+                in_=exps[(qi, h)][:, :, :seen],
+                func=ACT.Exp,
+                bias=neg_maxes[(qi, h)][:],
+                scale=1.0,
+                accum_out=row_sums[(qi, h)][:],
+            )
+
+        def gain_of(qi, h):
+            inv_sum = stats.tile([P, 1], F32, tag="inv_sum")
+            nc.vector.reciprocal(out=inv_sum[:], in_=row_sums[(qi, h)][:])
+            gains[(qi, h)] = stats.tile([P, 1], F32, tag="gain", name="gain")
+            nc.vector.tensor_scalar(
+                out=gains[(qi, h)][:], in0=inv_sum[:], scalar1=beta_f[:, 0:1], scalar2=None, op0=ALU.mult
+            )
+
+        def scale_low(qi, h):
+            if h == 0:
+                a_tiles[qi] = a_pool.tile([P, 2 * HEADS, HALF], BF16, tag="a", name="a", align_bytes=64)
+            below = qi * TILE_COLS
+            split = (qi // VECTOR_SHARE) * TILE_COLS
+            if below > split:
                 nc.scalar.activation(
-                    out=e[:, :, :seen],
-                    in_=e[:, :, :seen],
-                    func=ACT.Exp,
-                    bias=neg_max[:, h : h + 1],
-                    scale=1.0,
-                    accum_out=row_sum[:, h : h + 1],
+                    out=a_tiles[qi][:, 2 * h : 2 * h + 2, split:below],
+                    in_=exps[(qi, h)][:, :, split:below],
+                    func=ACT.Identity,
+                    bias=mc_below[:, qi : qi + 1],
+                    scale=gains[(qi, h)][:],
                 )
 
-        def weights(qi):
-            below = qi * TILE_COLS
-            seen = below + TILE_COLS
-            end = (qi // TILES_PER_PASS + 1) * PASS_COLS
-            inv_sum = stats.tile([P, HEADS], F32, tag="inv_sum")
-            nc.vector.reciprocal(out=inv_sum[:], in_=sums[qi][:])
-            gain = stats.tile([P, HEADS], F32, tag="gain")
-            nc.vector.tensor_scalar(
-                out=gain[:], in0=inv_sum[:], scalar1=beta_f[:, 0:1], scalar2=None, op0=ALU.mult
-            )
-            a = a_pool.tile([P, 2 * HEADS, HALF], BF16, tag="a", align_bytes=64)
-            a_tiles[qi] = a
-            for h in range(HEADS):
-                e = exps[(qi, h)]
-                if below > 0:
-                    nc.scalar.activation(
-                        out=a[:, 2 * h : 2 * h + 2, :below],
-                        in_=e[:, :, :below],
-                        func=ACT.Identity,
-                        bias=mc_below[:, qi : qi + 1],
-                        scale=gain[:, h : h + 1],
-                    )
-                nc.vector.scalar_tensor_tensor(
-                    out=a[:, 2 * h : 2 * h + 2, below:seen],
-                    in0=e[:, :, below:seen],
-                    scalar=gain[:, h : h + 1],
-                    in1=diag_add[:, qi, :].rearrange("p (u x) -> p u x", u=2),
+        def scale_low_on_vector(qi, h):
+            split = (qi // VECTOR_SHARE) * TILE_COLS
+            if split > 0:
+                nc.vector.tensor_scalar(
+                    out=a_tiles[qi][:, 2 * h : 2 * h + 2, :split],
+                    in0=exps[(qi, h)][:, :, :split],
+                    scalar1=gains[(qi, h)][:],
+                    scalar2=mc_below[:, qi : qi + 1],
                     op0=ALU.mult,
                     op1=ALU.add,
                 )
+
+        def scale_diag(qi, h):
+            block = slice(qi * TILE_COLS, (qi + 1) * TILE_COLS)
+            nc.vector.scalar_tensor_tensor(
+                out=a_tiles[qi][:, 2 * h : 2 * h + 2, block],
+                in0=exps[(qi, h)][:, :, block],
+                scalar=gains[(qi, h)][:],
+                in1=diag_add[:, qi, :].rearrange("p (u x) -> p u x", u=2),
+                op0=ALU.mult,
+                op1=ALU.add,
+            )
+
+        def fill_above(qi):
+            seen = (qi + 1) * TILE_COLS
+            end = (qi // TILES_PER_PASS + 1) * PASS_COLS
             if end > seen:
-                nc.gpsimd.tensor_scalar(
-                    out=a[:, :, seen:end],
+                nc.vector.tensor_scalar(
+                    out=a_tiles[qi][:, :, seen:end],
                     in0=ones_bf[:, :, : end - seen],
                     scalar1=mc_above[:, qi : qi + 1],
                     scalar2=0.0,
@@ -353,39 +360,63 @@ def tile_causalshapedattention_pa_kernel(tc, q, k, v, alpha, beta, gamma, out):
                     op1=ALU.add,
                 )
 
-        def turn_and_quantise(qi):
+        def turn(qi, g):
             a_words = a_tiles[qi][:].bitcast(F32)
-            a_codes[qi] = []
-            for g in range(qi // TILES_PER_PASS + 1):
-                turned = psum_turn.tile([P, HEADS, 2, P], F32, tag="turn")
-                for h in range(HEADS):
-                    for u in range(2):
-                        nc.tensor.transpose(
-                            turned[:, h, u, :], a_words[:, 2 * h + u, g * P : (g + 1) * P], ident_f[:]
-                        )
-                grouped = grouped_pool.tile([P, HEADS * P * PACK], BF16, tag="grouped", align_bytes=64)
-                nc.vector.tensor_copy(
-                    out=grouped[:].bitcast(F32).rearrange("p (h x u) -> p h x u", h=HEADS, u=2),
-                    in_=turned[:].rearrange("p h u x -> p h x u"),
-                )
-                codes = code_pool.tile([P, HEADS * P], U32, tag="codes", align_bytes=64)
-                scales = code_pool.tile([P, HEADS * P], U8, tag="scales", align_bytes=64)
-                nc.vector.quantize_mx(out=codes[:].bitcast(FP8X4), scales=scales[:], in_=grouped[:])
-                a_codes[qi].append((codes, scales))
+            turned_a[(qi, g)] = psum_turn.tile([P, HEADS, 2, P], F32, tag="turn", name="turned_a")
+            for h in range(HEADS):
+                for u in range(2):
+                    nc.tensor.transpose(
+                        turned_a[(qi, g)][:, h, u, :], a_words[:, 2 * h + u, g * P : (g + 1) * P], ident_f[:]
+                    )
+
+        def regroup(qi, g):
+            grouped_a[(qi, g)] = grouped_pool.tile(
+                [P, HEADS * P * PACK], BF16, tag="grouped", name="grouped", align_bytes=64
+            )
+            nc.vector.tensor_copy(
+                out=grouped_a[(qi, g)][:].bitcast(F32).rearrange("p (h x u) -> p h x u", h=HEADS, u=2),
+                in_=turned_a[(qi, g)][:].rearrange("p h u x -> p h x u"),
+            )
+
+        def quantise(qi, g):
+            codes = code_pool.tile([P, HEADS * P], U32, tag="codes", align_bytes=64)
+            scales = code_pool.tile([P, HEADS * P], U8, tag="scales", align_bytes=64)
+            nc.vector.quantize_mx(out=codes[:].bitcast(FP8X4), scales=scales[:], in_=grouped_a[(qi, g)][:])
+            a_codes[(qi, g)] = (codes, scales)
+
+        def spread_above(qi):
+            spread = psum_turn.tile([P, P, PACK], BF16, tag="turn")
+            nc.tensor.matmul(
+                out=spread[:],
+                lhsT=mc_above_bf[:, qi : qi + 1].to_broadcast([P, P]),
+                rhs=ident_bf[:].unsqueeze(2).to_broadcast([P, P, PACK]),
+                start=True,
+                stop=True,
+            )
+            above_grouped[qi] = grouped_pool.tile(
+                [P, P * PACK], BF16, tag="above_grouped", name="above_grouped", align_bytes=64
+            )
+            nc.scalar.copy(out=above_grouped[qi][:], in_=spread[:].rearrange("p x t -> p (x t)"))
+
+        def quantise_above(qi):
+            cols = slice(qi * P, (qi + 1) * P)
+            nc.vector.quantize_mx(
+                out=above_codes[:, cols].bitcast(FP8X4), scales=above_scales[:, cols], in_=above_grouped[qi][:]
+            )
 
         def attend(qi):
-            o_ps = psum_out.tile([P, HEADS, D], F32, tag="o")
+            o_tiles[qi] = psum_out.tile([P, HEADS, D], F32, tag="o", name="o_ps")
             for h in range(HEADS):
                 for g in range(PASSES):
-                    if g < len(a_codes[qi]):
-                        codes, scales = a_codes[qi][g]
+                    if g in own_passes(qi):
+                        codes, scales = a_codes[(qi, g)]
                         lhs_codes = codes[:, h * P : (h + 1) * P]
                         lhs_scales = scales[:, h * P : (h + 1) * P]
                     else:
-                        lhs_codes = u_codes[:, qi * P : (qi + 1) * P]
-                        lhs_scales = u_scales[:, qi * P : (qi + 1) * P]
+                        lhs_codes = above_codes[:, qi * P : (qi + 1) * P]
+                        lhs_scales = above_scales[:, qi * P : (qi + 1) * P]
                     nc.tensor.matmul_mx(
-                        out=o_ps[:, h, :],
+                        out=o_tiles[qi][:, h, :],
                         lhsT=lhs_codes.bitcast(FP8X4),
                         lhsT_scale=lhs_scales,
                         rhs=v_codes[:, g, h * D : (h + 1) * D].bitcast(FP8X4),
@@ -393,19 +424,79 @@ def tile_causalshapedattention_pa_kernel(tc, q, k, v, alpha, beta, gamma, out):
                         start=(g == 0),
                         stop=(g == PASSES - 1),
                     )
+
+        def store(qi):
             o_sb = out_pool.tile([P, C], F32, tag="o_sb")
-            nc.scalar.copy(out=o_sb[:], in_=o_ps[:].rearrange("p h d -> p (h d)"))
+            nc.scalar.copy(out=o_sb[:], in_=o_tiles[qi][:].rearrange("p h d -> p (h d)"))
             nc.sync.dma_start(out=out_rows[qi * P : (qi + 1) * P, :], in_=o_sb[:])
 
         order = list(range(TILES - 1, -1, -1))
+
+        def in_work(step, lag):
+            return order[step - lag] if 0 <= step - lag < TILES else None
+
+        turn_q(order[0])
+        turn_q(order[1])
         for step in range(TILES + 3):
-            if step + 1 < TILES:
-                turn_q(order[step + 1])
-            if step < TILES:
-                scores(order[step])
-            if 0 <= step - 1 < TILES:
-                weights(order[step - 1])
-            if 0 <= step - 2 < TILES:
-                turn_and_quantise(order[step - 2])
-            if 0 <= step - 3 < TILES:
-                attend(order[step - 3])
+            new = in_work(step, 0)
+            mid = in_work(step, 1)
+            ripe = in_work(step, 2)
+            old = in_work(step, 3)
+
+            if new is not None:
+                if step == 0:
+                    for t in range(TILES_PER_PASS):
+                        turn_k(t)
+                score_pass(new, 0, 0)
+            if mid is not None:
+                gain_of(mid, 1)
+                scale_low(mid, 0)
+                scale_low(mid, 1)
+            if new is not None:
+                for g in own_passes(new)[1:]:
+                    if step == 0:
+                        for t in range(g * TILES_PER_PASS, (g + 1) * TILES_PER_PASS):
+                            turn_k(t)
+                    score_pass(new, 0, g)
+            if mid is not None:
+                scale_diag(mid, 0)
+            if new is not None:
+                row_max(new, 0)
+                exponent(new, 0)
+            if old is not None:
+                attend(old)
+                store(old)
+            if new is not None:
+                for g in own_passes(new):
+                    score_pass(new, 1, g)
+            if mid is not None:
+                scale_diag(mid, 1)
+                fill_above(mid)
+            if new is not None:
+                row_max(new, 1)
+                exponent(new, 1)
+            if mid is not None:
+                scale_low_on_vector(mid, 0)
+                scale_low_on_vector(mid, 1)
+            if ripe is not None:
+                turn(ripe, 0)
+                regroup(ripe, 0)
+                for g in own_passes(ripe)[1:]:
+                    turn(ripe, g)
+                    regroup(ripe, g)
+                    quantise(ripe, g - 1)
+            if new is not None:
+                gain_of(new, 0)
+            if ripe is not None:
+                quantise(ripe, own_passes(ripe)[-1])
+                if ripe < U_TILES:
+                    spread_above(ripe)
+            if step + 2 < TILES:
+                turn_q(order[step + 2])
+            if step < PASSES // 2:
+                regroup_v(2 * step)
+                regroup_v(2 * step + 1)
+                quantise_v(2 * step)
+                quantise_v(2 * step + 1)
+            if ripe is not None and ripe < U_TILES:
+                quantise_above(ripe)

@@ -29,7 +29,6 @@ PASS_COLS = K_PASS // 2
 D_BLOCKS = C // P
 MASKED = -1.0e30
 U_TILES = TILES - TILES_PER_PASS
-VECTOR_SHARE = 4
 
 FLOPS = 2 * 2 * T * T * D * HEADS
 
@@ -47,12 +46,13 @@ def tile_causalshapedattention_pa_kernel(tc, q, k, v, alpha, beta, gamma, out):
         stats = ctx.enter_context(tc.tile_pool(name="stats", bufs=6))
         score_pool = ctx.enter_context(tc.tile_pool(name="scores", bufs=5))
         a_pool = ctx.enter_context(tc.tile_pool(name="a", bufs=3))
-        grouped_pool = ctx.enter_context(tc.tile_pool(name="grouped", bufs=3))
+        grouped_pool = ctx.enter_context(tc.tile_pool(name="grouped", bufs=5))
         code_pool = ctx.enter_context(tc.tile_pool(name="codes", bufs=10))
         out_pool = ctx.enter_context(tc.tile_pool(name="out", bufs=3))
         psum_scores = ctx.enter_context(tc.psum_pool(name="psum_scores", bufs=3))
         psum_turn = ctx.enter_context(tc.psum_pool(name="psum_turn", bufs=4))
         psum_out = ctx.enter_context(tc.psum_pool(name="psum_out", bufs=1))
+        ctx.enter_context(tc.manual_schedule())
 
         q_sb = keep.tile([P, TILES, C], BF16)
         k_sb = keep.tile([P, TILES, C], BF16)
@@ -71,9 +71,10 @@ def tile_causalshapedattention_pa_kernel(tc, q, k, v, alpha, beta, gamma, out):
             tiles = slice(first, first + TILES_PER_PASS)
             nc.sync.dma_start(out=dst[:, tiles, :], in_=src[:, tiles, :])
 
-        load_tiles(q_sb, q_view, TILES - TILES_PER_PASS)
+        nc.sync.dma_start(out=q_sb[:, TILES - 2 :, :], in_=q_view[:, TILES - 2 :, :])
         for g in range(PASSES):
             load_tiles(k_sb, k_view, g * TILES_PER_PASS)
+        nc.sync.dma_start(out=q_sb[:, TILES - 4 : TILES - 2, :], in_=q_view[:, TILES - 4 : TILES - 2, :])
         nc.sync.dma_start(
             out=v_raw[:].rearrange("p g t c -> p g (t c)"),
             in_=v_rows.rearrange("(g p t) c -> p g (t c)", p=P, t=PACK),
@@ -201,6 +202,10 @@ def tile_causalshapedattention_pa_kernel(tc, q, k, v, alpha, beta, gamma, out):
                 in_=turned[:].rearrange("p b (u x) -> p b u x", u=2),
             )
 
+        def turn_keys(g):
+            for t in range(g * TILES_PER_PASS, (g + 1) * TILES_PER_PASS):
+                turn_k(t)
+
         v_codes = keep.tile([P, PASSES, C], U32, align_bytes=64)
         v_scales = keep.tile([P, PASSES, C], U8, align_bytes=64)
         v_grouped = {}
@@ -221,11 +226,12 @@ def tile_causalshapedattention_pa_kernel(tc, q, k, v, alpha, beta, gamma, out):
         neg_maxes = {}
         row_sums = {}
         gains = {}
+        inv_sums = {}
+        above_grouped = {}
         a_tiles = {}
         turned_a = {}
         grouped_a = {}
         a_codes = {}
-        above_grouped = {}
         o_tiles = {}
         above_codes = keep.tile([P, U_TILES * P], U32, align_bytes=64)
         above_scales = keep.tile([P, U_TILES * P], U8, align_bytes=64)
@@ -291,7 +297,8 @@ def tile_causalshapedattention_pa_kernel(tc, q, k, v, alpha, beta, gamma, out):
             )
 
         def exponent(qi, h):
-            row_sums[(qi, h)] = stats.tile([P, 1], F32, tag="row_sum", name="row_sum")
+            if h == 0:
+                row_sums[qi] = stats.tile([P, HEADS], F32, tag="row_sum", name="row_sum")
             seen = (qi + 1) * TILE_COLS
             nc.scalar.activation(
                 out=exps[(qi, h)][:, :, :seen],
@@ -299,38 +306,28 @@ def tile_causalshapedattention_pa_kernel(tc, q, k, v, alpha, beta, gamma, out):
                 func=ACT.Exp,
                 bias=neg_maxes[(qi, h)][:],
                 scale=1.0,
-                accum_out=row_sums[(qi, h)][:],
+                accum_out=row_sums[qi][:, h : h + 1],
             )
 
-        def gain_of(qi, h):
-            inv_sum = stats.tile([P, 1], F32, tag="inv_sum")
-            nc.vector.reciprocal(out=inv_sum[:], in_=row_sums[(qi, h)][:])
-            gains[(qi, h)] = stats.tile([P, 1], F32, tag="gain", name="gain")
+        def invert_sum(qi):
+            inv_sums[qi] = stats.tile([P, HEADS], F32, tag="inv_sum", name="inv_sum")
+            nc.vector.reciprocal(out=inv_sums[qi][:], in_=row_sums[qi][:])
+
+        def gain_of(qi):
+            gains[qi] = stats.tile([P, HEADS], F32, tag="gain", name="gain")
             nc.vector.tensor_scalar(
-                out=gains[(qi, h)][:], in0=inv_sum[:], scalar1=beta_f[:, 0:1], scalar2=None, op0=ALU.mult
+                out=gains[qi][:], in0=inv_sums[qi][:], scalar1=beta_f[:, 0:1], scalar2=None, op0=ALU.mult
             )
 
         def scale_low(qi, h):
             if h == 0:
                 a_tiles[qi] = a_pool.tile([P, 2 * HEADS, HALF], BF16, tag="a", name="a", align_bytes=64)
             below = qi * TILE_COLS
-            split = (qi // VECTOR_SHARE) * TILE_COLS
-            if below > split:
-                nc.scalar.activation(
-                    out=a_tiles[qi][:, 2 * h : 2 * h + 2, split:below],
-                    in_=exps[(qi, h)][:, :, split:below],
-                    func=ACT.Identity,
-                    bias=mc_below[:, qi : qi + 1],
-                    scale=gains[(qi, h)][:],
-                )
-
-        def scale_low_on_vector(qi, h):
-            split = (qi // VECTOR_SHARE) * TILE_COLS
-            if split > 0:
+            if below > 0:
                 nc.vector.tensor_scalar(
-                    out=a_tiles[qi][:, 2 * h : 2 * h + 2, :split],
-                    in0=exps[(qi, h)][:, :, :split],
-                    scalar1=gains[(qi, h)][:],
+                    out=a_tiles[qi][:, 2 * h : 2 * h + 2, :below],
+                    in0=exps[(qi, h)][:, :, :below],
+                    scalar1=gains[qi][:, h : h + 1],
                     scalar2=mc_below[:, qi : qi + 1],
                     op0=ALU.mult,
                     op1=ALU.add,
@@ -341,7 +338,7 @@ def tile_causalshapedattention_pa_kernel(tc, q, k, v, alpha, beta, gamma, out):
             nc.vector.scalar_tensor_tensor(
                 out=a_tiles[qi][:, 2 * h : 2 * h + 2, block],
                 in0=exps[(qi, h)][:, :, block],
-                scalar=gains[(qi, h)][:],
+                scalar=gains[qi][:, h : h + 1],
                 in1=diag_add[:, qi, :].rearrange("p (u x) -> p u x", u=2),
                 op0=ALU.mult,
                 op1=ALU.add,
@@ -373,7 +370,7 @@ def tile_causalshapedattention_pa_kernel(tc, q, k, v, alpha, beta, gamma, out):
             grouped_a[(qi, g)] = grouped_pool.tile(
                 [P, HEADS * P * PACK], BF16, tag="grouped", name="grouped", align_bytes=64
             )
-            nc.vector.tensor_copy(
+            nc.scalar.copy(
                 out=grouped_a[(qi, g)][:].bitcast(F32).rearrange("p (h x u) -> p h x u", h=HEADS, u=2),
                 in_=turned_a[(qi, g)][:].rearrange("p h u x -> p h x u"),
             )
@@ -384,24 +381,27 @@ def tile_causalshapedattention_pa_kernel(tc, q, k, v, alpha, beta, gamma, out):
             nc.vector.quantize_mx(out=codes[:].bitcast(FP8X4), scales=scales[:], in_=grouped_a[(qi, g)][:])
             a_codes[(qi, g)] = (codes, scales)
 
-        def spread_above(qi):
-            spread = psum_turn.tile([P, P, PACK], BF16, tag="turn")
-            nc.tensor.matmul(
-                out=spread[:],
-                lhsT=mc_above_bf[:, qi : qi + 1].to_broadcast([P, P]),
-                rhs=ident_bf[:].unsqueeze(2).to_broadcast([P, P, PACK]),
-                start=True,
-                stop=True,
+        def make_above(first):
+            spread = psum_turn.tile([P, K_PASS], F32, tag="turn")
+            for j in range(TILES_PER_PASS):
+                nc.tensor.matmul(
+                    out=spread[:, j * P : (j + 1) * P],
+                    lhsT=mc_above_bf[:, first + j : first + j + 1].to_broadcast([P, P]),
+                    rhs=ident_bf[:],
+                    start=True,
+                    stop=True,
+                )
+            above_grouped[first] = wide.tile([P, K_PASS, PACK], BF16, tag="above", name="above_grouped", align_bytes=64)
+            nc.scalar.copy(
+                out=above_grouped[first][:], in_=spread[:].unsqueeze(2).to_broadcast([P, K_PASS, PACK])
             )
-            above_grouped[qi] = grouped_pool.tile(
-                [P, P * PACK], BF16, tag="above_grouped", name="above_grouped", align_bytes=64
-            )
-            nc.scalar.copy(out=above_grouped[qi][:], in_=spread[:].rearrange("p x t -> p (x t)"))
 
-        def quantise_above(qi):
-            cols = slice(qi * P, (qi + 1) * P)
+        def quantise_above(first):
+            cols = slice(first * P, first * P + K_PASS)
             nc.vector.quantize_mx(
-                out=above_codes[:, cols].bitcast(FP8X4), scales=above_scales[:, cols], in_=above_grouped[qi][:]
+                out=above_codes[:, cols].bitcast(FP8X4),
+                scales=above_scales[:, cols],
+                in_=above_grouped[first][:].rearrange("p x t -> p (x t)"),
             )
 
         def attend(qi):
@@ -436,6 +436,7 @@ def tile_causalshapedattention_pa_kernel(tc, q, k, v, alpha, beta, gamma, out):
             return order[step - lag] if 0 <= step - lag < TILES else None
 
         turn_q(order[0])
+        turn_keys(0)
         turn_q(order[1])
         for step in range(TILES + 3):
             new = in_work(step, 0)
@@ -444,59 +445,48 @@ def tile_causalshapedattention_pa_kernel(tc, q, k, v, alpha, beta, gamma, out):
             old = in_work(step, 3)
 
             if new is not None:
-                if step == 0:
-                    for t in range(TILES_PER_PASS):
-                        turn_k(t)
-                score_pass(new, 0, 0)
-            if mid is not None:
-                gain_of(mid, 1)
-                scale_low(mid, 0)
-                scale_low(mid, 1)
-            if new is not None:
-                for g in own_passes(new)[1:]:
-                    if step == 0:
-                        for t in range(g * TILES_PER_PASS, (g + 1) * TILES_PER_PASS):
-                            turn_k(t)
+                for g in own_passes(new):
+                    if step == 0 and g + 1 < PASSES:
+                        turn_keys(g + 1)
                     score_pass(new, 0, g)
             if mid is not None:
-                scale_diag(mid, 0)
+                invert_sum(mid)
             if new is not None:
                 row_max(new, 0)
                 exponent(new, 0)
+            if mid is not None:
+                gain_of(mid)
+            if step + 2 < TILES:
+                turn_q(order[step + 2])
             if old is not None:
-                attend(old)
-                store(old)
+                for g in own_passes(old):
+                    quantise(old, g)
+            if 1 <= step <= U_TILES // TILES_PER_PASS:
+                quantise_above(U_TILES - step * TILES_PER_PASS)
             if new is not None:
                 for g in own_passes(new):
                     score_pass(new, 1, g)
             if mid is not None:
-                scale_diag(mid, 1)
-                fill_above(mid)
+                scale_low(mid, 0)
             if new is not None:
                 row_max(new, 1)
                 exponent(new, 1)
             if mid is not None:
-                scale_low_on_vector(mid, 0)
-                scale_low_on_vector(mid, 1)
+                scale_diag(mid, 0)
+                scale_low(mid, 1)
+                scale_diag(mid, 1)
+                fill_above(mid)
             if ripe is not None:
-                turn(ripe, 0)
-                regroup(ripe, 0)
-                for g in own_passes(ripe)[1:]:
+                for g in own_passes(ripe):
                     turn(ripe, g)
                     regroup(ripe, g)
-                    quantise(ripe, g - 1)
-            if new is not None:
-                gain_of(new, 0)
-            if ripe is not None:
-                quantise(ripe, own_passes(ripe)[-1])
-                if ripe < U_TILES:
-                    spread_above(ripe)
-            if step + 2 < TILES:
-                turn_q(order[step + 2])
+            if old is not None:
+                attend(old)
+                store(old)
             if step < PASSES // 2:
                 regroup_v(2 * step)
                 regroup_v(2 * step + 1)
                 quantise_v(2 * step)
                 quantise_v(2 * step + 1)
-            if ripe is not None and ripe < U_TILES:
-                quantise_above(ripe)
+            if step < U_TILES // TILES_PER_PASS:
+                make_above(U_TILES - (step + 1) * TILES_PER_PASS)

@@ -52,7 +52,6 @@ def tile_causalshapedattention_pa_kernel(tc, q, k, v, alpha, beta, gamma, out):
         psum_scores = ctx.enter_context(tc.psum_pool(name="psum_scores", bufs=3))
         psum_turn = ctx.enter_context(tc.psum_pool(name="psum_turn", bufs=4))
         psum_out = ctx.enter_context(tc.psum_pool(name="psum_out", bufs=1))
-        ctx.enter_context(tc.manual_schedule())
 
         q_sb = keep.tile([P, TILES, C], BF16)
         k_sb = keep.tile([P, TILES, C], BF16)

@@ -42,9 +42,9 @@ def tile_causalshapedattention_pa_kernel(tc, q, k, v, alpha, beta, gamma, out):
 
     with ExitStack() as ctx:
         keep = ctx.enter_context(tc.tile_pool(name="keep", bufs=1))
-        wide = ctx.enter_context(tc.tile_pool(name="wide", bufs=2))
+        wide = ctx.enter_context(tc.tile_pool(name="wide", bufs=4))
         stats = ctx.enter_context(tc.tile_pool(name="stats", bufs=6))
-        score_pool = ctx.enter_context(tc.tile_pool(name="scores", bufs=5))
+        score_pool = ctx.enter_context(tc.tile_pool(name="scores", bufs=6))
         a_pool = ctx.enter_context(tc.tile_pool(name="a", bufs=3))
         grouped_pool = ctx.enter_context(tc.tile_pool(name="grouped", bufs=5))
         code_pool = ctx.enter_context(tc.tile_pool(name="codes", bufs=10))
@@ -71,13 +71,20 @@ def tile_causalshapedattention_pa_kernel(tc, q, k, v, alpha, beta, gamma, out):
             nc.sync.dma_start(out=dst[:, tiles, :], in_=src[:, tiles, :])
 
         nc.sync.dma_start(out=q_sb[:, TILES - 2 :, :], in_=q_view[:, TILES - 2 :, :])
-        for g in range(PASSES):
-            load_tiles(k_sb, k_view, g * TILES_PER_PASS)
+        v_view = v_rows.rearrange("(g p t) c -> p g (t c)", p=P, t=PACK)
+
+        def load_v(g):
+            nc.sync.dma_start(out=v_raw[:, g].rearrange("p t c -> p (t c)"), in_=v_view[:, g, :])
+
+        load_tiles(k_sb, k_view, 0)
+        load_tiles(k_sb, k_view, TILES_PER_PASS)
+        load_v(0)
+        load_tiles(k_sb, k_view, 2 * TILES_PER_PASS)
+        load_v(1)
+        load_tiles(k_sb, k_view, 3 * TILES_PER_PASS)
+        load_v(2)
+        load_v(3)
         nc.sync.dma_start(out=q_sb[:, TILES - 4 : TILES - 2, :], in_=q_view[:, TILES - 4 : TILES - 2, :])
-        nc.sync.dma_start(
-            out=v_raw[:].rearrange("p g t c -> p g (t c)"),
-            in_=v_rows.rearrange("(g p t) c -> p g (t c)", p=P, t=PACK),
-        )
         for g in range(PASSES - 2, -1, -1):
             load_tiles(q_sb, q_view, g * TILES_PER_PASS)
 
@@ -159,19 +166,19 @@ def tile_causalshapedattention_pa_kernel(tc, q, k, v, alpha, beta, gamma, out):
         nc.vector.tensor_copy(out=beta_f[:], in_=beta_bf[:])
 
         diag_add = keep.tile([P, TILES, P], F32)
-        nc.gpsimd.tensor_tensor(
+        nc.vector.tensor_tensor(
             out=diag_add[:],
             in0=above_halves[:].unsqueeze(1).to_broadcast([P, TILES, P]),
             in1=mc_above[:].unsqueeze(2).to_broadcast([P, TILES, P]),
             op=ALU.mult,
         )
-        nc.gpsimd.tensor_tensor(
+        nc.vector.tensor_tensor(
             out=diag_add[:],
             in0=diag_add[:],
             in1=alpha_eye[:].unsqueeze(1).to_broadcast([P, TILES, P]),
             op=ALU.add,
         )
-        nc.gpsimd.tensor_scalar(
+        nc.vector.tensor_scalar(
             out=diag_add[:, TILES - 1, :],
             in0=diag_add[:, TILES - 1, :],
             scalar1=1.0,
@@ -195,7 +202,7 @@ def tile_causalshapedattention_pa_kernel(tc, q, k, v, alpha, beta, gamma, out):
                 nc.tensor.transpose(
                     turned[:, b, :], k_sb[:, t, b * P : (b + 1) * P], ident_halves_bf[:]
                 )
-            copy_out = nc.scalar.copy if t % 2 == 0 else nc.vector.tensor_copy
+            copy_out = nc.scalar.copy
             copy_out(
                 out=k_t[:, :, :, t * TILE_COLS : (t + 1) * TILE_COLS],
                 in_=turned[:].rearrange("p b (u x) -> p b u x", u=2),
@@ -211,7 +218,14 @@ def tile_causalshapedattention_pa_kernel(tc, q, k, v, alpha, beta, gamma, out):
 
         def regroup_v(g):
             v_grouped[g] = wide.tile([P, C, PACK], BF16, tag="wide", name="v_grouped", align_bytes=64)
-            nc.vector.tensor_copy(out=v_grouped[g][:], in_=v_raw[:, g].rearrange("p t c -> p c t"))
+            nc.gpsimd.tensor_scalar(
+                out=v_grouped[g][:],
+                in0=v_raw[:, g].rearrange("p t c -> p c t"),
+                scalar1=1.0,
+                scalar2=0.0,
+                op0=ALU.mult,
+                op1=ALU.add,
+            )
 
         def quantise_v(g):
             nc.vector.quantize_mx(
@@ -390,7 +404,7 @@ def tile_causalshapedattention_pa_kernel(tc, q, k, v, alpha, beta, gamma, out):
                     start=True,
                     stop=True,
                 )
-            above_grouped[first] = wide.tile([P, K_PASS, PACK], BF16, tag="above", name="above_grouped", align_bytes=64)
+            above_grouped[first] = wide.tile([P, K_PASS, PACK], BF16, tag="wide", name="above_grouped", align_bytes=64)
             nc.scalar.copy(
                 out=above_grouped[first][:], in_=spread[:].unsqueeze(2).to_broadcast([P, K_PASS, PACK])
             )
@@ -437,6 +451,8 @@ def tile_causalshapedattention_pa_kernel(tc, q, k, v, alpha, beta, gamma, out):
         turn_q(order[0])
         turn_keys(0)
         turn_q(order[1])
+        for g in range(PASSES):
+            regroup_v(g)
         for step in range(TILES + 3):
             new = in_work(step, 0)
             mid = in_work(step, 1)
@@ -482,10 +498,8 @@ def tile_causalshapedattention_pa_kernel(tc, q, k, v, alpha, beta, gamma, out):
             if old is not None:
                 attend(old)
                 store(old)
-            if step < PASSES // 2:
-                regroup_v(2 * step)
-                regroup_v(2 * step + 1)
-                quantise_v(2 * step)
-                quantise_v(2 * step + 1)
+            if step == 1:
+                for g in range(PASSES):
+                    quantise_v(g)
             if step < U_TILES // TILES_PER_PASS:
                 make_above(U_TILES - (step + 1) * TILES_PER_PASS)

@@ -28,6 +28,8 @@ TILE_COLS = P // 2
 PASS_COLS = K_PASS // 2
 D_BLOCKS = C // P
 MASKED = -1.0e30
+SCORE_BANKS = 4
+ORDER = [3, 7, 11, 15, 14, 13, 12, 10, 9, 8, 6, 5, 4, 2, 1, 0]
 U_TILES = TILES - TILES_PER_PASS
 
 FLOPS = 2 * 2 * T * T * D * HEADS
@@ -41,6 +43,7 @@ def tile_causalshapedattention_pa_kernel(tc, q, k, v, alpha, beta, gamma, out):
     out_rows = out.flatten_outer_dims()
 
     with ExitStack() as ctx:
+        ctx.enter_context(tc.manual_schedule())
         keep = ctx.enter_context(tc.tile_pool(name="keep", bufs=1))
         wide = ctx.enter_context(tc.tile_pool(name="wide", bufs=4))
         stats = ctx.enter_context(tc.tile_pool(name="stats", bufs=6))
@@ -49,8 +52,8 @@ def tile_causalshapedattention_pa_kernel(tc, q, k, v, alpha, beta, gamma, out):
         grouped_pool = ctx.enter_context(tc.tile_pool(name="grouped", bufs=5))
         code_pool = ctx.enter_context(tc.tile_pool(name="codes", bufs=10))
         out_pool = ctx.enter_context(tc.tile_pool(name="out", bufs=3))
-        psum_scores = ctx.enter_context(tc.psum_pool(name="psum_scores", bufs=3))
-        psum_turn = ctx.enter_context(tc.psum_pool(name="psum_turn", bufs=4))
+        psum_scores = ctx.enter_context(tc.psum_pool(name="psum_scores", bufs=SCORE_BANKS))
+        psum_turn = ctx.enter_context(tc.psum_pool(name="psum_turn", bufs=3))
         psum_out = ctx.enter_context(tc.psum_pool(name="psum_out", bufs=1))
 
         q_sb = keep.tile([P, TILES, C], BF16)
@@ -58,35 +61,36 @@ def tile_causalshapedattention_pa_kernel(tc, q, k, v, alpha, beta, gamma, out):
         q_view = q_rows.rearrange("(t p) c -> p t c", p=P)
         k_view = k_rows.rearrange("(t p) c -> p t c", p=P)
         v_raw = keep.tile([P, PASSES, PACK, C], BF16)
-
+        v_view = v_rows.rearrange("(g p t) c -> p g (t c)", p=P, t=PACK)
         alpha_bf = keep.tile([P, 1], BF16)
         beta_bf = keep.tile([P, 1], BF16)
         gamma_bf = keep.tile([P, 1], BF16)
-        nc.scalar.dma_start(out=gamma_bf[:], in_=gamma.partition_broadcast(P))
-        nc.scalar.dma_start(out=alpha_bf[:], in_=alpha.partition_broadcast(P))
-        nc.scalar.dma_start(out=beta_bf[:], in_=beta.partition_broadcast(P))
 
-        def load_tiles(dst, src, first):
-            tiles = slice(first, first + TILES_PER_PASS)
-            nc.sync.dma_start(out=dst[:, tiles, :], in_=src[:, tiles, :])
+        def load_q(tiles):
+            nc.sync.dma_start(out=q_sb[:, tiles, :], in_=q_view[:, tiles, :])
 
-        nc.sync.dma_start(out=q_sb[:, TILES - 2 :, :], in_=q_view[:, TILES - 2 :, :])
-        v_view = v_rows.rearrange("(g p t) c -> p g (t c)", p=P, t=PACK)
+        def load_k(g):
+            tiles = slice(g * TILES_PER_PASS, (g + 1) * TILES_PER_PASS)
+            nc.sync.dma_start(out=k_sb[:, tiles, :], in_=k_view[:, tiles, :])
 
         def load_v(g):
             nc.sync.dma_start(out=v_raw[:, g].rearrange("p t c -> p (t c)"), in_=v_view[:, g, :])
 
-        load_tiles(k_sb, k_view, 0)
-        load_tiles(k_sb, k_view, TILES_PER_PASS)
+        load_q(slice(3, 4))
+        load_k(0)
+        load_k(1)
+        load_q(slice(7, TILES, 4))
         load_v(0)
-        load_tiles(k_sb, k_view, 2 * TILES_PER_PASS)
+        nc.sync.dma_start(out=gamma_bf[:], in_=gamma.partition_broadcast(P))
+        nc.sync.dma_start(out=alpha_bf[:], in_=alpha.partition_broadcast(P))
+        nc.sync.dma_start(out=beta_bf[:], in_=beta.partition_broadcast(P))
         load_v(1)
-        load_tiles(k_sb, k_view, 3 * TILES_PER_PASS)
+        load_k(2)
         load_v(2)
+        load_k(3)
         load_v(3)
-        nc.sync.dma_start(out=q_sb[:, TILES - 4 : TILES - 2, :], in_=q_view[:, TILES - 4 : TILES - 2, :])
-        for g in range(PASSES - 2, -1, -1):
-            load_tiles(q_sb, q_view, g * TILES_PER_PASS)
+        for g in range(PASSES - 1, -1, -1):
+            load_q(slice(g * TILES_PER_PASS, (g + 1) * TILES_PER_PASS - 1))
 
         warm = keep.tile([P, 1], F32)
         nc.vector.memset(warm[:], 0.0)
@@ -94,8 +98,6 @@ def tile_causalshapedattention_pa_kernel(tc, q, k, v, alpha, beta, gamma, out):
 
         ident_bf = keep.tile([P, P], BF16)
         make_identity(nc, ident_bf[:])
-        ident_f = keep.tile([P, P], F32)
-        make_identity(nc, ident_f[:])
         above = keep.tile([P, P], F32)
         nc.gpsimd.memset(above[:], 0.0)
         nc.gpsimd.affine_select(
@@ -107,6 +109,8 @@ def tile_causalshapedattention_pa_kernel(tc, q, k, v, alpha, beta, gamma, out):
             pattern=[[-1, P]],
             channel_multiplier=1,
         )
+        ident_f = keep.tile([P, P], F32)
+        make_identity(nc, ident_f[:])
         left_i = keep.tile([P, TILES], I32)
         nc.gpsimd.iota(left_i[:], pattern=[[-P, TILES]], base=T - 1, channel_multiplier=-1)
         ones_bf = keep.tile([P, 2 * HEADS, PASS_COLS - TILE_COLS], BF16)
@@ -118,19 +122,16 @@ def tile_causalshapedattention_pa_kernel(tc, q, k, v, alpha, beta, gamma, out):
         def in_halves(square):
             return square.rearrange("p (u m e) -> p u m e", u=2, e=2)
 
-        ident_halves_f = keep.tile([P, P], F32)
-        nc.vector.tensor_copy(out=in_halves(ident_halves_f[:]), in_=natural(ident_f[:]))
         ident_halves_bf = keep.tile([P, P], BF16)
-        nc.vector.tensor_copy(out=ident_halves_bf[:], in_=ident_halves_f[:])
+        nc.vector.tensor_copy(out=in_halves(ident_halves_bf[:]), in_=natural(ident_bf[:]))
         above_halves = keep.tile([P, P], F32)
         nc.vector.tensor_copy(out=in_halves(above_halves[:]), in_=natural(above[:]))
+        left = keep.tile([P, TILES], F32)
+        nc.vector.tensor_copy(out=left[:], in_=left_i[:])
         masked_bf = keep.tile([P, P], BF16)
         nc.vector.tensor_scalar(
             out=masked_bf[:], in0=above_halves[:], scalar1=MASKED, scalar2=None, op0=ALU.mult
         )
-
-        left = keep.tile([P, TILES], F32)
-        nc.vector.tensor_copy(out=left[:], in_=left_i[:])
         is_last = keep.tile([P, TILES], F32)
         nc.vector.tensor_scalar(
             out=is_last[:], in0=left[:], scalar1=0.0, scalar2=None, op0=ALU.is_equal
@@ -141,51 +142,54 @@ def tile_causalshapedattention_pa_kernel(tc, q, k, v, alpha, beta, gamma, out):
         )
         share = keep.tile([P, TILES], F32)
         nc.vector.reciprocal(out=share[:], in_=count[:])
+
         alpha_f = keep.tile([P, 1], F32)
         beta_f = keep.tile([P, 1], F32)
         gamma_f = keep.tile([P, 1], F32)
-        nc.vector.tensor_copy(out=gamma_f[:], in_=gamma_bf[:])
         mc_above = keep.tile([P, TILES], F32)
-        nc.vector.tensor_scalar(
-            out=mc_above[:],
-            in0=share[:],
-            scalar1=gamma_f[:, 0:1],
-            scalar2=-1.0,
-            op0=ALU.mult,
-            op1=ALU.mult,
-        )
-        nc.vector.tensor_copy(out=alpha_f[:], in_=alpha_bf[:])
-        alpha_eye = keep.tile([P, P], F32)
-        nc.vector.tensor_scalar(
-            out=alpha_eye[:], in0=ident_halves_f[:], scalar1=alpha_f[:, 0:1], scalar2=None, op0=ALU.mult
-        )
-        mc_below = keep.tile([P, TILES], F32)
-        nc.vector.tensor_tensor(out=mc_below[:], in0=mc_above[:], in1=is_last[:], op=ALU.mult)
         mc_above_bf = keep.tile([P, TILES], BF16)
-        nc.vector.tensor_copy(out=mc_above_bf[:], in_=mc_above[:])
-        nc.vector.tensor_copy(out=beta_f[:], in_=beta_bf[:])
+        mc_below = keep.tile([P, TILES], F32)
+        alpha_eye = keep.tile([P, P], F32)
 
-        diag_add = keep.tile([P, TILES, P], F32)
-        nc.vector.tensor_tensor(
-            out=diag_add[:],
-            in0=above_halves[:].unsqueeze(1).to_broadcast([P, TILES, P]),
-            in1=mc_above[:].unsqueeze(2).to_broadcast([P, TILES, P]),
-            op=ALU.mult,
-        )
-        nc.vector.tensor_tensor(
-            out=diag_add[:],
-            in0=diag_add[:],
-            in1=alpha_eye[:].unsqueeze(1).to_broadcast([P, TILES, P]),
-            op=ALU.add,
-        )
-        nc.vector.tensor_scalar(
-            out=diag_add[:, TILES - 1, :],
-            in0=diag_add[:, TILES - 1, :],
-            scalar1=1.0,
-            scalar2=mc_below[:, TILES - 1 : TILES],
-            op0=ALU.mult,
-            op1=ALU.add,
-        )
+        def take_scalars():
+            nc.vector.tensor_copy(out=gamma_f[:], in_=gamma_bf[:])
+            nc.vector.tensor_copy(out=alpha_f[:], in_=alpha_bf[:])
+            nc.vector.tensor_copy(out=beta_f[:], in_=beta_bf[:])
+            nc.vector.tensor_scalar(
+                out=mc_above[:],
+                in0=share[:],
+                scalar1=gamma_f[:, 0:1],
+                scalar2=-1.0,
+                op0=ALU.mult,
+                op1=ALU.mult,
+            )
+            nc.vector.tensor_scalar(
+                out=alpha_eye[:], in0=ident_halves_bf[:], scalar1=alpha_f[:, 0:1], scalar2=None, op0=ALU.mult
+            )
+            nc.vector.tensor_copy(out=mc_above_bf[:], in_=mc_above[:])
+            nc.vector.tensor_tensor(out=mc_below[:], in0=mc_above[:], in1=is_last[:], op=ALU.mult)
+
+        diag_adds = {}
+
+        def diag_addend(qi):
+            diag_adds[qi] = stats.tile([P, P], F32, tag="diag_add", name="diag_add")
+            nc.vector.scalar_tensor_tensor(
+                out=diag_adds[qi][:],
+                in0=above_halves[:],
+                scalar=mc_above[:, qi : qi + 1],
+                in1=alpha_eye[:],
+                op0=ALU.mult,
+                op1=ALU.add,
+            )
+            if qi == TILES - 1:
+                nc.vector.tensor_scalar(
+                    out=diag_adds[qi][:],
+                    in0=diag_adds[qi][:],
+                    scalar1=1.0,
+                    scalar2=mc_below[:, qi : qi + 1],
+                    op0=ALU.mult,
+                    op1=ALU.add,
+                )
 
         q_t = keep.tile([P, D_BLOCKS, T], BF16)
         k_t = keep.tile([P, D_BLOCKS, 2, HALF], BF16)
@@ -196,21 +200,18 @@ def tile_causalshapedattention_pa_kernel(tc, q, k, v, alpha, beta, gamma, out):
                 nc.tensor.transpose(turned[:, b, :], q_sb[:, t, b * P : (b + 1) * P], ident_bf[:])
             nc.scalar.copy(out=q_t[:, :, t * P : (t + 1) * P], in_=turned[:])
 
-        def turn_k(t):
-            turned = psum_turn.tile([P, D_BLOCKS, P], BF16, tag="turn")
-            for b in range(D_BLOCKS):
-                nc.tensor.transpose(
-                    turned[:, b, :], k_sb[:, t, b * P : (b + 1) * P], ident_halves_bf[:]
-                )
-            copy_out = nc.scalar.copy
-            copy_out(
-                out=k_t[:, :, :, t * TILE_COLS : (t + 1) * TILE_COLS],
-                in_=turned[:].rearrange("p b (u x) -> p b u x", u=2),
-            )
-
         def turn_keys(g):
             for t in range(g * TILES_PER_PASS, (g + 1) * TILES_PER_PASS):
-                turn_k(t)
+                turned = psum_turn.tile([P, D_BLOCKS, P], BF16, tag="turn")
+                for b in range(D_BLOCKS):
+                    nc.tensor.transpose(
+                        turned[:, b, :], k_sb[:, t, b * P : (b + 1) * P], ident_halves_bf[:]
+                    )
+                copy_out = nc.scalar.copy if t % 2 == 0 else nc.vector.tensor_copy
+                copy_out(
+                    out=k_t[:, :, :, t * TILE_COLS : (t + 1) * TILE_COLS],
+                    in_=turned[:].rearrange("p b (u x) -> p b u x", u=2),
+                )
 
         v_codes = keep.tile([P, PASSES, C], U32, align_bytes=64)
         v_scales = keep.tile([P, PASSES, C], U8, align_bytes=64)
@@ -218,14 +219,13 @@ def tile_causalshapedattention_pa_kernel(tc, q, k, v, alpha, beta, gamma, out):
 
         def regroup_v(g):
             v_grouped[g] = wide.tile([P, C, PACK], BF16, tag="wide", name="v_grouped", align_bytes=64)
-            nc.gpsimd.tensor_scalar(
-                out=v_grouped[g][:],
-                in0=v_raw[:, g].rearrange("p t c -> p c t"),
-                scalar1=1.0,
-                scalar2=0.0,
-                op0=ALU.mult,
-                op1=ALU.add,
-            )
+            in_order = v_raw[:, g].rearrange("p t c -> p c t")
+            if g < 2:
+                nc.gpsimd.tensor_scalar(
+                    out=v_grouped[g][:], in0=in_order, scalar1=1.0, scalar2=0.0, op0=ALU.mult, op1=ALU.add
+                )
+            else:
+                nc.vector.tensor_copy(out=v_grouped[g][:], in_=in_order)
 
         def quantise_v(g):
             nc.vector.quantize_mx(
@@ -252,14 +252,14 @@ def tile_causalshapedattention_pa_kernel(tc, q, k, v, alpha, beta, gamma, out):
         def own_passes(qi):
             return range(qi // TILES_PER_PASS + 1)
 
-        def score_pass(qi, h, g):
-            if g == 0:
-                exps[(qi, h)] = score_pool.tile([P, 2, HALF], F32, tag="e", name="e")
-                pass_maxes[(qi, h)] = stats.tile([P, PASSES], F32, tag="pass_max", name="pass_max")
+        score_banks = {}
+
+        def multiply_scores(qi, h, g):
             last_pass = qi // TILES_PER_PASS
             before = (qi % TILES_PER_PASS) * TILE_COLS
             q_cols = slice(qi * P, (qi + 1) * P)
-            s_ps = psum_scores.tile([P, 2, PASS_COLS], F32, tag="scores")
+            s_ps = psum_scores.tile([P, 2, PASS_COLS], F32, tag="scores", name="s_ps")
+            score_banks[(qi, h, g)] = s_ps
             first = g * PASS_COLS
             width = PASS_COLS if g < last_pass else before
             if width > 0:
@@ -288,10 +288,16 @@ def tile_causalshapedattention_pa_kernel(tc, q, k, v, alpha, beta, gamma, out):
                     start=False,
                     stop=True,
                 )
-                width = before + TILE_COLS
+
+        def drain_scores(qi, h, g):
+            if g == 0:
+                exps[(qi, h)] = score_pool.tile([P, 2, HALF], F32, tag="e", name="e")
+                pass_maxes[(qi, h)] = stats.tile([P, PASSES], F32, tag="pass_max", name="pass_max")
+            first = g * PASS_COLS
+            width = min(PASS_COLS, (qi + 1) * TILE_COLS - first)
             nc.vector.tensor_scalar(
                 out=exps[(qi, h)][:, :, first : first + width],
-                in0=s_ps[:, :, :width],
+                in0=score_banks[(qi, h, g)][:, :, :width],
                 scalar1=1.0 / 16.0,
                 scalar2=None,
                 op0=ALU.mult,
@@ -326,18 +332,23 @@ def tile_causalshapedattention_pa_kernel(tc, q, k, v, alpha, beta, gamma, out):
             inv_sums[qi] = stats.tile([P, HEADS], F32, tag="inv_sum", name="inv_sum")
             nc.vector.reciprocal(out=inv_sums[qi][:], in_=row_sums[qi][:])
 
-        def gain_of(qi):
+        def gain_of(qi, engine):
             gains[qi] = stats.tile([P, HEADS], F32, tag="gain", name="gain")
-            nc.vector.tensor_scalar(
-                out=gains[qi][:], in0=inv_sums[qi][:], scalar1=beta_f[:, 0:1], scalar2=None, op0=ALU.mult
+            engine.tensor_scalar(
+                out=gains[qi][:],
+                in0=inv_sums[qi][:],
+                scalar1=beta_f[:, 0:1],
+                scalar2=0.0,
+                op0=ALU.mult,
+                op1=ALU.add,
             )
 
-        def scale_low(qi, h):
+        def scale_low(qi, h, engine):
             if h == 0:
                 a_tiles[qi] = a_pool.tile([P, 2 * HEADS, HALF], BF16, tag="a", name="a", align_bytes=64)
             below = qi * TILE_COLS
             if below > 0:
-                nc.vector.tensor_scalar(
+                engine.tensor_scalar(
                     out=a_tiles[qi][:, 2 * h : 2 * h + 2, :below],
                     in0=exps[(qi, h)][:, :, :below],
                     scalar1=gains[qi][:, h : h + 1],
@@ -352,7 +363,7 @@ def tile_causalshapedattention_pa_kernel(tc, q, k, v, alpha, beta, gamma, out):
                 out=a_tiles[qi][:, 2 * h : 2 * h + 2, block],
                 in0=exps[(qi, h)][:, :, block],
                 scalar=gains[qi][:, h : h + 1],
-                in1=diag_add[:, qi, :].rearrange("p (u x) -> p u x", u=2),
+                in1=diag_adds[qi][:].rearrange("p (u x) -> p u x", u=2),
                 op0=ALU.mult,
                 op1=ALU.add,
             )
@@ -395,18 +406,19 @@ def tile_causalshapedattention_pa_kernel(tc, q, k, v, alpha, beta, gamma, out):
             a_codes[(qi, g)] = (codes, scales)
 
         def make_above(first):
-            spread = psum_turn.tile([P, K_PASS], F32, tag="turn")
+            spread = psum_turn.tile([P, K_PASS, 2], BF16, tag="turn", name="spread")
             for j in range(TILES_PER_PASS):
                 nc.tensor.matmul(
-                    out=spread[:, j * P : (j + 1) * P],
+                    out=spread[:, j * P : (j + 1) * P, :],
                     lhsT=mc_above_bf[:, first + j : first + j + 1].to_broadcast([P, P]),
-                    rhs=ident_bf[:],
+                    rhs=ident_bf[:].unsqueeze(2).to_broadcast([P, P, 2]),
                     start=True,
                     stop=True,
                 )
             above_grouped[first] = wide.tile([P, K_PASS, PACK], BF16, tag="wide", name="above_grouped", align_bytes=64)
             nc.scalar.copy(
-                out=above_grouped[first][:], in_=spread[:].unsqueeze(2).to_broadcast([P, K_PASS, PACK])
+                out=above_grouped[first][:].rearrange("p x t -> p (x t)").bitcast(F32).rearrange("p (x u) -> p x u", u=2),
+                in_=spread[:].rearrange("p x u -> p (x u)").bitcast(F32).unsqueeze(2).to_broadcast([P, K_PASS, 2]),
             )
 
         def quantise_above(first):
@@ -440,66 +452,92 @@ def tile_causalshapedattention_pa_kernel(tc, q, k, v, alpha, beta, gamma, out):
 
         def store(qi):
             o_sb = out_pool.tile([P, C], F32, tag="o_sb")
-            nc.scalar.copy(out=o_sb[:], in_=o_tiles[qi][:].rearrange("p h d -> p (h d)"))
+            nc.vector.tensor_copy(out=o_sb[:], in_=o_tiles[qi][:].rearrange("p h d -> p (h d)"))
             nc.sync.dma_start(out=out_rows[qi * P : (qi + 1) * P, :], in_=o_sb[:])
 
-        order = list(range(TILES - 1, -1, -1))
+        def in_work(step):
+            return ORDER[step] if 0 <= step < TILES else None
 
-        def in_work(step, lag):
-            return order[step - lag] if 0 <= step - lag < TILES else None
+        def banks_of(qi):
+            return [] if qi is None else [(qi, h, g) for h in range(HEADS) for g in own_passes(qi)]
 
-        turn_q(order[0])
+        all_banks = [bank for qi in ORDER for bank in banks_of(qi)]
+        progress = {"multiplied": 0, "drained": 0}
+
+        def multiply_ahead(limit):
+            while progress["multiplied"] < min(limit, progress["drained"] + SCORE_BANKS):
+                multiply_scores(*all_banks[progress["multiplied"]])
+                progress["multiplied"] += 1
+
         turn_keys(0)
-        turn_q(order[1])
-        for g in range(PASSES):
-            regroup_v(g)
+        turn_q(ORDER[0])
+        turn_q(ORDER[1])
+        regroup_v(0)
+        regroup_v(1)
+        known = len(banks_of(ORDER[0]))
+        multiply_ahead(known)
         for step in range(TILES + 3):
-            new = in_work(step, 0)
-            mid = in_work(step, 1)
-            ripe = in_work(step, 2)
-            old = in_work(step, 3)
+            new = in_work(step)
+            mid = in_work(step - 1)
+            ripe = in_work(step - 2)
+            old = in_work(step - 3)
+            known += len(banks_of(in_work(step + 1)))
 
-            if new is not None:
-                for g in own_passes(new):
-                    if step == 0 and g + 1 < PASSES:
-                        turn_keys(g + 1)
-                    score_pass(new, 0, g)
-            if mid is not None:
-                invert_sum(mid)
-            if new is not None:
-                row_max(new, 0)
-                exponent(new, 0)
-            if mid is not None:
-                gain_of(mid)
-            if step + 2 < TILES:
-                turn_q(order[step + 2])
-            if old is not None:
-                for g in own_passes(old):
-                    quantise(old, g)
-            if 1 <= step <= U_TILES // TILES_PER_PASS:
-                quantise_above(U_TILES - step * TILES_PER_PASS)
-            if new is not None:
-                for g in own_passes(new):
-                    score_pass(new, 1, g)
-            if mid is not None:
-                scale_low(mid, 0)
-            if new is not None:
-                row_max(new, 1)
-                exponent(new, 1)
-            if mid is not None:
-                scale_diag(mid, 0)
-                scale_low(mid, 1)
-                scale_diag(mid, 1)
-                fill_above(mid)
+            if in_work(step + 2) is not None:
+                turn_q(in_work(step + 2))
             if ripe is not None:
                 for g in own_passes(ripe):
                     turn(ripe, g)
                     regroup(ripe, g)
-            if old is not None:
-                attend(old)
-                store(old)
+            if step + 1 < PASSES:
+                turn_keys(step + 1)
+            if 1 <= step <= U_TILES // TILES_PER_PASS:
+                make_above((step - 1) * TILES_PER_PASS)
+
+            multiply_ahead(known)
+            drains = banks_of(new)
+            helper = nc.vector if step == 1 else nc.gpsimd
+            for i in range(max(len(drains), 2)):
+                if i < len(drains):
+                    drain_scores(*drains[i])
+                    progress["drained"] += 1
+                    multiply_ahead(known)
+                if i == 0 and old is not None:
+                    store(old)
+                if i == 1 and mid is not None:
+                    invert_sum(mid)
+                    gain_of(mid, helper)
+                    if step > 1:
+                        for h in range(HEADS):
+                            scale_low(mid, h, helper)
+                if new is not None and i == len(drains) // 2:
+                    row_max(new, 0)
+                    exponent(new, 0)
+            if step == 0:
+                take_scalars()
+            if mid is not None:
+                diag_addend(mid)
+            if new is not None:
+                row_max(new, 1)
+                exponent(new, 1)
             if step == 1:
-                for g in range(PASSES):
-                    quantise_v(g)
-            if step < U_TILES // TILES_PER_PASS:
-                make_above(U_TILES - (step + 1) * TILES_PER_PASS)
+                quantise_v(0)
+                quantise_v(1)
+            if step == 2:
+                quantise_v(2)
+                quantise_v(3)
+            if 2 <= step <= 1 + U_TILES // TILES_PER_PASS:
+                quantise_above((step - 2) * TILES_PER_PASS)
+            if ripe is not None:
+                for g in own_passes(ripe):
+                    quantise(ripe, g)
+                attend(ripe)
+            if mid is not None:
+                for h in range(HEADS):
+                    if step == 1:
+                        scale_low(mid, h, nc.vector)
+                    scale_diag(mid, h)
+                fill_above(mid)
+            if step == 1:
+                regroup_v(2)
+                regroup_v(3)

@@ -80,15 +80,14 @@ def tile_causalshapedattention_pa_kernel(tc, q, k, v, alpha, beta, gamma, out):
         load_k(0)
         load_k(1)
         load_q(slice(7, TILES, 4))
+        load_k(2)
         load_v(0)
         nc.sync.dma_start(out=gamma_bf[:], in_=gamma.partition_broadcast(P))
         nc.sync.dma_start(out=alpha_bf[:], in_=alpha.partition_broadcast(P))
         nc.sync.dma_start(out=beta_bf[:], in_=beta.partition_broadcast(P))
-        load_v(1)
-        load_k(2)
-        load_v(2)
         load_k(3)
-        load_v(3)
+        for g in range(1, PASSES):
+            load_v(g)
         for g in range(PASSES - 1, -1, -1):
             load_q(slice(g * TILES_PER_PASS, (g + 1) * TILES_PER_PASS - 1))
 
@@ -194,11 +193,11 @@ def tile_causalshapedattention_pa_kernel(tc, q, k, v, alpha, beta, gamma, out):
         q_t = keep.tile([P, D_BLOCKS, T], BF16)
         k_t = keep.tile([P, D_BLOCKS, 2, HALF], BF16)
 
-        def turn_q(t):
+        def turn_q(t, copy_out=nc.scalar.copy):
             turned = psum_turn.tile([P, D_BLOCKS, P], BF16, tag="turn")
             for b in range(D_BLOCKS):
                 nc.tensor.transpose(turned[:, b, :], q_sb[:, t, b * P : (b + 1) * P], ident_bf[:])
-            nc.scalar.copy(out=q_t[:, :, t * P : (t + 1) * P], in_=turned[:])
+            copy_out(out=q_t[:, :, t * P : (t + 1) * P], in_=turned[:])
 
         def turn_keys(g):
             for t in range(g * TILES_PER_PASS, (g + 1) * TILES_PER_PASS):
@@ -207,7 +206,7 @@ def tile_causalshapedattention_pa_kernel(tc, q, k, v, alpha, beta, gamma, out):
                     nc.tensor.transpose(
                         turned[:, b, :], k_sb[:, t, b * P : (b + 1) * P], ident_halves_bf[:]
                     )
-                copy_out = nc.scalar.copy if t % 2 == 0 else nc.vector.tensor_copy
+                copy_out = nc.scalar.copy if t % 2 == 0 or t >= 2 * TILES_PER_PASS else nc.vector.tensor_copy
                 copy_out(
                     out=k_t[:, :, :, t * TILE_COLS : (t + 1) * TILE_COLS],
                     in_=turned[:].rearrange("p b (u x) -> p b u x", u=2),
@@ -217,15 +216,17 @@ def tile_causalshapedattention_pa_kernel(tc, q, k, v, alpha, beta, gamma, out):
         v_scales = keep.tile([P, PASSES, C], U8, align_bytes=64)
         v_grouped = {}
 
-        def regroup_v(g):
+        def regroup_v(g, engine):
             v_grouped[g] = wide.tile([P, C, PACK], BF16, tag="wide", name="v_grouped", align_bytes=64)
-            in_order = v_raw[:, g].rearrange("p t c -> p c t")
-            if g < 2:
-                nc.gpsimd.tensor_scalar(
-                    out=v_grouped[g][:], in0=in_order, scalar1=1.0, scalar2=0.0, op0=ALU.mult, op1=ALU.add
+            for c in range(0, C, P):
+                engine.tensor_scalar(
+                    out=v_grouped[g][:, c : c + P, :],
+                    in0=v_raw[:, g, :, c : c + P].rearrange("p t c -> p c t"),
+                    scalar1=1.0,
+                    scalar2=0.0,
+                    op0=ALU.mult,
+                    op1=ALU.add,
                 )
-            else:
-                nc.vector.tensor_copy(out=v_grouped[g][:], in_=in_order)
 
         def quantise_v(g):
             nc.vector.quantize_mx(
@@ -452,7 +453,7 @@ def tile_causalshapedattention_pa_kernel(tc, q, k, v, alpha, beta, gamma, out):
 
         def store(qi):
             o_sb = out_pool.tile([P, C], F32, tag="o_sb")
-            nc.vector.tensor_copy(out=o_sb[:], in_=o_tiles[qi][:].rearrange("p h d -> p (h d)"))
+            nc.scalar.copy(out=o_sb[:], in_=o_tiles[qi][:].rearrange("p h d -> p (h d)"))
             nc.sync.dma_start(out=out_rows[qi * P : (qi + 1) * P, :], in_=o_sb[:])
 
         def in_work(step):
@@ -469,75 +470,83 @@ def tile_causalshapedattention_pa_kernel(tc, q, k, v, alpha, beta, gamma, out):
                 multiply_scores(*all_banks[progress["multiplied"]])
                 progress["multiplied"] += 1
 
+        for g in range(PASSES):
+            regroup_v(g, nc.gpsimd)
         turn_keys(0)
         turn_q(ORDER[0])
-        turn_q(ORDER[1])
-        regroup_v(0)
-        regroup_v(1)
         known = len(banks_of(ORDER[0]))
         multiply_ahead(known)
+        waiting_q = ORDER[2:]
+        def work_scores():
+            drains = banks_of(new)
+            for i in range(len(drains)):
+                drain_scores(*drains[i])
+                progress["drained"] += 1
+                multiply_ahead(known)
+                if i == len(drains) // 2:
+                    row_max(new, 0)
+                    exponent(new, 0)
+            if new is not None:
+                row_max(new, 1)
+                exponent(new, 1)
+
         for step in range(TILES + 3):
             new = in_work(step)
             mid = in_work(step - 1)
             ripe = in_work(step - 2)
             old = in_work(step - 3)
             known += len(banks_of(in_work(step + 1)))
+            if step == 0:
+                turn_q(ORDER[1])
+                for h, g in [(h, g) for h in range(HEADS) for g in own_passes(new)]:
+                    drain_scores(new, h, g)
+                    progress["drained"] += 1
+                for h in range(HEADS):
+                    row_max(new, h)
+                turn_keys(1)
+                for h in range(HEADS):
+                    exponent(new, h)
 
-            if in_work(step + 2) is not None:
-                turn_q(in_work(step + 2))
             if ripe is not None:
                 for g in own_passes(ripe):
                     turn(ripe, g)
                     regroup(ripe, g)
-            if step + 1 < PASSES:
-                turn_keys(step + 1)
-            if 1 <= step <= U_TILES // TILES_PER_PASS:
-                make_above((step - 1) * TILES_PER_PASS)
-
+            if 2 <= step <= 1 + U_TILES // TILES_PER_PASS:
+                make_above((step - 2) * TILES_PER_PASS)
+            if step == 2:
+                quantise_v(0)
+                quantise_v(1)
+            if step == 3:
+                quantise_v(2)
+                quantise_v(3)
+            if 3 <= step <= 2 + U_TILES // TILES_PER_PASS:
+                quantise_above((step - 3) * TILES_PER_PASS)
+            if old is not None:
+                for g in own_passes(old):
+                    quantise(old, g)
+                attend(old)
             multiply_ahead(known)
-            drains = banks_of(new)
-            helper = nc.vector if step == 1 else nc.gpsimd
-            for i in range(max(len(drains), 2)):
-                if i < len(drains):
-                    drain_scores(*drains[i])
-                    progress["drained"] += 1
-                    multiply_ahead(known)
-                if i == 0 and old is not None:
-                    store(old)
-                if i == 1 and mid is not None:
-                    invert_sum(mid)
-                    gain_of(mid, helper)
-                    if step > 1:
-                        for h in range(HEADS):
-                            scale_low(mid, h, helper)
-                if new is not None and i == len(drains) // 2:
-                    row_max(new, 0)
-                    exponent(new, 0)
+            if step + 2 < PASSES:
+                turn_keys(step + 2)
+            for qi in waiting_q[: [1, 2, 3, 4, 4, 4][min(step, 5)]]:
+                turn_q(qi, nc.scalar.copy)
+            waiting_q = waiting_q[[1, 2, 3, 4, 4, 4][min(step, 5)] :]
             if step == 0:
                 take_scalars()
             if mid is not None:
-                diag_addend(mid)
-            if new is not None:
-                row_max(new, 1)
-                exponent(new, 1)
-            if step == 1:
-                quantise_v(0)
-                quantise_v(1)
-            if step == 2:
-                quantise_v(2)
-                quantise_v(3)
-            if 2 <= step <= 1 + U_TILES // TILES_PER_PASS:
-                quantise_above((step - 2) * TILES_PER_PASS)
-            if ripe is not None:
-                for g in own_passes(ripe):
-                    quantise(ripe, g)
-                attend(ripe)
+                invert_sum(mid)
+                gain_of(mid, nc.vector if step <= 1 else nc.gpsimd)
+                if step > 1:
+                    for h in range(HEADS):
+                        scale_low(mid, h, nc.gpsimd)
+            if old is not None:
+                store(old)
+            if step > 0:
+                work_scores()
             if mid is not None:
+                diag_addend(mid)
                 for h in range(HEADS):
-                    if step == 1:
+                    if step <= 1:
                         scale_low(mid, h, nc.vector)
                     scale_diag(mid, h)
                 fill_above(mid)
-            if step == 1:
-                regroup_v(2)
-                regroup_v(3)

@@ -196,15 +196,25 @@ def tile_causalshapedattention_pa_kernel(tc, q, k, v, alpha, beta, gamma, out):
         def turn_q(t, copy_out=nc.scalar.copy):
             turned = psum_turn.tile([P, D_BLOCKS, P], BF16, tag="turn")
             for b in range(D_BLOCKS):
-                nc.tensor.transpose(turned[:, b, :], q_sb[:, t, b * P : (b + 1) * P], ident_bf[:])
+                nc.tensor.matmul(
+                    out=turned[:, b, :],
+                    lhsT=q_sb[:, t, b * P : (b + 1) * P],
+                    rhs=ident_bf[:],
+                    start=True,
+                    stop=True,
+                )
             copy_out(out=q_t[:, :, t * P : (t + 1) * P], in_=turned[:])
 
         def turn_keys(g):
             for t in range(g * TILES_PER_PASS, (g + 1) * TILES_PER_PASS):
                 turned = psum_turn.tile([P, D_BLOCKS, P], BF16, tag="turn")
                 for b in range(D_BLOCKS):
-                    nc.tensor.transpose(
-                        turned[:, b, :], k_sb[:, t, b * P : (b + 1) * P], ident_halves_bf[:]
+                    nc.tensor.matmul(
+                        out=turned[:, b, :],
+                        lhsT=k_sb[:, t, b * P : (b + 1) * P],
+                        rhs=ident_halves_bf[:],
+                        start=True,
+                        stop=True,
                     )
                 copy_out = nc.scalar.copy if t % 2 == 0 or t >= 2 * TILES_PER_PASS else nc.vector.tensor_copy
                 copy_out(
@@ -483,12 +493,21 @@ def tile_causalshapedattention_pa_kernel(tc, q, k, v, alpha, beta, gamma, out):
                 drain_scores(*drains[i])
                 progress["drained"] += 1
                 multiply_ahead(known)
+                turn_some(1)
                 if i == len(drains) // 2:
                     row_max(new, 0)
                     exponent(new, 0)
             if new is not None:
                 row_max(new, 1)
                 exponent(new, 1)
+
+        pending_turns = []
+
+        def turn_some(count):
+            for i in range(min(count, len(pending_turns))):
+                qi, g = pending_turns.pop(0)
+                turn(qi, g)
+                regroup(qi, g)
 
         for step in range(TILES + 3):
             new = in_work(step)
@@ -507,10 +526,8 @@ def tile_causalshapedattention_pa_kernel(tc, q, k, v, alpha, beta, gamma, out):
                 for h in range(HEADS):
                     exponent(new, h)
 
-            if ripe is not None:
-                for g in own_passes(ripe):
-                    turn(ripe, g)
-                    regroup(ripe, g)
+            pending_turns.extend([] if ripe is None else [(ripe, g) for g in own_passes(ripe)])
+            turn_some(3)
             if 2 <= step <= 1 + U_TILES // TILES_PER_PASS:
                 make_above((step - 2) * TILES_PER_PASS)
             if step == 2:
@@ -528,9 +545,9 @@ def tile_causalshapedattention_pa_kernel(tc, q, k, v, alpha, beta, gamma, out):
             multiply_ahead(known)
             if step + 2 < PASSES:
                 turn_keys(step + 2)
-            for qi in waiting_q[: [1, 2, 3, 4, 4, 4][min(step, 5)]]:
+            for qi in waiting_q[: [1, 1, 2, 2, 2, 2][min(step, 5)]]:
                 turn_q(qi, nc.scalar.copy)
-            waiting_q = waiting_q[[1, 2, 3, 4, 4, 4][min(step, 5)] :]
+            waiting_q = waiting_q[[1, 1, 2, 2, 2, 2][min(step, 5)] :]
             if step == 0:
                 take_scalars()
             if mid is not None:
@@ -543,6 +560,7 @@ def tile_causalshapedattention_pa_kernel(tc, q, k, v, alpha, beta, gamma, out):
                 store(old)
             if step > 0:
                 work_scores()
+            turn_some(PASSES)
             if mid is not None:
                 diag_addend(mid)
                 for h in range(HEADS):

@@ -30,6 +30,7 @@ D_BLOCKS = C // P
 MASKED = -1.0e30
 SCORE_BANKS = 4
 ORDER = [3, 7, 11, 15, 14, 13, 12, 10, 9, 8, 6, 5, 4, 2, 1, 0]
+OUT_IN_TURN = ORDER[-3::2]
 U_TILES = TILES - TILES_PER_PASS
 
 FLOPS = 2 * 2 * T * T * D * HEADS
@@ -246,8 +247,8 @@ def tile_causalshapedattention_pa_kernel(tc, q, k, v, alpha, beta, gamma, out):
             )
 
         exps = {}
-        pass_maxes = {}
-        neg_maxes = {}
+        pass_mins = {}
+        row_mins = {}
         row_sums = {}
         gains = {}
         inv_sums = {}
@@ -272,28 +273,20 @@ def tile_causalshapedattention_pa_kernel(tc, q, k, v, alpha, beta, gamma, out):
             s_ps = psum_scores.tile([P, 2, PASS_COLS], F32, tag="scores", name="s_ps")
             score_banks[(qi, h, g)] = s_ps
             first = g * PASS_COLS
-            width = PASS_COLS if g < last_pass else before
-            if width > 0:
-                for b in range(2):
-                    nc.tensor.matmul(
-                        out=s_ps[:, :, :width],
-                        lhsT=q_t[:, 2 * h + b, q_cols],
-                        rhs=k_t[:, 2 * h + b, :, first : first + width],
-                        start=(b == 0),
-                        stop=(b == 1),
-                    )
+            width = PASS_COLS
             if g == last_pass:
-                diag = slice(before, before + TILE_COLS)
-                for b in range(2):
-                    nc.tensor.matmul(
-                        out=s_ps[:, :, diag],
-                        lhsT=q_t[:, 2 * h + b, q_cols],
-                        rhs=k_t[:, 2 * h + b, :, qi * TILE_COLS : (qi + 1) * TILE_COLS],
-                        start=(b == 0),
-                        stop=False,
-                    )
+                width = before + TILE_COLS
+            for b in range(2):
                 nc.tensor.matmul(
-                    out=s_ps[:, :, diag],
+                    out=s_ps[:, :, :width],
+                    lhsT=q_t[:, 2 * h + b, q_cols],
+                    rhs=k_t[:, 2 * h + b, :, first : first + width],
+                    start=(b == 0),
+                    stop=(b == 1 and g < last_pass),
+                )
+            if g == last_pass:
+                nc.tensor.matmul(
+                    out=s_ps[:, :, before : before + TILE_COLS],
                     lhsT=ident_bf[:],
                     rhs=masked_bf[:].rearrange("p (u x) -> p u x", u=2),
                     start=False,
@@ -303,27 +296,33 @@ def tile_causalshapedattention_pa_kernel(tc, q, k, v, alpha, beta, gamma, out):
         def drain_scores(qi, h, g):
             if g == 0:
                 exps[(qi, h)] = score_pool.tile([P, 2, HALF], F32, tag="e", name="e")
-                pass_maxes[(qi, h)] = stats.tile([P, PASSES], F32, tag="pass_max", name="pass_max")
+                pass_mins[(qi, h)] = stats.tile([P, PASSES], F32, tag="pass_min", name="pass_min")
             first = g * PASS_COLS
             width = min(PASS_COLS, (qi + 1) * TILE_COLS - first)
             nc.vector.tensor_scalar(
                 out=exps[(qi, h)][:, :, first : first + width],
                 in0=score_banks[(qi, h, g)][:, :, :width],
-                scalar1=1.0 / 16.0,
-                scalar2=None,
+                scalar1=-1.0 / 16.0,
+                scalar2=pass_mins[(qi, h)][:, g - 1 : g] if g == 1 and not needs_row_min(qi) else None,
                 op0=ALU.mult,
-                op1=ALU.max,
-                accum_out=pass_maxes[(qi, h)][:, g : g + 1],
+                op1=ALU.min,
+                accum_out=pass_mins[(qi, h)][:, g : g + 1],
             )
 
-        def row_max(qi, h):
-            neg_maxes[(qi, h)] = stats.tile([P, 1], F32, tag="neg_max", name="neg_max")
+        def needs_row_min(qi):
+            return len(own_passes(qi)) > 2
+
+        def row_min(qi, h):
+            if not needs_row_min(qi):
+                last_pass = qi // TILES_PER_PASS
+                row_mins[(qi, h)] = pass_mins[(qi, h)][:, last_pass : last_pass + 1]
+                return
+            row_mins[(qi, h)] = stats.tile([P, 1], F32, tag="row_min", name="row_min")
             nc.vector.tensor_reduce(
-                out=neg_maxes[(qi, h)][:],
-                in_=pass_maxes[(qi, h)][:, : qi // TILES_PER_PASS + 1],
+                out=row_mins[(qi, h)][:],
+                in_=pass_mins[(qi, h)][:, : qi // TILES_PER_PASS + 1],
                 axis=AXIS.X,
-                op=ALU.max,
-                negate=True,
+                op=ALU.min,
             )
 
         def exponent(qi, h):
@@ -334,8 +333,8 @@ def tile_causalshapedattention_pa_kernel(tc, q, k, v, alpha, beta, gamma, out):
                 out=exps[(qi, h)][:, :, :seen],
                 in_=exps[(qi, h)][:, :, :seen],
                 func=ACT.Exp,
-                bias=neg_maxes[(qi, h)][:],
-                scale=1.0,
+                bias=row_mins[(qi, h)][:],
+                scale=-1.0,
                 accum_out=row_sums[qi][:, h : h + 1],
             )
 
@@ -441,7 +440,10 @@ def tile_causalshapedattention_pa_kernel(tc, q, k, v, alpha, beta, gamma, out):
             )
 
         def attend(qi):
-            o_tiles[qi] = psum_out.tile([P, HEADS, D], F32, tag="o", name="o_ps")
+            if qi in OUT_IN_TURN:
+                o_tiles[qi] = psum_turn.tile([P, HEADS, D], F32, tag="turn", name="o_ps")
+            else:
+                o_tiles[qi] = psum_out.tile([P, HEADS, D], F32, tag="o", name="o_ps")
             for h in range(HEADS):
                 for g in range(PASSES):
                     if g in own_passes(qi):
@@ -461,16 +463,20 @@ def tile_causalshapedattention_pa_kernel(tc, q, k, v, alpha, beta, gamma, out):
                         stop=(g == PASSES - 1),
                     )
 
-        def store(qi):
+        def store(qi, copy_out=nc.scalar.copy):
             o_sb = out_pool.tile([P, C], F32, tag="o_sb")
-            nc.scalar.copy(out=o_sb[:], in_=o_tiles[qi][:].rearrange("p h d -> p (h d)"))
+            copy_out(out=o_sb[:], in_=o_tiles[qi][:].rearrange("p h d -> p (h d)"))
             nc.sync.dma_start(out=out_rows[qi * P : (qi + 1) * P, :], in_=o_sb[:])
 
         def in_work(step):
             return ORDER[step] if 0 <= step < TILES else None
 
         def banks_of(qi):
-            return [] if qi is None else [(qi, h, g) for h in range(HEADS) for g in own_passes(qi)]
+            if qi is None:
+                return []
+            if needs_row_min(qi):
+                return [(qi, h, g) for h in range(HEADS) for g in own_passes(qi)]
+            return [(qi, h, g) for g in own_passes(qi) for h in range(HEADS)]
 
         all_banks = [bank for qi in ORDER for bank in banks_of(qi)]
         progress = {"multiplied": 0, "drained": 0}
@@ -494,11 +500,11 @@ def tile_causalshapedattention_pa_kernel(tc, q, k, v, alpha, beta, gamma, out):
                 progress["drained"] += 1
                 multiply_ahead(known)
                 turn_some(1)
-                if i == len(drains) // 2:
-                    row_max(new, 0)
+                if i == (len(drains) // 2 if needs_row_min(new) else len(drains) - 2):
+                    row_min(new, 0)
                     exponent(new, 0)
             if new is not None:
-                row_max(new, 1)
+                row_min(new, 1)
                 exponent(new, 1)
 
         pending_turns = []
@@ -521,7 +527,7 @@ def tile_causalshapedattention_pa_kernel(tc, q, k, v, alpha, beta, gamma, out):
                     drain_scores(new, h, g)
                     progress["drained"] += 1
                 for h in range(HEADS):
-                    row_max(new, h)
+                    row_min(new, h)
                 turn_keys(1)
                 for h in range(HEADS):
                     exponent(new, h)
@@ -566,5 +572,6 @@ def tile_causalshapedattention_pa_kernel(tc, q, k, v, alpha, beta, gamma, out):
                 for h in range(HEADS):
                     if step <= 1:
                         scale_low(mid, h, nc.vector)
+                for h in range(HEADS):
                     scale_diag(mid, h)
                 fill_above(mid)

@@ -46,7 +46,7 @@ def tile_causalshapedattention_pa_kernel(tc, q, k, v, alpha, beta, gamma, out):
     with ExitStack() as ctx:
         ctx.enter_context(tc.manual_schedule())
         keep = ctx.enter_context(tc.tile_pool(name="keep", bufs=1))
-        wide = ctx.enter_context(tc.tile_pool(name="wide", bufs=4))
+        wide = ctx.enter_context(tc.tile_pool(name="wide", bufs=7))
         stats = ctx.enter_context(tc.tile_pool(name="stats", bufs=6))
         score_pool = ctx.enter_context(tc.tile_pool(name="scores", bufs=6))
         a_pool = ctx.enter_context(tc.tile_pool(name="a", bufs=3))
@@ -488,8 +488,8 @@ def tile_causalshapedattention_pa_kernel(tc, q, k, v, alpha, beta, gamma, out):
 
         for g in range(PASSES):
             regroup_v(g, nc.gpsimd)
-        turn_keys(0)
         turn_q(ORDER[0])
+        turn_keys(0)
         known = len(banks_of(ORDER[0]))
         multiply_ahead(known)
         waiting_q = ORDER[2:]
@@ -503,6 +503,8 @@ def tile_causalshapedattention_pa_kernel(tc, q, k, v, alpha, beta, gamma, out):
                 if i == (len(drains) // 2 if needs_row_min(new) else len(drains) - 2):
                     row_min(new, 0)
                     exponent(new, 0)
+            if step > 0 and mid is not None:
+                diag_addend(mid)
             if new is not None:
                 row_min(new, 1)
                 exponent(new, 1)
@@ -534,8 +536,8 @@ def tile_causalshapedattention_pa_kernel(tc, q, k, v, alpha, beta, gamma, out):
 
             pending_turns.extend([] if ripe is None else [(ripe, g) for g in own_passes(ripe)])
             turn_some(3)
-            if 2 <= step <= 1 + U_TILES // TILES_PER_PASS:
-                make_above((step - 2) * TILES_PER_PASS)
+            for first in {1: [0], 2: [4], 3: [8]}.get(step, []):
+                make_above(first)
             if step == 2:
                 quantise_v(0)
                 quantise_v(1)
@@ -560,18 +562,19 @@ def tile_causalshapedattention_pa_kernel(tc, q, k, v, alpha, beta, gamma, out):
                 invert_sum(mid)
                 gain_of(mid, nc.vector if step <= 1 else nc.gpsimd)
                 if step > 1:
-                    for h in range(HEADS):
-                        scale_low(mid, h, nc.gpsimd)
-            if old is not None:
+                    scale_low(mid, 0, nc.gpsimd)
+            early = new is not None and needs_row_min(new)
+            if old is not None and early:
                 store(old)
             if step > 0:
                 work_scores()
+            if old is not None and not early:
+                store(old)
             turn_some(PASSES)
             if mid is not None:
-                diag_addend(mid)
                 for h in range(HEADS):
-                    if step <= 1:
+                    if step <= 1 or h == 1:
                         scale_low(mid, h, nc.vector)
+                fill_above(mid)
                 for h in range(HEADS):
                     scale_diag(mid, h)
-                fill_above(mid)

@@ -353,14 +353,13 @@ def tile_causalshapedattention_pa_kernel(tc, q, k, v, alpha, beta, gamma, out):
                 op1=ALU.add,
             )
 
-        def scale_low(qi, h, engine):
-            if h == 0:
+        def scale_low(qi, h, engine, cols):
+            if qi not in a_tiles:
                 a_tiles[qi] = a_pool.tile([P, 2 * HEADS, HALF], BF16, tag="a", name="a", align_bytes=64)
-            below = qi * TILE_COLS
-            if below > 0:
+            if cols.stop > cols.start:
                 engine.tensor_scalar(
-                    out=a_tiles[qi][:, 2 * h : 2 * h + 2, :below],
-                    in0=exps[(qi, h)][:, :, :below],
+                    out=a_tiles[qi][:, 2 * h : 2 * h + 2, cols],
+                    in0=exps[(qi, h)][:, :, cols],
                     scalar1=gains[qi][:, h : h + 1],
                     scalar2=mc_below[:, qi : qi + 1],
                     op0=ALU.mult,
@@ -468,6 +467,9 @@ def tile_causalshapedattention_pa_kernel(tc, q, k, v, alpha, beta, gamma, out):
             copy_out(out=o_sb[:], in_=o_tiles[qi][:].rearrange("p h d -> p (h d)"))
             nc.sync.dma_start(out=out_rows[qi * P : (qi + 1) * P, :], in_=o_sb[:])
 
+        def cut_of(qi):
+            return qi // 3
+
         def in_work(step):
             return ORDER[step] if 0 <= step < TILES else None
 
@@ -486,8 +488,8 @@ def tile_causalshapedattention_pa_kernel(tc, q, k, v, alpha, beta, gamma, out):
                 multiply_scores(*all_banks[progress["multiplied"]])
                 progress["multiplied"] += 1
 
-        for g in range(PASSES):
-            regroup_v(g, nc.gpsimd)
+        regroup_v(0, nc.gpsimd)
+        regroup_v(1, nc.gpsimd)
         turn_q(ORDER[0])
         turn_keys(0)
         known = len(banks_of(ORDER[0]))
@@ -562,7 +564,8 @@ def tile_causalshapedattention_pa_kernel(tc, q, k, v, alpha, beta, gamma, out):
                 invert_sum(mid)
                 gain_of(mid, nc.vector if step <= 1 else nc.gpsimd)
                 if step > 1:
-                    scale_low(mid, 0, nc.gpsimd)
+                    scale_low(mid, 0, nc.gpsimd, slice(0, mid * TILE_COLS))
+                    scale_low(mid, 1, nc.gpsimd, slice(0, cut_of(mid) * TILE_COLS))
             early = new is not None and needs_row_min(new)
             if old is not None and early:
                 store(old)
@@ -572,9 +575,14 @@ def tile_causalshapedattention_pa_kernel(tc, q, k, v, alpha, beta, gamma, out):
                 store(old)
             turn_some(PASSES)
             if mid is not None:
-                for h in range(HEADS):
-                    if step <= 1 or h == 1:
-                        scale_low(mid, h, nc.vector)
+                if step <= 1:
+                    scale_low(mid, 0, nc.vector, slice(0, mid * TILE_COLS))
+                    scale_low(mid, 1, nc.vector, slice(0, mid * TILE_COLS))
+                else:
+                    scale_low(mid, 1, nc.vector, slice(cut_of(mid) * TILE_COLS, mid * TILE_COLS))
                 fill_above(mid)
                 for h in range(HEADS):
                     scale_diag(mid, h)
+            if step == 1:
+                regroup_v(2, nc.vector)
+                regroup_v(3, nc.vector)

@@ -79,16 +79,18 @@ def tile_causalshapedattention_pa_kernel(tc, q, k, v, alpha, beta, gamma, out):
 
         load_q(slice(3, 4))
         load_k(0)
+        load_q(slice(7, 8))
         load_k(1)
-        load_q(slice(7, TILES, 4))
-        load_k(2)
-        load_v(0)
         nc.sync.dma_start(out=gamma_bf[:], in_=gamma.partition_broadcast(P))
         nc.sync.dma_start(out=alpha_bf[:], in_=alpha.partition_broadcast(P))
         nc.sync.dma_start(out=beta_bf[:], in_=beta.partition_broadcast(P))
+        load_v(0)
+        load_v(1)
+        load_k(2)
+        load_q(slice(11, TILES, 4))
         load_k(3)
-        for g in range(1, PASSES):
-            load_v(g)
+        load_v(2)
+        load_v(3)
         for g in range(PASSES - 1, -1, -1):
             load_q(slice(g * TILES_PER_PASS, (g + 1) * TILES_PER_PASS - 1))
 
@@ -361,7 +363,7 @@ def tile_causalshapedattention_pa_kernel(tc, q, k, v, alpha, beta, gamma, out):
                     out=a_tiles[qi][:, 2 * h : 2 * h + 2, cols],
                     in0=exps[(qi, h)][:, :, cols],
                     scalar1=gains[qi][:, h : h + 1],
-                    scalar2=mc_below[:, qi : qi + 1],
+                    scalar2=mc_below[:, qi : qi + 1] if qi == TILES - 1 else 0.0,
                     op0=ALU.mult,
                     op1=ALU.add,
                 )

@@ -441,33 +441,57 @@ def tile_causalshapedattention_pa_kernel(tc, q, k, v, alpha, beta, gamma, out):
             )
 
         def attend(qi):
+            above_passes = list(range(qi // TILES_PER_PASS + 1, PASSES))
+            passes = above_passes + list(own_passes(qi))
+
+            def multiply(h, g, out):
+                if g in above_passes:
+                    lhs_codes = above_codes[:, qi * P : (qi + 1) * P]
+                    lhs_scales = above_scales[:, qi * P : (qi + 1) * P]
+                else:
+                    codes, scales = a_codes[(qi, g)]
+                    lhs_codes = codes[:, h * P : (h + 1) * P]
+                    lhs_scales = scales[:, h * P : (h + 1) * P]
+                nc.tensor.matmul_mx(
+                    out=out,
+                    lhsT=lhs_codes.bitcast(FP8X4),
+                    lhsT_scale=lhs_scales,
+                    rhs=v_codes[:, g, h * D : (h + 1) * D].bitcast(FP8X4),
+                    rhs_scale=v_scales[:, g, h * D : (h + 1) * D],
+                    start=(g == passes[0]),
+                    stop=(g == passes[-1]),
+                )
+
+            if qi == ORDER[-1]:
+                halves = [
+                    psum_turn.tile([P, D], F32, tag="turn", name="o_first"),
+                    psum_turn.tile([P, D], F32, tag="turn", name="o_second"),
+                ]
+                for group in (above_passes, own_passes(qi)):
+                    for h in range(HEADS):
+                        for g in group:
+                            multiply(h, g, halves[h][:])
+                o_tiles[qi] = halves
+                return
             if qi in OUT_IN_TURN:
                 o_tiles[qi] = psum_turn.tile([P, HEADS, D], F32, tag="turn", name="o_ps")
             else:
                 o_tiles[qi] = psum_out.tile([P, HEADS, D], F32, tag="o", name="o_ps")
             for h in range(HEADS):
-                for g in range(PASSES):
-                    if g in own_passes(qi):
-                        codes, scales = a_codes[(qi, g)]
-                        lhs_codes = codes[:, h * P : (h + 1) * P]
-                        lhs_scales = scales[:, h * P : (h + 1) * P]
-                    else:
-                        lhs_codes = above_codes[:, qi * P : (qi + 1) * P]
-                        lhs_scales = above_scales[:, qi * P : (qi + 1) * P]
-                    nc.tensor.matmul_mx(
-                        out=o_tiles[qi][:, h, :],
-                        lhsT=lhs_codes.bitcast(FP8X4),
-                        lhsT_scale=lhs_scales,
-                        rhs=v_codes[:, g, h * D : (h + 1) * D].bitcast(FP8X4),
-                        rhs_scale=v_scales[:, g, h * D : (h + 1) * D],
-                        start=(g == 0),
-                        stop=(g == PASSES - 1),
-                    )
+                for g in passes:
+                    multiply(h, g, o_tiles[qi][:, h, :])
 
-        def store(qi, copy_out=nc.scalar.copy):
+        def store(qi):
             o_sb = out_pool.tile([P, C], F32, tag="o_sb")
-            copy_out(out=o_sb[:], in_=o_tiles[qi][:].rearrange("p h d -> p (h d)"))
-            nc.sync.dma_start(out=out_rows[qi * P : (qi + 1) * P, :], in_=o_sb[:])
+            rows = out_rows[qi * P : (qi + 1) * P, :]
+            if qi == ORDER[-1]:
+                for h, copy_out in enumerate((nc.vector.tensor_copy, nc.scalar.copy)):
+                    cols = slice(h * D, (h + 1) * D)
+                    copy_out(out=o_sb[:, cols], in_=o_tiles[qi][h][:])
+                    nc.sync.dma_start(out=rows[:, cols], in_=o_sb[:, cols])
+                return
+            nc.scalar.copy(out=o_sb[:], in_=o_tiles[qi][:].rearrange("p h d -> p (h d)"))
+            nc.sync.dma_start(out=rows, in_=o_sb[:])
 
         def cut_of(qi):
             return qi // 3
@@ -497,6 +521,13 @@ def tile_causalshapedattention_pa_kernel(tc, q, k, v, alpha, beta, gamma, out):
         known = len(banks_of(ORDER[0]))
         multiply_ahead(known)
         waiting_q = ORDER[2:]
+
+        def turn_inputs(step):
+            if step + 2 < PASSES:
+                turn_keys(step + 2)
+            for j in range(min(1 if step < 2 else 2, len(waiting_q))):
+                turn_q(waiting_q.pop(0))
+
         def work_scores():
             drains = banks_of(new)
             for i in range(len(drains)):
@@ -540,7 +571,7 @@ def tile_causalshapedattention_pa_kernel(tc, q, k, v, alpha, beta, gamma, out):
 
             pending_turns.extend([] if ripe is None else [(ripe, g) for g in own_passes(ripe)])
             turn_some(3)
-            for first in {1: [0], 2: [4], 3: [8]}.get(step, []):
+            for first in {2: [0, 4], 3: [8]}.get(step, []):
                 make_above(first)
             if step == 2:
                 quantise_v(0)
@@ -555,24 +586,23 @@ def tile_causalshapedattention_pa_kernel(tc, q, k, v, alpha, beta, gamma, out):
                     quantise(old, g)
                 attend(old)
             multiply_ahead(known)
-            if step + 2 < PASSES:
-                turn_keys(step + 2)
-            for qi in waiting_q[: [1, 1, 2, 2, 2, 2][min(step, 5)]]:
-                turn_q(qi, nc.scalar.copy)
-            waiting_q = waiting_q[[1, 1, 2, 2, 2, 2][min(step, 5)] :]
+            if not (step == 1):
+                turn_inputs(step)
             if step == 0:
                 take_scalars()
             if mid is not None:
                 invert_sum(mid)
-                gain_of(mid, nc.vector if step <= 1 else nc.gpsimd)
+                gain_of(mid, nc.vector if step <= 1 or mid == ORDER[-1] else nc.gpsimd)
                 if step > 1:
                     scale_low(mid, 0, nc.gpsimd, slice(0, mid * TILE_COLS))
                     scale_low(mid, 1, nc.gpsimd, slice(0, cut_of(mid) * TILE_COLS))
-            early = new is not None and needs_row_min(new)
+            early = new is not None and new >= TILES_PER_PASS
             if old is not None and early:
                 store(old)
             if step > 0:
                 work_scores()
+            if step == 1:
+                turn_inputs(step)
             if old is not None and not early:
                 store(old)
             turn_some(PASSES)

@@ -50,8 +50,8 @@ def tile_causalshapedattention_pa_kernel(tc, q, k, v, alpha, beta, gamma, out):
         stats = ctx.enter_context(tc.tile_pool(name="stats", bufs=6))
         score_pool = ctx.enter_context(tc.tile_pool(name="scores", bufs=6))
         a_pool = ctx.enter_context(tc.tile_pool(name="a", bufs=3))
-        grouped_pool = ctx.enter_context(tc.tile_pool(name="grouped", bufs=5))
-        code_pool = ctx.enter_context(tc.tile_pool(name="codes", bufs=10))
+        grouped_pool = ctx.enter_context(tc.tile_pool(name="grouped", bufs=4))
+        code_pool = ctx.enter_context(tc.tile_pool(name="codes", bufs=4))
         out_pool = ctx.enter_context(tc.tile_pool(name="out", bufs=3))
         psum_scores = ctx.enter_context(tc.psum_pool(name="psum_scores", bufs=SCORE_BANKS))
         psum_turn = ctx.enter_context(tc.psum_pool(name="psum_turn", bufs=3))
@@ -231,10 +231,11 @@ def tile_causalshapedattention_pa_kernel(tc, q, k, v, alpha, beta, gamma, out):
 
         def regroup_v(g, engine):
             v_grouped[g] = wide.tile([P, C, PACK], BF16, tag="wide", name="v_grouped", align_bytes=64)
-            for c in range(0, C, P):
+            width = P if engine is nc.gpsimd else C
+            for c in range(0, C, width):
                 engine.tensor_scalar(
-                    out=v_grouped[g][:, c : c + P, :],
-                    in0=v_raw[:, g, :, c : c + P].rearrange("p t c -> p c t"),
+                    out=v_grouped[g][:, c : c + width, :],
+                    in0=v_raw[:, g, :, c : c + width].rearrange("p t c -> p c t"),
                     scalar1=1.0,
                     scalar2=0.0,
                     op0=ALU.mult,
@@ -362,10 +363,10 @@ def tile_causalshapedattention_pa_kernel(tc, q, k, v, alpha, beta, gamma, out):
                 engine.tensor_scalar(
                     out=a_tiles[qi][:, 2 * h : 2 * h + 2, cols],
                     in0=exps[(qi, h)][:, :, cols],
-                    scalar1=gains[qi][:, h : h + 1],
-                    scalar2=mc_below[:, qi : qi + 1] if qi == TILES - 1 else 0.0,
+                    scalar1=(gains if qi == TILES - 1 else inv_sums)[qi][:, h : h + 1],
+                    scalar2=mc_below[:, qi : qi + 1] if qi == TILES - 1 else beta_f[:, 0:1],
                     op0=ALU.mult,
-                    op1=ALU.add,
+                    op1=ALU.add if qi == TILES - 1 else ALU.mult,
                 )
 
         def scale_diag(qi, h):
@@ -402,19 +403,26 @@ def tile_causalshapedattention_pa_kernel(tc, q, k, v, alpha, beta, gamma, out):
                     )
 
         def regroup(qi, g):
-            grouped_a[(qi, g)] = grouped_pool.tile(
-                [P, HEADS * P * PACK], BF16, tag="grouped", name="grouped", align_bytes=64
-            )
+            if g % 2 == 0:
+                grouped_a[(qi, g)] = grouped_pool.tile(
+                    [P, 2, HEADS * P * PACK], BF16, tag="grouped", name="grouped", align_bytes=64
+                )
             nc.scalar.copy(
-                out=grouped_a[(qi, g)][:].bitcast(F32).rearrange("p (h x u) -> p h x u", h=HEADS, u=2),
+                out=grouped_a[(qi, g - g % 2)][:, g % 2, :].bitcast(F32).rearrange("p (h x u) -> p h x u", h=HEADS, u=2),
                 in_=turned_a[(qi, g)][:].rearrange("p h u x -> p h x u"),
             )
 
         def quantise(qi, g):
-            codes = code_pool.tile([P, HEADS * P], U32, tag="codes", align_bytes=64)
-            scales = code_pool.tile([P, HEADS * P], U8, tag="scales", align_bytes=64)
-            nc.vector.quantize_mx(out=codes[:].bitcast(FP8X4), scales=scales[:], in_=grouped_a[(qi, g)][:])
-            a_codes[(qi, g)] = (codes, scales)
+            count = min(2, len(own_passes(qi)) - g)
+            codes = code_pool.tile([P, 2, HEADS * P], U32, tag="codes", align_bytes=64)
+            scales = code_pool.tile([P, 2, HEADS * P], U8, tag="scales", align_bytes=64)
+            nc.vector.quantize_mx(
+                out=codes[:, :count, :].rearrange("p n x -> p (n x)").bitcast(FP8X4),
+                scales=scales[:, :count, :].rearrange("p n x -> p (n x)"),
+                in_=grouped_a[(qi, g)][:, :count, :].rearrange("p n x -> p (n x)"),
+            )
+            for n in range(count):
+                a_codes[(qi, g + n)] = (codes[:, n, :], scales[:, n, :])
 
         def make_above(first):
             spread = psum_turn.tile([P, K_PASS, 2], BF16, tag="turn", name="spread")
@@ -494,7 +502,7 @@ def tile_causalshapedattention_pa_kernel(tc, q, k, v, alpha, beta, gamma, out):
             nc.sync.dma_start(out=rows, in_=o_sb[:])
 
         def cut_of(qi):
-            return qi // 3
+            return 2 * qi // 3
 
         def in_work(step):
             return ORDER[step] if 0 <= step < TILES else None
@@ -582,7 +590,7 @@ def tile_causalshapedattention_pa_kernel(tc, q, k, v, alpha, beta, gamma, out):
             if 3 <= step <= 2 + U_TILES // TILES_PER_PASS:
                 quantise_above((step - 3) * TILES_PER_PASS)
             if old is not None:
-                for g in own_passes(old):
+                for g in own_passes(old)[::2]:
                     quantise(old, g)
                 attend(old)
             multiply_ahead(known)
@@ -592,9 +600,13 @@ def tile_causalshapedattention_pa_kernel(tc, q, k, v, alpha, beta, gamma, out):
                 take_scalars()
             if mid is not None:
                 invert_sum(mid)
-                gain_of(mid, nc.vector if step <= 1 or mid == ORDER[-1] else nc.gpsimd)
+                on_vector = step <= 1 or mid == ORDER[-1]
+                if on_vector or mid == TILES - 1:
+                    gain_of(mid, nc.vector if on_vector else nc.gpsimd)
                 if step > 1:
                     scale_low(mid, 0, nc.gpsimd, slice(0, mid * TILE_COLS))
+                    if mid not in gains:
+                        gain_of(mid, nc.gpsimd)
                     scale_low(mid, 1, nc.gpsimd, slice(0, cut_of(mid) * TILE_COLS))
             early = new is not None and new >= TILES_PER_PASS
             if old is not None and early:

@@ -124,6 +124,10 @@ def tile_causalshapedattention_pa_kernel(tc, q, k, v, alpha, beta, gamma, out):
         def in_halves(square):
             return square.rearrange("p (u m e) -> p u m e", u=2, e=2)
 
+        ident_scaled_bf = keep.tile([P, P], BF16)
+        nc.vector.tensor_scalar(
+            out=ident_scaled_bf[:], in0=ident_bf[:], scalar1=1.0 / 16.0, scalar2=None, op0=ALU.mult
+        )
         ident_halves_bf = keep.tile([P, P], BF16)
         nc.vector.tensor_copy(out=in_halves(ident_halves_bf[:]), in_=natural(ident_bf[:]))
         above_halves = keep.tile([P, P], F32)
@@ -202,7 +206,7 @@ def tile_causalshapedattention_pa_kernel(tc, q, k, v, alpha, beta, gamma, out):
                 nc.tensor.matmul(
                     out=turned[:, b, :],
                     lhsT=q_sb[:, t, b * P : (b + 1) * P],
-                    rhs=ident_bf[:],
+                    rhs=ident_scaled_bf[:],
                     start=True,
                     stop=True,
                 )
@@ -297,6 +301,17 @@ def tile_causalshapedattention_pa_kernel(tc, q, k, v, alpha, beta, gamma, out):
                 )
 
         def drain_scores(qi, h, g):
+            if qi < TILES_PER_PASS:
+                exps[(qi, h)] = score_pool.tile([P, 2, HALF], F32, tag="e", name="e")
+                row_mins[(qi, h)] = stats.tile([P, 1], F32, tag="row_min", name="row_min")
+                nc.vector.tensor_reduce(
+                    out=row_mins[(qi, h)][:],
+                    in_=score_banks[(qi, h, g)][:, :, : (qi + 1) * TILE_COLS],
+                    axis=AXIS.XY,
+                    op=ALU.max,
+                    negate=True,
+                )
+                return
             if g == 0:
                 exps[(qi, h)] = score_pool.tile([P, 2, HALF], F32, tag="e", name="e")
                 pass_mins[(qi, h)] = stats.tile([P, PASSES], F32, tag="pass_min", name="pass_min")
@@ -305,7 +320,7 @@ def tile_causalshapedattention_pa_kernel(tc, q, k, v, alpha, beta, gamma, out):
             nc.vector.tensor_scalar(
                 out=exps[(qi, h)][:, :, first : first + width],
                 in0=score_banks[(qi, h, g)][:, :, :width],
-                scalar1=-1.0 / 16.0,
+                scalar1=-1.0,
                 scalar2=pass_mins[(qi, h)][:, g - 1 : g] if g == 1 and not needs_row_min(qi) else None,
                 op0=ALU.mult,
                 op1=ALU.min,
@@ -316,6 +331,8 @@ def tile_causalshapedattention_pa_kernel(tc, q, k, v, alpha, beta, gamma, out):
             return len(own_passes(qi)) > 2
 
         def row_min(qi, h):
+            if qi < TILES_PER_PASS:
+                return
             if not needs_row_min(qi):
                 last_pass = qi // TILES_PER_PASS
                 row_mins[(qi, h)] = pass_mins[(qi, h)][:, last_pass : last_pass + 1]
@@ -332,12 +349,13 @@ def tile_causalshapedattention_pa_kernel(tc, q, k, v, alpha, beta, gamma, out):
             if h == 0:
                 row_sums[qi] = stats.tile([P, HEADS], F32, tag="row_sum", name="row_sum")
             seen = (qi + 1) * TILE_COLS
+            one_pass = qi < TILES_PER_PASS
             nc.scalar.activation(
                 out=exps[(qi, h)][:, :, :seen],
-                in_=exps[(qi, h)][:, :, :seen],
+                in_=(score_banks[(qi, h, 0)] if one_pass else exps[(qi, h)])[:, :, :seen],
                 func=ACT.Exp,
                 bias=row_mins[(qi, h)][:],
-                scale=-1.0,
+                scale=1.0 if one_pass else -1.0,
                 accum_out=row_sums[qi][:, h : h + 1],
             )
 
@@ -531,24 +549,26 @@ def tile_causalshapedattention_pa_kernel(tc, q, k, v, alpha, beta, gamma, out):
         waiting_q = ORDER[2:]
 
         def turn_inputs(step):
-            if step + 2 < PASSES:
-                turn_keys(step + 2)
             for j in range(min(1 if step < 2 else 2, len(waiting_q))):
                 turn_q(waiting_q.pop(0))
+            if step + 2 < PASSES:
+                turn_keys(step + 2)
 
         def work_scores():
             drains = banks_of(new)
             for i in range(len(drains)):
                 drain_scores(*drains[i])
+                if new < TILES_PER_PASS:
+                    exponent(new, i)
                 progress["drained"] += 1
                 multiply_ahead(known)
                 turn_some(1)
-                if i == (len(drains) // 2 if needs_row_min(new) else len(drains) - 2):
+                if new >= TILES_PER_PASS and i == (len(drains) // 2 if needs_row_min(new) else len(drains) - 2):
                     row_min(new, 0)
                     exponent(new, 0)
             if step > 0 and mid is not None:
                 diag_addend(mid)
-            if new is not None:
+            if new is not None and new >= TILES_PER_PASS:
                 row_min(new, 1)
                 exponent(new, 1)
 
@@ -587,8 +607,6 @@ def tile_causalshapedattention_pa_kernel(tc, q, k, v, alpha, beta, gamma, out):
             if step == 3:
                 quantise_v(2)
                 quantise_v(3)
-            if 3 <= step <= 2 + U_TILES // TILES_PER_PASS:
-                quantise_above((step - 3) * TILES_PER_PASS)
             if old is not None:
                 for g in own_passes(old)[::2]:
                     quantise(old, g)
@@ -630,3 +648,5 @@ def tile_causalshapedattention_pa_kernel(tc, q, k, v, alpha, beta, gamma, out):
             if step == 1:
                 regroup_v(2, nc.vector)
                 regroup_v(3, nc.vector)
+            if 2 <= step <= 1 + U_TILES // TILES_PER_PASS:
+                quantise_above((step - 2) * TILES_PER_PASS)

@@ -28,10 +28,18 @@ TILE_COLS = P // 2
 PASS_COLS = K_PASS // 2
 D_BLOCKS = C // P
 MASKED = -1.0e30
+CONST_TILES = TILES - TILES_PER_PASS
+
+WARM_MATMULS = 3
+LATE_ADDENDS = 3
+
+SCALAR_STEP = 16
+
 SCORE_BANKS = 4
+TURN_BANKS = 3
+
 ORDER = [3, 7, 11, 15, 14, 13, 12, 10, 9, 8, 6, 5, 4, 2, 1, 0]
-OUT_IN_TURN = ORDER[-3::2]
-U_TILES = TILES - TILES_PER_PASS
+OUT_IN_TURN_BANK = ORDER[-3::2]
 
 FLOPS = 2 * 2 * T * T * D * HEADS
 
@@ -46,7 +54,7 @@ def tile_causalshapedattention_pa_kernel(tc, q, k, v, alpha, beta, gamma, out):
     with ExitStack() as ctx:
         ctx.enter_context(tc.manual_schedule())
         keep = ctx.enter_context(tc.tile_pool(name="keep", bufs=1))
-        wide = ctx.enter_context(tc.tile_pool(name="wide", bufs=7))
+        wide = ctx.enter_context(tc.tile_pool(name="wide", bufs=2 * PASSES))
         stats = ctx.enter_context(tc.tile_pool(name="stats", bufs=6))
         score_pool = ctx.enter_context(tc.tile_pool(name="scores", bufs=6))
         a_pool = ctx.enter_context(tc.tile_pool(name="a", bufs=3))
@@ -54,40 +62,46 @@ def tile_causalshapedattention_pa_kernel(tc, q, k, v, alpha, beta, gamma, out):
         code_pool = ctx.enter_context(tc.tile_pool(name="codes", bufs=4))
         out_pool = ctx.enter_context(tc.tile_pool(name="out", bufs=3))
         psum_scores = ctx.enter_context(tc.psum_pool(name="psum_scores", bufs=SCORE_BANKS))
-        psum_turn = ctx.enter_context(tc.psum_pool(name="psum_turn", bufs=3))
+        psum_turn = ctx.enter_context(tc.psum_pool(name="psum_turn", bufs=TURN_BANKS))
         psum_out = ctx.enter_context(tc.psum_pool(name="psum_out", bufs=1))
 
         q_sb = keep.tile([P, TILES, C], BF16)
-        k_sb = keep.tile([P, TILES, C], BF16)
+        k_sb = [
+            wide.tile([P, TILES_PER_PASS, C], BF16, tag="wide", name="k_pass", align_bytes=64)
+            for g in range(PASSES)
+        ]
         q_view = q_rows.rearrange("(t p) c -> p t c", p=P)
         k_view = k_rows.rearrange("(t p) c -> p t c", p=P)
         v_raw = keep.tile([P, PASSES, PACK, C], BF16)
         v_view = v_rows.rearrange("(g p t) c -> p g (t c)", p=P, t=PACK)
-        alpha_bf = keep.tile([P, 1], BF16)
-        beta_bf = keep.tile([P, 1], BF16)
-        gamma_bf = keep.tile([P, 1], BF16)
+        scalars_bf = keep.tile([P, 3 * SCALAR_STEP], BF16)
+        nc.gpsimd.memset(scalars_bf[:], 0.0)
 
         def load_q(tiles):
             nc.sync.dma_start(out=q_sb[:, tiles, :], in_=q_view[:, tiles, :])
 
         def load_k(g):
-            tiles = slice(g * TILES_PER_PASS, (g + 1) * TILES_PER_PASS)
-            nc.sync.dma_start(out=k_sb[:, tiles, :], in_=k_view[:, tiles, :])
+            for first in range(g * TILES_PER_PASS, (g + 1) * TILES_PER_PASS, 2):
+                nc.sync.dma_start(
+                    out=k_sb[g][:, first % TILES_PER_PASS : first % TILES_PER_PASS + 2, :],
+                    in_=k_view[:, first : first + 2, :],
+                )
 
         def load_v(g):
             nc.sync.dma_start(out=v_raw[:, g].rearrange("p t c -> p (t c)"), in_=v_view[:, g, :])
 
-        load_q(slice(3, 4))
+        for i, scalar in enumerate((alpha, beta, gamma)):
+            nc.scalar.dma_start(
+                out=scalars_bf[0:1, i * SCALAR_STEP : i * SCALAR_STEP + 1], in_=scalar.partition_broadcast(1)
+            )
+        load_q(slice(ORDER[0], ORDER[0] + 1))
         load_k(0)
-        load_q(slice(7, 8))
+        load_q(slice(ORDER[1], ORDER[1] + 1))
         load_k(1)
-        nc.sync.dma_start(out=gamma_bf[:], in_=gamma.partition_broadcast(P))
-        nc.sync.dma_start(out=alpha_bf[:], in_=alpha.partition_broadcast(P))
-        nc.sync.dma_start(out=beta_bf[:], in_=beta.partition_broadcast(P))
         load_v(0)
         load_v(1)
         load_k(2)
-        load_q(slice(11, TILES, 4))
+        load_q(slice(ORDER[2], TILES, TILES_PER_PASS))
         load_k(3)
         load_v(2)
         load_v(3)
@@ -98,13 +112,19 @@ def tile_causalshapedattention_pa_kernel(tc, q, k, v, alpha, beta, gamma, out):
         nc.vector.memset(warm[:], 0.0)
         nc.scalar.activation(out=warm[:], in_=warm[:], func=ACT.Exp)
 
+        zeros_bf = keep.tile([P, K_PASS], BF16)
+        nc.vector.memset(zeros_bf[:], 0.0)
+        warm_ps = psum_out.tile([P, K_PASS], F32, tag="o", name="warm_ps")
+        for i in range(WARM_MATMULS):
+            nc.tensor.matmul(out=warm_ps[:], lhsT=zeros_bf[:, :P], rhs=zeros_bf[:], start=True, stop=True)
+
         ident_bf = keep.tile([P, P], BF16)
         make_identity(nc, ident_bf[:])
-        above = keep.tile([P, P], F32)
-        nc.gpsimd.memset(above[:], 0.0)
+        upper = keep.tile([P, P], F32)
+        nc.gpsimd.memset(upper[:], 0.0)
         nc.gpsimd.affine_select(
-            out=above[:],
-            in_=above[:],
+            out=upper[:],
+            in_=upper[:],
             compare_op=ALU.is_ge,
             fill=1.0,
             base=0,
@@ -130,13 +150,13 @@ def tile_causalshapedattention_pa_kernel(tc, q, k, v, alpha, beta, gamma, out):
         )
         ident_halves_bf = keep.tile([P, P], BF16)
         nc.vector.tensor_copy(out=in_halves(ident_halves_bf[:]), in_=natural(ident_bf[:]))
-        above_halves = keep.tile([P, P], F32)
-        nc.vector.tensor_copy(out=in_halves(above_halves[:]), in_=natural(above[:]))
+        upper_halves = keep.tile([P, P], F32)
+        nc.vector.tensor_copy(out=in_halves(upper_halves[:]), in_=natural(upper[:]))
         left = keep.tile([P, TILES], F32)
         nc.vector.tensor_copy(out=left[:], in_=left_i[:])
         masked_bf = keep.tile([P, P], BF16)
         nc.vector.tensor_scalar(
-            out=masked_bf[:], in0=above_halves[:], scalar1=MASKED, scalar2=None, op0=ALU.mult
+            out=masked_bf[:], in0=upper_halves[:], scalar1=MASKED, scalar2=None, op0=ALU.mult
         )
         is_last = keep.tile([P, TILES], F32)
         nc.vector.tensor_scalar(
@@ -149,81 +169,62 @@ def tile_causalshapedattention_pa_kernel(tc, q, k, v, alpha, beta, gamma, out):
         share = keep.tile([P, TILES], F32)
         nc.vector.reciprocal(out=share[:], in_=count[:])
 
-        alpha_f = keep.tile([P, 1], F32)
-        beta_f = keep.tile([P, 1], F32)
-        gamma_f = keep.tile([P, 1], F32)
+        scalars = keep.tile([P, 3], F32)
+        alpha_f = scalars[:, 0:1]
+        beta_f = scalars[:, 1:2]
+        gamma_f = scalars[:, 2:3]
         mc_above = keep.tile([P, TILES], F32)
         mc_above_bf = keep.tile([P, TILES], BF16)
         mc_below = keep.tile([P, TILES], F32)
         alpha_eye = keep.tile([P, P], F32)
+        diag_all = keep.tile([P, TILES, P], F32)
 
         def take_scalars():
-            nc.vector.tensor_copy(out=gamma_f[:], in_=gamma_bf[:])
-            nc.vector.tensor_copy(out=alpha_f[:], in_=alpha_bf[:])
-            nc.vector.tensor_copy(out=beta_f[:], in_=beta_bf[:])
+            spread = psum_out.tile([P, 3, SCALAR_STEP], F32, tag="o", name="scalars_ps")
+            nc.tensor.matmul(
+                out=spread[:].rearrange("p n x -> p (n x)"),
+                lhsT=ones_bf[:, 0, :P],
+                rhs=scalars_bf[:],
+                start=True,
+                stop=True,
+            )
+            nc.vector.tensor_copy(out=scalars[:], in_=spread[:, :, 0])
             nc.vector.tensor_scalar(
                 out=mc_above[:],
                 in0=share[:],
-                scalar1=gamma_f[:, 0:1],
+                scalar1=gamma_f,
                 scalar2=-1.0,
                 op0=ALU.mult,
                 op1=ALU.mult,
             )
             nc.vector.tensor_scalar(
-                out=alpha_eye[:], in0=ident_halves_bf[:], scalar1=alpha_f[:, 0:1], scalar2=None, op0=ALU.mult
+                out=alpha_eye[:], in0=ident_halves_bf[:], scalar1=alpha_f, scalar2=None, op0=ALU.mult
             )
-            nc.vector.tensor_copy(out=mc_above_bf[:], in_=mc_above[:])
-            nc.vector.tensor_tensor(out=mc_below[:], in0=mc_above[:], in1=is_last[:], op=ALU.mult)
-
-        diag_adds = {}
-
-        def diag_addend(qi):
-            diag_adds[qi] = stats.tile([P, P], F32, tag="diag_add", name="diag_add")
-            nc.vector.scalar_tensor_tensor(
-                out=diag_adds[qi][:],
-                in0=above_halves[:],
-                scalar=mc_above[:, qi : qi + 1],
-                in1=alpha_eye[:],
-                op0=ALU.mult,
-                op1=ALU.add,
-            )
-            if qi == TILES - 1:
-                nc.vector.tensor_scalar(
-                    out=diag_adds[qi][:],
-                    in0=diag_adds[qi][:],
-                    scalar1=1.0,
-                    scalar2=mc_below[:, qi : qi + 1],
-                    op0=ALU.mult,
-                    op1=ALU.add,
-                )
 
         q_t = keep.tile([P, D_BLOCKS, T], BF16)
         k_t = keep.tile([P, D_BLOCKS, 2, HALF], BF16)
 
-        def turn_q(t, copy_out=nc.scalar.copy):
-            turned = psum_turn.tile([P, D_BLOCKS, P], BF16, tag="turn")
+        def turn_blocks(tokens, identity):
+            turned = psum_turn.tile([P, D_BLOCKS, P], BF16, tag="turn", name="turned")
             for b in range(D_BLOCKS):
                 nc.tensor.matmul(
                     out=turned[:, b, :],
-                    lhsT=q_sb[:, t, b * P : (b + 1) * P],
-                    rhs=ident_scaled_bf[:],
+                    lhsT=tokens[:, b * P : (b + 1) * P],
+                    rhs=identity[:],
                     start=True,
                     stop=True,
                 )
-            copy_out(out=q_t[:, :, t * P : (t + 1) * P], in_=turned[:])
+            return turned
+
+        def turn_q(t):
+            turned = turn_blocks(q_sb[:, t, :], ident_scaled_bf)
+            nc.scalar.copy(out=q_t[:, :, t * P : (t + 1) * P], in_=turned[:])
 
         def turn_keys(g):
             for t in range(g * TILES_PER_PASS, (g + 1) * TILES_PER_PASS):
-                turned = psum_turn.tile([P, D_BLOCKS, P], BF16, tag="turn")
-                for b in range(D_BLOCKS):
-                    nc.tensor.matmul(
-                        out=turned[:, b, :],
-                        lhsT=k_sb[:, t, b * P : (b + 1) * P],
-                        rhs=ident_halves_bf[:],
-                        start=True,
-                        stop=True,
-                    )
-                copy_out = nc.scalar.copy if t % 2 == 0 or t >= 2 * TILES_PER_PASS else nc.vector.tensor_copy
+                turned = turn_blocks(k_sb[g][:, t % TILES_PER_PASS, :], ident_halves_bf)
+                on_vector = g == 1 and t % 2 == 1
+                copy_out = nc.vector.tensor_copy if on_vector else nc.scalar.copy
                 copy_out(
                     out=k_t[:, :, :, t * TILE_COLS : (t + 1) * TILE_COLS],
                     in_=turned[:].rearrange("p b (u x) -> p b u x", u=2),
@@ -233,9 +234,8 @@ def tile_causalshapedattention_pa_kernel(tc, q, k, v, alpha, beta, gamma, out):
         v_scales = keep.tile([P, PASSES, C], U8, align_bytes=64)
         v_grouped = {}
 
-        def regroup_v(g, engine):
+        def regroup_v(g, engine, width):
             v_grouped[g] = wide.tile([P, C, PACK], BF16, tag="wide", name="v_grouped", align_bytes=64)
-            width = P if engine is nc.gpsimd else C
             for c in range(0, C, width):
                 engine.tensor_scalar(
                     out=v_grouped[g][:, c : c + width, :],
@@ -253,47 +253,53 @@ def tile_causalshapedattention_pa_kernel(tc, q, k, v, alpha, beta, gamma, out):
                 in_=v_grouped[g][:].rearrange("p c t -> p (c t)"),
             )
 
+        score_banks = {}
         exps = {}
         pass_mins = {}
-        row_mins = {}
+        score_mins = {}
         row_sums = {}
-        gains = {}
         inv_sums = {}
-        above_grouped = {}
+        gains = {}
+        diag_adds = {}
         a_tiles = {}
         turned_a = {}
         grouped_a = {}
         a_codes = {}
+        above_grouped = {}
         o_tiles = {}
-        above_codes = keep.tile([P, U_TILES * P], U32, align_bytes=64)
-        above_scales = keep.tile([P, U_TILES * P], U8, align_bytes=64)
+        above_codes = keep.tile([P, CONST_TILES * P], U32, align_bytes=64)
+        above_scales = keep.tile([P, CONST_TILES * P], U8, align_bytes=64)
 
         def own_passes(qi):
             return range(qi // TILES_PER_PASS + 1)
 
-        score_banks = {}
+        def above_passes(qi):
+            return range(qi // TILES_PER_PASS + 1, PASSES)
+
+        def one_pass(qi):
+            return len(own_passes(qi)) == 1
+
+        def many_passes(qi):
+            return len(own_passes(qi)) > 2
 
         def multiply_scores(qi, h, g):
             last_pass = qi // TILES_PER_PASS
             before = (qi % TILES_PER_PASS) * TILE_COLS
-            q_cols = slice(qi * P, (qi + 1) * P)
-            s_ps = psum_scores.tile([P, 2, PASS_COLS], F32, tag="scores", name="s_ps")
-            score_banks[(qi, h, g)] = s_ps
+            width = before + TILE_COLS if g == last_pass else PASS_COLS
             first = g * PASS_COLS
-            width = PASS_COLS
-            if g == last_pass:
-                width = before + TILE_COLS
+            bank = psum_scores.tile([P, 2, PASS_COLS], F32, tag="scores", name="bank")
+            score_banks[(qi, h, g)] = bank
             for b in range(2):
                 nc.tensor.matmul(
-                    out=s_ps[:, :, :width],
-                    lhsT=q_t[:, 2 * h + b, q_cols],
+                    out=bank[:, :, :width],
+                    lhsT=q_t[:, 2 * h + b, qi * P : (qi + 1) * P],
                     rhs=k_t[:, 2 * h + b, :, first : first + width],
                     start=(b == 0),
                     stop=(b == 1 and g < last_pass),
                 )
             if g == last_pass:
                 nc.tensor.matmul(
-                    out=s_ps[:, :, before : before + TILE_COLS],
+                    out=bank[:, :, before : before + TILE_COLS],
                     lhsT=ident_bf[:],
                     rhs=masked_bf[:].rearrange("p (u x) -> p u x", u=2),
                     start=False,
@@ -301,61 +307,57 @@ def tile_causalshapedattention_pa_kernel(tc, q, k, v, alpha, beta, gamma, out):
                 )
 
         def drain_scores(qi, h, g):
-            if qi < TILES_PER_PASS:
+            width = min(PASS_COLS, (qi + 1) * TILE_COLS - g * PASS_COLS)
+            bank = score_banks[(qi, h, g)]
+            if g == 0:
                 exps[(qi, h)] = score_pool.tile([P, 2, HALF], F32, tag="e", name="e")
-                row_mins[(qi, h)] = stats.tile([P, 1], F32, tag="row_min", name="row_min")
+            if one_pass(qi):
+                score_mins[(qi, h)] = stats.tile([P, 1], F32, tag="score_min", name="score_min")
                 nc.vector.tensor_reduce(
-                    out=row_mins[(qi, h)][:],
-                    in_=score_banks[(qi, h, g)][:, :, : (qi + 1) * TILE_COLS],
+                    out=score_mins[(qi, h)][:],
+                    in_=bank[:, :, :width],
                     axis=AXIS.XY,
                     op=ALU.max,
                     negate=True,
                 )
                 return
             if g == 0:
-                exps[(qi, h)] = score_pool.tile([P, 2, HALF], F32, tag="e", name="e")
                 pass_mins[(qi, h)] = stats.tile([P, PASSES], F32, tag="pass_min", name="pass_min")
-            first = g * PASS_COLS
-            width = min(PASS_COLS, (qi + 1) * TILE_COLS - first)
+            chained = g == 1 and not many_passes(qi)
             nc.vector.tensor_scalar(
-                out=exps[(qi, h)][:, :, first : first + width],
-                in0=score_banks[(qi, h, g)][:, :, :width],
+                out=exps[(qi, h)][:, :, g * PASS_COLS : g * PASS_COLS + width],
+                in0=bank[:, :, :width],
                 scalar1=-1.0,
-                scalar2=pass_mins[(qi, h)][:, g - 1 : g] if g == 1 and not needs_row_min(qi) else None,
+                scalar2=pass_mins[(qi, h)][:, g - 1 : g] if chained else None,
                 op0=ALU.mult,
                 op1=ALU.min,
                 accum_out=pass_mins[(qi, h)][:, g : g + 1],
             )
 
-        def needs_row_min(qi):
-            return len(own_passes(qi)) > 2
-
         def row_min(qi, h):
-            if qi < TILES_PER_PASS:
-                return
-            if not needs_row_min(qi):
-                last_pass = qi // TILES_PER_PASS
-                row_mins[(qi, h)] = pass_mins[(qi, h)][:, last_pass : last_pass + 1]
-                return
-            row_mins[(qi, h)] = stats.tile([P, 1], F32, tag="row_min", name="row_min")
-            nc.vector.tensor_reduce(
-                out=row_mins[(qi, h)][:],
-                in_=pass_mins[(qi, h)][:, : qi // TILES_PER_PASS + 1],
-                axis=AXIS.X,
-                op=ALU.min,
-            )
+            count_passes = len(own_passes(qi))
+            if many_passes(qi):
+                score_mins[(qi, h)] = stats.tile([P, 1], F32, tag="score_min", name="score_min")
+                nc.vector.tensor_reduce(
+                    out=score_mins[(qi, h)][:],
+                    in_=pass_mins[(qi, h)][:, :count_passes],
+                    axis=AXIS.X,
+                    op=ALU.min,
+                )
+            else:
+                score_mins[(qi, h)] = pass_mins[(qi, h)][:, count_passes - 1 : count_passes]
 
         def exponent(qi, h):
             if h == 0:
                 row_sums[qi] = stats.tile([P, HEADS], F32, tag="row_sum", name="row_sum")
             seen = (qi + 1) * TILE_COLS
-            one_pass = qi < TILES_PER_PASS
+            source = score_banks[(qi, h, 0)] if one_pass(qi) else exps[(qi, h)]
             nc.scalar.activation(
                 out=exps[(qi, h)][:, :, :seen],
-                in_=(score_banks[(qi, h, 0)] if one_pass else exps[(qi, h)])[:, :, :seen],
+                in_=source[:, :, :seen],
                 func=ACT.Exp,
-                bias=row_mins[(qi, h)][:],
-                scale=1.0 if one_pass else -1.0,
+                bias=score_mins[(qi, h)][:],
+                scale=1.0 if one_pass(qi) else -1.0,
                 accum_out=row_sums[qi][:, h : h + 1],
             )
 
@@ -368,23 +370,44 @@ def tile_causalshapedattention_pa_kernel(tc, q, k, v, alpha, beta, gamma, out):
             engine.tensor_scalar(
                 out=gains[qi][:],
                 in0=inv_sums[qi][:],
-                scalar1=beta_f[:, 0:1],
+                scalar1=beta_f,
                 scalar2=0.0,
                 op0=ALU.mult,
                 op1=ALU.add,
             )
 
-        def scale_low(qi, h, engine, cols):
-            if qi not in a_tiles:
-                a_tiles[qi] = a_pool.tile([P, 2 * HEADS, HALF], BF16, tag="a", name="a", align_bytes=64)
-            if cols.stop > cols.start:
-                engine.tensor_scalar(
-                    out=a_tiles[qi][:, 2 * h : 2 * h + 2, cols],
-                    in0=exps[(qi, h)][:, :, cols],
-                    scalar1=(gains if qi == TILES - 1 else inv_sums)[qi][:, h : h + 1],
-                    scalar2=mc_below[:, qi : qi + 1] if qi == TILES - 1 else beta_f[:, 0:1],
+        def scale_low(qi, h, engine, first, end):
+            if end == first:
+                return
+            cols = slice(first * TILE_COLS, end * TILE_COLS)
+            last_tile = qi == TILES - 1
+            engine.tensor_scalar(
+                out=a_tiles[qi][:, 2 * h : 2 * h + 2, cols],
+                in0=exps[(qi, h)][:, :, cols],
+                scalar1=(gains if last_tile else inv_sums)[qi][:, h : h + 1],
+                scalar2=mc_below[:, qi : qi + 1] if last_tile else beta_f,
+                op0=ALU.mult,
+                op1=ALU.add if last_tile else ALU.mult,
+            )
+
+        def diag_addend(qi):
+            diag_adds[qi] = diag_all[:, qi, :]
+            nc.vector.scalar_tensor_tensor(
+                out=diag_adds[qi],
+                in0=upper_halves[:],
+                scalar=mc_above[:, qi : qi + 1],
+                in1=alpha_eye[:],
+                op0=ALU.mult,
+                op1=ALU.add,
+            )
+            if qi == TILES - 1:
+                nc.vector.tensor_scalar(
+                    out=diag_adds[qi],
+                    in0=diag_adds[qi],
+                    scalar1=1.0,
+                    scalar2=mc_below[:, qi : qi + 1],
                     op0=ALU.mult,
-                    op1=ALU.add if qi == TILES - 1 else ALU.mult,
+                    op1=ALU.add,
                 )
 
         def scale_diag(qi, h):
@@ -393,14 +416,14 @@ def tile_causalshapedattention_pa_kernel(tc, q, k, v, alpha, beta, gamma, out):
                 out=a_tiles[qi][:, 2 * h : 2 * h + 2, block],
                 in0=exps[(qi, h)][:, :, block],
                 scalar=gains[qi][:, h : h + 1],
-                in1=diag_adds[qi][:].rearrange("p (u x) -> p u x", u=2),
+                in1=diag_adds[qi].rearrange("p (u x) -> p u x", u=2),
                 op0=ALU.mult,
                 op1=ALU.add,
             )
 
         def fill_above(qi):
             seen = (qi + 1) * TILE_COLS
-            end = (qi // TILES_PER_PASS + 1) * PASS_COLS
+            end = len(own_passes(qi)) * PASS_COLS
             if end > seen:
                 nc.vector.tensor_scalar(
                     out=a_tiles[qi][:, :, seen:end],
@@ -411,7 +434,7 @@ def tile_causalshapedattention_pa_kernel(tc, q, k, v, alpha, beta, gamma, out):
                     op1=ALU.add,
                 )
 
-        def turn(qi, g):
+        def turn_a(qi, g):
             a_words = a_tiles[qi][:].bitcast(F32)
             turned_a[(qi, g)] = psum_turn.tile([P, HEADS, 2, P], F32, tag="turn", name="turned_a")
             for h in range(HEADS):
@@ -420,27 +443,28 @@ def tile_causalshapedattention_pa_kernel(tc, q, k, v, alpha, beta, gamma, out):
                         turned_a[(qi, g)][:, h, u, :], a_words[:, 2 * h + u, g * P : (g + 1) * P], ident_f[:]
                     )
 
-        def regroup(qi, g):
-            if g % 2 == 0:
-                grouped_a[(qi, g)] = grouped_pool.tile(
+        def regroup_a(qi, g):
+            pair = g - g % 2
+            if g == pair:
+                grouped_a[(qi, pair)] = grouped_pool.tile(
                     [P, 2, HEADS * P * PACK], BF16, tag="grouped", name="grouped", align_bytes=64
                 )
             nc.scalar.copy(
-                out=grouped_a[(qi, g - g % 2)][:, g % 2, :].bitcast(F32).rearrange("p (h x u) -> p h x u", h=HEADS, u=2),
+                out=grouped_a[(qi, pair)][:, g - pair, :].bitcast(F32).rearrange("p (h x u) -> p h x u", h=HEADS, u=2),
                 in_=turned_a[(qi, g)][:].rearrange("p h u x -> p h x u"),
             )
 
-        def quantise(qi, g):
-            count = min(2, len(own_passes(qi)) - g)
+        def quantise_a(qi, pair):
+            size = min(2, len(own_passes(qi)) - pair)
             codes = code_pool.tile([P, 2, HEADS * P], U32, tag="codes", align_bytes=64)
             scales = code_pool.tile([P, 2, HEADS * P], U8, tag="scales", align_bytes=64)
             nc.vector.quantize_mx(
-                out=codes[:, :count, :].rearrange("p n x -> p (n x)").bitcast(FP8X4),
-                scales=scales[:, :count, :].rearrange("p n x -> p (n x)"),
-                in_=grouped_a[(qi, g)][:, :count, :].rearrange("p n x -> p (n x)"),
+                out=codes[:, :size, :].rearrange("p n x -> p (n x)").bitcast(FP8X4),
+                scales=scales[:, :size, :].rearrange("p n x -> p (n x)"),
+                in_=grouped_a[(qi, pair)][:, :size, :].rearrange("p n x -> p (n x)"),
             )
-            for n in range(count):
-                a_codes[(qi, g + n)] = (codes[:, n, :], scales[:, n, :])
+            for n in range(size):
+                a_codes[(qi, pair + n)] = (codes[:, n, :], scales[:, n, :])
 
         def make_above(first):
             spread = psum_turn.tile([P, K_PASS, 2], BF16, tag="turn", name="spread")
@@ -453,8 +477,9 @@ def tile_causalshapedattention_pa_kernel(tc, q, k, v, alpha, beta, gamma, out):
                     stop=True,
                 )
             above_grouped[first] = wide.tile([P, K_PASS, PACK], BF16, tag="wide", name="above_grouped", align_bytes=64)
+            words = above_grouped[first][:].rearrange("p x t -> p (x t)").bitcast(F32)
             nc.scalar.copy(
-                out=above_grouped[first][:].rearrange("p x t -> p (x t)").bitcast(F32).rearrange("p (x u) -> p x u", u=2),
+                out=words.rearrange("p (x u) -> p x u", u=2),
                 in_=spread[:].rearrange("p x u -> p (x u)").bitcast(F32).unsqueeze(2).to_broadcast([P, K_PASS, 2]),
             )
 
@@ -467,45 +492,57 @@ def tile_causalshapedattention_pa_kernel(tc, q, k, v, alpha, beta, gamma, out):
             )
 
         def attend(qi):
-            above_passes = list(range(qi // TILES_PER_PASS + 1, PASSES))
-            passes = above_passes + list(own_passes(qi))
+            above = above_passes(qi)
+            above_lhs = (
+                above_codes[:, qi * P : (qi + 1) * P].bitcast(FP8X4) if above else None,
+                above_scales[:, qi * P : (qi + 1) * P] if above else None,
+            )
 
-            def multiply(h, g, out):
-                if g in above_passes:
-                    lhs_codes = above_codes[:, qi * P : (qi + 1) * P]
-                    lhs_scales = above_scales[:, qi * P : (qi + 1) * P]
-                else:
-                    codes, scales = a_codes[(qi, g)]
-                    lhs_codes = codes[:, h * P : (h + 1) * P]
-                    lhs_scales = scales[:, h * P : (h + 1) * P]
+            def multiply(o_ps, lhs, g, channels, start, stop):
                 nc.tensor.matmul_mx(
-                    out=out,
-                    lhsT=lhs_codes.bitcast(FP8X4),
-                    lhsT_scale=lhs_scales,
-                    rhs=v_codes[:, g, h * D : (h + 1) * D].bitcast(FP8X4),
-                    rhs_scale=v_scales[:, g, h * D : (h + 1) * D],
-                    start=(g == passes[0]),
-                    stop=(g == passes[-1]),
+                    out=o_ps,
+                    lhsT=lhs[0],
+                    lhsT_scale=lhs[1],
+                    rhs=v_codes[:, g, channels].bitcast(FP8X4),
+                    rhs_scale=v_scales[:, g, channels],
+                    start=start,
+                    stop=stop,
                 )
 
+            def own_lhs(g, h):
+                codes, scales = a_codes[(qi, g)]
+                queries = slice(h * P, (h + 1) * P)
+                return codes[:, queries].bitcast(FP8X4), scales[:, queries]
+
+            def head(h):
+                return slice(h * D, (h + 1) * D)
+
+            own = own_passes(qi)
             if qi == ORDER[-1]:
-                halves = [
+                o_tiles[qi] = [
                     psum_turn.tile([P, D], F32, tag="turn", name="o_first"),
                     psum_turn.tile([P, D], F32, tag="turn", name="o_second"),
                 ]
-                for group in (above_passes, own_passes(qi)):
-                    for h in range(HEADS):
-                        for g in group:
-                            multiply(h, g, halves[h][:])
-                o_tiles[qi] = halves
+                for h in range(HEADS):
+                    for g in above:
+                        multiply(o_tiles[qi][h][:], above_lhs, g, head(h), g == above[0], False)
+                for h in range(HEADS):
+                    for g in own:
+                        multiply(o_tiles[qi][h][:], own_lhs(g, h), g, head(h), False, g == own[-1])
                 return
-            if qi in OUT_IN_TURN:
+            if qi in OUT_IN_TURN_BANK:
                 o_tiles[qi] = psum_turn.tile([P, HEADS, D], F32, tag="turn", name="o_ps")
             else:
                 o_tiles[qi] = psum_out.tile([P, HEADS, D], F32, tag="o", name="o_ps")
+            for g in above:
+                multiply(
+                    o_tiles[qi][:].rearrange("p h d -> p (h d)"), above_lhs, g, slice(0, C), g == above[0], False
+                )
             for h in range(HEADS):
-                for g in passes:
-                    multiply(h, g, o_tiles[qi][:, h, :])
+                for g in own:
+                    start = not above and g == own[0]
+                    stop = g == own[-1] and (not above or h == HEADS - 1)
+                    multiply(o_tiles[qi][:, h, :], own_lhs(g, h), g, head(h), start, stop)
 
         def store(qi):
             o_sb = out_pool.tile([P, C], F32, tag="o_sb")
@@ -519,134 +556,143 @@ def tile_causalshapedattention_pa_kernel(tc, q, k, v, alpha, beta, gamma, out):
             nc.scalar.copy(out=o_sb[:], in_=o_tiles[qi][:].rearrange("p h d -> p (h d)"))
             nc.sync.dma_start(out=rows, in_=o_sb[:])
 
-        def cut_of(qi):
-            return 2 * qi // 3
-
         def in_work(step):
             return ORDER[step] if 0 <= step < TILES else None
 
         def banks_of(qi):
             if qi is None:
                 return []
-            if needs_row_min(qi):
+            if many_passes(qi):
                 return [(qi, h, g) for h in range(HEADS) for g in own_passes(qi)]
             return [(qi, h, g) for g in own_passes(qi) for h in range(HEADS)]
 
         all_banks = [bank for qi in ORDER for bank in banks_of(qi)]
-        progress = {"multiplied": 0, "drained": 0}
+        progress = {"multiplied": 0, "drained": 0, "known": 0}
 
-        def multiply_ahead(limit):
-            while progress["multiplied"] < min(limit, progress["drained"] + SCORE_BANKS):
+        def multiply_ahead():
+            while progress["multiplied"] < min(progress["known"], progress["drained"] + SCORE_BANKS):
                 multiply_scores(*all_banks[progress["multiplied"]])
                 progress["multiplied"] += 1
 
-        regroup_v(0, nc.gpsimd)
-        regroup_v(1, nc.gpsimd)
-        turn_q(ORDER[0])
-        turn_keys(0)
-        known = len(banks_of(ORDER[0]))
-        multiply_ahead(known)
-        waiting_q = ORDER[2:]
+        turns_left = []
+
+        def turn_some(count):
+            for turn in turns_left[:count]:
+                turn_a(*turn)
+                regroup_a(*turn)
+            turns_left[:count] = []
+
+        queries_left = ORDER[2:]
 
         def turn_inputs(step):
-            for j in range(min(1 if step < 2 else 2, len(waiting_q))):
-                turn_q(waiting_q.pop(0))
+            count = 1 if step == 0 else 2
+            for qi in queries_left[:count]:
+                turn_q(qi)
+            queries_left[:count] = []
             if step + 2 < PASSES:
                 turn_keys(step + 2)
 
-        def work_scores():
-            drains = banks_of(new)
-            for i in range(len(drains)):
-                drain_scores(*drains[i])
-                if new < TILES_PER_PASS:
-                    exponent(new, i)
+        def work_first_scores(qi):
+            for bank in banks_of(qi):
+                drain_scores(*bank)
                 progress["drained"] += 1
-                multiply_ahead(known)
+            turn_keys(1)
+            for h in range(HEADS):
+                exponent(qi, h)
+
+        def work_scores(qi, mid):
+            banks = banks_of(qi)
+            first_ready = len(banks) // 2 if qi is not None and many_passes(qi) else len(banks) - 2
+            for i, bank in enumerate(banks):
+                drain_scores(*bank)
+                if one_pass(qi):
+                    exponent(qi, i)
+                progress["drained"] += 1
+                multiply_ahead()
                 turn_some(1)
-                if new >= TILES_PER_PASS and i == (len(drains) // 2 if needs_row_min(new) else len(drains) - 2):
-                    row_min(new, 0)
-                    exponent(new, 0)
-            if step > 0 and mid is not None:
-                diag_addend(mid)
-            if new is not None and new >= TILES_PER_PASS:
-                row_min(new, 1)
-                exponent(new, 1)
+                if not one_pass(qi) and i == first_ready:
+                    row_min(qi, 0)
+                    exponent(qi, 0)
+            if mid is not None:
+                if mid in ORDER[-LATE_ADDENDS:]:
+                    diag_addend(mid)
+                fill_above(mid)
+            if qi is not None and not one_pass(qi):
+                row_min(qi, 1)
+                exponent(qi, 1)
 
-        pending_turns = []
-
-        def turn_some(count):
-            for i in range(min(count, len(pending_turns))):
-                qi, g = pending_turns.pop(0)
-                turn(qi, g)
-                regroup(qi, g)
-
+        regroup_v(0, nc.gpsimd, P)
+        regroup_v(1, nc.gpsimd, P)
+        take_scalars()
+        turn_q(ORDER[0])
+        nc.vector.tensor_tensor(out=mc_below[:], in0=mc_above[:], in1=is_last[:], op=ALU.mult)
+        for qi in ORDER[:-LATE_ADDENDS]:
+            diag_addend(qi)
+        nc.vector.tensor_copy(out=mc_above_bf[:], in_=mc_above[:])
+        turn_keys(0)
+        progress["known"] = len(banks_of(ORDER[0]))
+        multiply_ahead()
         for step in range(TILES + 3):
             new = in_work(step)
             mid = in_work(step - 1)
             ripe = in_work(step - 2)
             old = in_work(step - 3)
-            known += len(banks_of(in_work(step + 1)))
+            progress["known"] += len(banks_of(in_work(step + 1)))
             if step == 0:
                 turn_q(ORDER[1])
-                for h, g in [(h, g) for h in range(HEADS) for g in own_passes(new)]:
-                    drain_scores(new, h, g)
-                    progress["drained"] += 1
-                for h in range(HEADS):
-                    row_min(new, h)
-                turn_keys(1)
-                for h in range(HEADS):
-                    exponent(new, h)
+                work_first_scores(new)
 
-            pending_turns.extend([] if ripe is None else [(ripe, g) for g in own_passes(ripe)])
-            turn_some(3)
-            for first in {2: [0, 4], 3: [8]}.get(step, []):
-                make_above(first)
+            if ripe is not None:
+                turns_left.extend((ripe, g) for g in own_passes(ripe))
+            turn_some(TURN_BANKS)
             if step == 2:
+                make_above(0)
+                make_above(TILES_PER_PASS)
                 quantise_v(0)
                 quantise_v(1)
             if step == 3:
+                make_above(2 * TILES_PER_PASS)
                 quantise_v(2)
                 quantise_v(3)
             if old is not None:
-                for g in own_passes(old)[::2]:
-                    quantise(old, g)
+                for pair in own_passes(old)[::2]:
+                    quantise_a(old, pair)
                 attend(old)
-            multiply_ahead(known)
-            if not (step == 1):
+            multiply_ahead()
+            if step != 1:
                 turn_inputs(step)
-            if step == 0:
-                take_scalars()
+
             if mid is not None:
+                a_tiles[mid] = a_pool.tile([P, 2 * HEADS, HALF], BF16, tag="a", name="a", align_bytes=64)
                 invert_sum(mid)
-                on_vector = step <= 1 or mid == ORDER[-1]
+                on_vector = step == 1 or mid == ORDER[-1]
                 if on_vector or mid == TILES - 1:
                     gain_of(mid, nc.vector if on_vector else nc.gpsimd)
+                cut = 0
                 if step > 1:
-                    scale_low(mid, 0, nc.gpsimd, slice(0, mid * TILE_COLS))
+                    cut = 2 * mid // 3
+                    scale_low(mid, 0, nc.gpsimd, 0, mid)
                     if mid not in gains:
                         gain_of(mid, nc.gpsimd)
-                    scale_low(mid, 1, nc.gpsimd, slice(0, cut_of(mid) * TILE_COLS))
-            early = new is not None and new >= TILES_PER_PASS
-            if old is not None and early:
+                    scale_low(mid, 1, nc.gpsimd, 0, cut)
+            store_early = new is not None and not one_pass(new)
+            if old is not None and store_early:
                 store(old)
             if step > 0:
-                work_scores()
+                work_scores(new, mid)
             if step == 1:
                 turn_inputs(step)
-            if old is not None and not early:
+            if old is not None and not store_early:
                 store(old)
             turn_some(PASSES)
             if mid is not None:
-                if step <= 1:
-                    scale_low(mid, 0, nc.vector, slice(0, mid * TILE_COLS))
-                    scale_low(mid, 1, nc.vector, slice(0, mid * TILE_COLS))
-                else:
-                    scale_low(mid, 1, nc.vector, slice(cut_of(mid) * TILE_COLS, mid * TILE_COLS))
-                fill_above(mid)
+                if step == 1:
+                    scale_low(mid, 0, nc.vector, 0, mid)
+                scale_low(mid, 1, nc.vector, cut, mid)
                 for h in range(HEADS):
                     scale_diag(mid, h)
             if step == 1:
-                regroup_v(2, nc.vector)
-                regroup_v(3, nc.vector)
-            if 2 <= step <= 1 + U_TILES // TILES_PER_PASS:
+                regroup_v(2, nc.vector, C)
+                regroup_v(3, nc.vector, C)
+            if 2 <= step < 2 + PASSES - 1:
                 quantise_above((step - 2) * TILES_PER_PASS)

from contextlib import ExitStack

import concourse.mybir as mybir
from concourse.masks import make_identity

F32 = mybir.dt.float32
BF16 = mybir.dt.bfloat16
I32 = mybir.dt.int32
U32 = mybir.dt.uint32
U8 = mybir.dt.uint8
FP8X4 = mybir.dt.float8_e4m3fn_x4
ALU = mybir.AluOpType
ACT = mybir.ActivationFunctionType
AXIS = mybir.AxisListType

P = 128
T = 2048
HEADS = 2
D = 256
C = HEADS * D
TILES = T // P
PACK = 4
K_PASS = P * PACK
PASSES = T // K_PASS
TILES_PER_PASS = K_PASS // P
HALF = T // 2
TILE_COLS = P // 2
PASS_COLS = K_PASS // 2
D_BLOCKS = C // P
MASKED = -1.0e30
CONST_TILES = TILES - TILES_PER_PASS

WARM_MATMULS = 3
LATE_ADDENDS = 3

SCALAR_STEP = 16

SCORE_BANKS = 4
TURN_BANKS = 3

ORDER = [3, 7, 11, 15, 14, 13, 12, 10, 9, 8, 6, 5, 4, 2, 1, 0]
OUT_IN_TURN_BANK = ORDER[-3::2]

FLOPS = 2 * 2 * T * T * D * HEADS


def tile_causalshapedattention_pa_kernel(tc, q, k, v, alpha, beta, gamma, out):
    nc = tc.nc
    q_rows = q.flatten_outer_dims()
    k_rows = k.flatten_outer_dims()
    v_rows = v.flatten_outer_dims()
    out_rows = out.flatten_outer_dims()

    with ExitStack() as ctx:
        ctx.enter_context(tc.manual_schedule())
        keep = ctx.enter_context(tc.tile_pool(name="keep", bufs=1))
        wide = ctx.enter_context(tc.tile_pool(name="wide", bufs=2 * PASSES))
        stats = ctx.enter_context(tc.tile_pool(name="stats", bufs=6))
        score_pool = ctx.enter_context(tc.tile_pool(name="scores", bufs=6))
        a_pool = ctx.enter_context(tc.tile_pool(name="a", bufs=3))
        grouped_pool = ctx.enter_context(tc.tile_pool(name="grouped", bufs=4))
        code_pool = ctx.enter_context(tc.tile_pool(name="codes", bufs=4))
        out_pool = ctx.enter_context(tc.tile_pool(name="out", bufs=3))
        psum_scores = ctx.enter_context(tc.psum_pool(name="psum_scores", bufs=SCORE_BANKS))
        psum_turn = ctx.enter_context(tc.psum_pool(name="psum_turn", bufs=TURN_BANKS))
        psum_out = ctx.enter_context(tc.psum_pool(name="psum_out", bufs=1))

        q_sb = keep.tile([P, TILES, C], BF16)
        k_sb = [
            wide.tile([P, TILES_PER_PASS, C], BF16, tag="wide", name="k_pass", align_bytes=64)
            for g in range(PASSES)
        ]
        q_view = q_rows.rearrange("(t p) c -> p t c", p=P)
        k_view = k_rows.rearrange("(t p) c -> p t c", p=P)
        v_raw = keep.tile([P, PASSES, PACK, C], BF16)
        v_view = v_rows.rearrange("(g p t) c -> p g (t c)", p=P, t=PACK)
        scalars_bf = keep.tile([P, 3 * SCALAR_STEP], BF16)
        nc.gpsimd.memset(scalars_bf[:], 0.0)

        def load_q(tiles):
            nc.sync.dma_start(out=q_sb[:, tiles, :], in_=q_view[:, tiles, :])

        def load_k(g):
            for first in range(g * TILES_PER_PASS, (g + 1) * TILES_PER_PASS, 2):
                nc.sync.dma_start(
                    out=k_sb[g][:, first % TILES_PER_PASS : first % TILES_PER_PASS + 2, :],
                    in_=k_view[:, first : first + 2, :],
                )

        def load_v(g):
            nc.sync.dma_start(out=v_raw[:, g].rearrange("p t c -> p (t c)"), in_=v_view[:, g, :])

        for i, scalar in enumerate((alpha, beta, gamma)):
            nc.scalar.dma_start(
                out=scalars_bf[0:1, i * SCALAR_STEP : i * SCALAR_STEP + 1], in_=scalar.partition_broadcast(1)
            )
        load_q(slice(ORDER[0], ORDER[0] + 1))
        load_k(0)
        load_q(slice(ORDER[1], ORDER[1] + 1))
        load_k(1)
        load_v(0)
        load_v(1)
        load_k(2)
        load_q(slice(ORDER[2], TILES, TILES_PER_PASS))
        load_k(3)
        load_v(2)
        load_v(3)
        for g in range(PASSES - 1, -1, -1):
            load_q(slice(g * TILES_PER_PASS, (g + 1) * TILES_PER_PASS - 1))

        warm = keep.tile([P, 1], F32)
        nc.vector.memset(warm[:], 0.0)
        nc.scalar.activation(out=warm[:], in_=warm[:], func=ACT.Exp)

        zeros_bf = keep.tile([P, K_PASS], BF16)
        nc.vector.memset(zeros_bf[:], 0.0)
        warm_ps = psum_out.tile([P, K_PASS], F32, tag="o", name="warm_ps")
        for i in range(WARM_MATMULS):
            nc.tensor.matmul(out=warm_ps[:], lhsT=zeros_bf[:, :P], rhs=zeros_bf[:], start=True, stop=True)

        ident_bf = keep.tile([P, P], BF16)
        make_identity(nc, ident_bf[:])
        upper = keep.tile([P, P], F32)
        nc.gpsimd.memset(upper[:], 0.0)
        nc.gpsimd.affine_select(
            out=upper[:],
            in_=upper[:],
            compare_op=ALU.is_ge,
            fill=1.0,
            base=0,
            pattern=[[-1, P]],
            channel_multiplier=1,
        )
        ident_f = keep.tile([P, P], F32)
        make_identity(nc, ident_f[:])
        left_i = keep.tile([P, TILES], I32)
        nc.gpsimd.iota(left_i[:], pattern=[[-P, TILES]], base=T - 1, channel_multiplier=-1)
        ones_bf = keep.tile([P, 2 * HEADS, PASS_COLS - TILE_COLS], BF16)
        nc.gpsimd.memset(ones_bf[:], 1.0)

        def natural(square):
            return square.rearrange("p (m u e) -> p u m e", u=2, e=2)

        def in_halves(square):
            return square.rearrange("p (u m e) -> p u m e", u=2, e=2)

        ident_scaled_bf = keep.tile([P, P], BF16)
        nc.vector.tensor_scalar(
            out=ident_scaled_bf[:], in0=ident_bf[:], scalar1=1.0 / 16.0, scalar2=None, op0=ALU.mult
        )
        ident_halves_bf = keep.tile([P, P], BF16)
        nc.vector.tensor_copy(out=in_halves(ident_halves_bf[:]), in_=natural(ident_bf[:]))
        upper_halves = keep.tile([P, P], F32)
        nc.vector.tensor_copy(out=in_halves(upper_halves[:]), in_=natural(upper[:]))
        left = keep.tile([P, TILES], F32)
        nc.vector.tensor_copy(out=left[:], in_=left_i[:])
        masked_bf = keep.tile([P, P], BF16)
        nc.vector.tensor_scalar(
            out=masked_bf[:], in0=upper_halves[:], scalar1=MASKED, scalar2=None, op0=ALU.mult
        )
        is_last = keep.tile([P, TILES], F32)
        nc.vector.tensor_scalar(
            out=is_last[:], in0=left[:], scalar1=0.0, scalar2=None, op0=ALU.is_equal
        )
        count = keep.tile([P, TILES], F32)
        nc.vector.scalar_tensor_tensor(
            out=count[:], in0=is_last[:], scalar=float(T), in1=left[:], op0=ALU.mult, op1=ALU.add
        )
        share = keep.tile([P, TILES], F32)
        nc.vector.reciprocal(out=share[:], in_=count[:])

        scalars = keep.tile([P, 3], F32)
        alpha_f = scalars[:, 0:1]
        beta_f = scalars[:, 1:2]
        gamma_f = scalars[:, 2:3]
        mc_above = keep.tile([P, TILES], F32)
        mc_above_bf = keep.tile([P, TILES], BF16)
        mc_below = keep.tile([P, TILES], F32)
        alpha_eye = keep.tile([P, P], F32)
        diag_all = keep.tile([P, TILES, P], F32)

        def take_scalars():
            spread = psum_out.tile([P, 3, SCALAR_STEP], F32, tag="o", name="scalars_ps")
            nc.tensor.matmul(
                out=spread[:].rearrange("p n x -> p (n x)"),
                lhsT=ones_bf[:, 0, :P],
                rhs=scalars_bf[:],
                start=True,
                stop=True,
            )
            nc.vector.tensor_copy(out=scalars[:], in_=spread[:, :, 0])
            nc.vector.tensor_scalar(
                out=mc_above[:],
                in0=share[:],
                scalar1=gamma_f,
                scalar2=-1.0,
                op0=ALU.mult,
                op1=ALU.mult,
            )
            nc.vector.tensor_scalar(
                out=alpha_eye[:], in0=ident_halves_bf[:], scalar1=alpha_f, scalar2=None, op0=ALU.mult
            )

        q_t = keep.tile([P, D_BLOCKS, T], BF16)
        k_t = keep.tile([P, D_BLOCKS, 2, HALF], BF16)

        def turn_blocks(tokens, identity):
            turned = psum_turn.tile([P, D_BLOCKS, P], BF16, tag="turn", name="turned")
            for b in range(D_BLOCKS):
                nc.tensor.matmul(
                    out=turned[:, b, :],
                    lhsT=tokens[:, b * P : (b + 1) * P],
                    rhs=identity[:],
                    start=True,
                    stop=True,
                )
            return turned

        def turn_q(t):
            turned = turn_blocks(q_sb[:, t, :], ident_scaled_bf)
            nc.scalar.copy(out=q_t[:, :, t * P : (t + 1) * P], in_=turned[:])

        def turn_keys(g):
            for t in range(g * TILES_PER_PASS, (g + 1) * TILES_PER_PASS):
                turned = turn_blocks(k_sb[g][:, t % TILES_PER_PASS, :], ident_halves_bf)
                on_vector = g == 1 and t % 2 == 1
                copy_out = nc.vector.tensor_copy if on_vector else nc.scalar.copy
                copy_out(
                    out=k_t[:, :, :, t * TILE_COLS : (t + 1) * TILE_COLS],
                    in_=turned[:].rearrange("p b (u x) -> p b u x", u=2),
                )

        v_codes = keep.tile([P, PASSES, C], U32, align_bytes=64)
        v_scales = keep.tile([P, PASSES, C], U8, align_bytes=64)
        v_grouped = {}

        def regroup_v(g, engine, width):
            v_grouped[g] = wide.tile([P, C, PACK], BF16, tag="wide", name="v_grouped", align_bytes=64)
            for c in range(0, C, width):
                engine.tensor_scalar(
                    out=v_grouped[g][:, c : c + width, :],
                    in0=v_raw[:, g, :, c : c + width].rearrange("p t c -> p c t"),
                    scalar1=1.0,
                    scalar2=0.0,
                    op0=ALU.mult,
                    op1=ALU.add,
                )

        def quantise_v(g):
            nc.vector.quantize_mx(
                out=v_codes[:, g, :].bitcast(FP8X4),
                scales=v_scales[:, g, :],
                in_=v_grouped[g][:].rearrange("p c t -> p (c t)"),
            )

        score_banks = {}
        exps = {}
        pass_mins = {}
        score_mins = {}
        row_sums = {}
        inv_sums = {}
        gains = {}
        diag_adds = {}
        a_tiles = {}
        turned_a = {}
        grouped_a = {}
        a_codes = {}
        above_grouped = {}
        o_tiles = {}
        above_codes = keep.tile([P, CONST_TILES * P], U32, align_bytes=64)
        above_scales = keep.tile([P, CONST_TILES * P], U8, align_bytes=64)

        def own_passes(qi):
            return range(qi // TILES_PER_PASS + 1)

        def above_passes(qi):
            return range(qi // TILES_PER_PASS + 1, PASSES)

        def one_pass(qi):
            return len(own_passes(qi)) == 1

        def many_passes(qi):
            return len(own_passes(qi)) > 2

        def multiply_scores(qi, h, g):
            last_pass = qi // TILES_PER_PASS
            before = (qi % TILES_PER_PASS) * TILE_COLS
            width = before + TILE_COLS if g == last_pass else PASS_COLS
            first = g * PASS_COLS
            bank = psum_scores.tile([P, 2, PASS_COLS], F32, tag="scores", name="bank")
            score_banks[(qi, h, g)] = bank
            for b in range(2):
                nc.tensor.matmul(
                    out=bank[:, :, :width],
                    lhsT=q_t[:, 2 * h + b, qi * P : (qi + 1) * P],
                    rhs=k_t[:, 2 * h + b, :, first : first + width],
                    start=(b == 0),
                    stop=(b == 1 and g < last_pass),
                )
            if g == last_pass:
                nc.tensor.matmul(
                    out=bank[:, :, before : before + TILE_COLS],
                    lhsT=ident_bf[:],
                    rhs=masked_bf[:].rearrange("p (u x) -> p u x", u=2),
                    start=False,
                    stop=True,
                )

        def drain_scores(qi, h, g):
            width = min(PASS_COLS, (qi + 1) * TILE_COLS - g * PASS_COLS)
            bank = score_banks[(qi, h, g)]
            if g == 0:
                exps[(qi, h)] = score_pool.tile([P, 2, HALF], F32, tag="e", name="e")
            if one_pass(qi):
                score_mins[(qi, h)] = stats.tile([P, 1], F32, tag="score_min", name="score_min")
                nc.vector.tensor_reduce(
                    out=score_mins[(qi, h)][:],
                    in_=bank[:, :, :width],
                    axis=AXIS.XY,
                    op=ALU.max,
                    negate=True,
                )
                return
            if g == 0:
                pass_mins[(qi, h)] = stats.tile([P, PASSES], F32, tag="pass_min", name="pass_min")
            chained = g == 1 and not many_passes(qi)
            nc.vector.tensor_scalar(
                out=exps[(qi, h)][:, :, g * PASS_COLS : g * PASS_COLS + width],
                in0=bank[:, :, :width],
                scalar1=-1.0,
                scalar2=pass_mins[(qi, h)][:, g - 1 : g] if chained else None,
                op0=ALU.mult,
                op1=ALU.min,
                accum_out=pass_mins[(qi, h)][:, g : g + 1],
            )

        def row_min(qi, h):
            count_passes = len(own_passes(qi))
            if many_passes(qi):
                score_mins[(qi, h)] = stats.tile([P, 1], F32, tag="score_min", name="score_min")
                nc.vector.tensor_reduce(
                    out=score_mins[(qi, h)][:],
                    in_=pass_mins[(qi, h)][:, :count_passes],
                    axis=AXIS.X,
                    op=ALU.min,
                )
            else:
                score_mins[(qi, h)] = pass_mins[(qi, h)][:, count_passes - 1 : count_passes]

        def exponent(qi, h):
            if h == 0:
                row_sums[qi] = stats.tile([P, HEADS], F32, tag="row_sum", name="row_sum")
            seen = (qi + 1) * TILE_COLS
            source = score_banks[(qi, h, 0)] if one_pass(qi) else exps[(qi, h)]
            nc.scalar.activation(
                out=exps[(qi, h)][:, :, :seen],
                in_=source[:, :, :seen],
                func=ACT.Exp,
                bias=score_mins[(qi, h)][:],
                scale=1.0 if one_pass(qi) else -1.0,
                accum_out=row_sums[qi][:, h : h + 1],
            )

        def invert_sum(qi):
            inv_sums[qi] = stats.tile([P, HEADS], F32, tag="inv_sum", name="inv_sum")
            nc.vector.reciprocal(out=inv_sums[qi][:], in_=row_sums[qi][:])

        def gain_of(qi, engine):
            gains[qi] = stats.tile([P, HEADS], F32, tag="gain", name="gain")
            engine.tensor_scalar(
                out=gains[qi][:],
                in0=inv_sums[qi][:],
                scalar1=beta_f,
                scalar2=0.0,
                op0=ALU.mult,
                op1=ALU.add,
            )

        def scale_low(qi, h, engine, first, end):
            if end == first:
                return
            cols = slice(first * TILE_COLS, end * TILE_COLS)
            last_tile = qi == TILES - 1
            engine.tensor_scalar(
                out=a_tiles[qi][:, 2 * h : 2 * h + 2, cols],
                in0=exps[(qi, h)][:, :, cols],
                scalar1=(gains if last_tile else inv_sums)[qi][:, h : h + 1],
                scalar2=mc_below[:, qi : qi + 1] if last_tile else beta_f,
                op0=ALU.mult,
                op1=ALU.add if last_tile else ALU.mult,
            )

        def diag_addend(qi):
            diag_adds[qi] = diag_all[:, qi, :]
            nc.vector.scalar_tensor_tensor(
                out=diag_adds[qi],
                in0=upper_halves[:],
                scalar=mc_above[:, qi : qi + 1],
                in1=alpha_eye[:],
                op0=ALU.mult,
                op1=ALU.add,
            )
            if qi == TILES - 1:
                nc.vector.tensor_scalar(
                    out=diag_adds[qi],
                    in0=diag_adds[qi],
                    scalar1=1.0,
                    scalar2=mc_below[:, qi : qi + 1],
                    op0=ALU.mult,
                    op1=ALU.add,
                )

        def scale_diag(qi, h):
            block = slice(qi * TILE_COLS, (qi + 1) * TILE_COLS)
            nc.vector.scalar_tensor_tensor(
                out=a_tiles[qi][:, 2 * h : 2 * h + 2, block],
                in0=exps[(qi, h)][:, :, block],
                scalar=gains[qi][:, h : h + 1],
                in1=diag_adds[qi].rearrange("p (u x) -> p u x", u=2),
                op0=ALU.mult,
                op1=ALU.add,
            )

        def fill_above(qi):
            seen = (qi + 1) * TILE_COLS
            end = len(own_passes(qi)) * PASS_COLS
            if end > seen:
                nc.vector.tensor_scalar(
                    out=a_tiles[qi][:, :, seen:end],
                    in0=ones_bf[:, :, : end - seen],
                    scalar1=mc_above[:, qi : qi + 1],
                    scalar2=0.0,
                    op0=ALU.mult,
                    op1=ALU.add,
                )

        def turn_a(qi, g):
            a_words = a_tiles[qi][:].bitcast(F32)
            turned_a[(qi, g)] = psum_turn.tile([P, HEADS, 2, P], F32, tag="turn", name="turned_a")
            for h in range(HEADS):
                for u in range(2):
                    nc.tensor.transpose(
                        turned_a[(qi, g)][:, h, u, :], a_words[:, 2 * h + u, g * P : (g + 1) * P], ident_f[:]
                    )

        def regroup_a(qi, g):
            pair = g - g % 2
            if g == pair:
                grouped_a[(qi, pair)] = grouped_pool.tile(
                    [P, 2, HEADS * P * PACK], BF16, tag="grouped", name="grouped", align_bytes=64
                )
            nc.scalar.copy(
                out=grouped_a[(qi, pair)][:, g - pair, :].bitcast(F32).rearrange("p (h x u) -> p h x u", h=HEADS, u=2),
                in_=turned_a[(qi, g)][:].rearrange("p h u x -> p h x u"),
            )

        def quantise_a(qi, pair):
            size = min(2, len(own_passes(qi)) - pair)
            codes = code_pool.tile([P, 2, HEADS * P], U32, tag="codes", align_bytes=64)
            scales = code_pool.tile([P, 2, HEADS * P], U8, tag="scales", align_bytes=64)
            nc.vector.quantize_mx(
                out=codes[:, :size, :].rearrange("p n x -> p (n x)").bitcast(FP8X4),
                scales=scales[:, :size, :].rearrange("p n x -> p (n x)"),
                in_=grouped_a[(qi, pair)][:, :size, :].rearrange("p n x -> p (n x)"),
            )
            for n in range(size):
                a_codes[(qi, pair + n)] = (codes[:, n, :], scales[:, n, :])

        def make_above(first):
            spread = psum_turn.tile([P, K_PASS, 2], BF16, tag="turn", name="spread")
            for j in range(TILES_PER_PASS):
                nc.tensor.matmul(
                    out=spread[:, j * P : (j + 1) * P, :],
                    lhsT=mc_above_bf[:, first + j : first + j + 1].to_broadcast([P, P]),
                    rhs=ident_bf[:].unsqueeze(2).to_broadcast([P, P, 2]),
                    start=True,
                    stop=True,
                )
            above_grouped[first] = wide.tile([P, K_PASS, PACK], BF16, tag="wide", name="above_grouped", align_bytes=64)
            words = above_grouped[first][:].rearrange("p x t -> p (x t)").bitcast(F32)
            nc.scalar.copy(
                out=words.rearrange("p (x u) -> p x u", u=2),
                in_=spread[:].rearrange("p x u -> p (x u)").bitcast(F32).unsqueeze(2).to_broadcast([P, K_PASS, 2]),
            )

        def quantise_above(first):
            cols = slice(first * P, first * P + K_PASS)
            nc.vector.quantize_mx(
                out=above_codes[:, cols].bitcast(FP8X4),
                scales=above_scales[:, cols],
                in_=above_grouped[first][:].rearrange("p x t -> p (x t)"),
            )

        def attend(qi):
            above = above_passes(qi)
            above_lhs = (
                above_codes[:, qi * P : (qi + 1) * P].bitcast(FP8X4) if above else None,
                above_scales[:, qi * P : (qi + 1) * P] if above else None,
            )

            def multiply(o_ps, lhs, g, channels, start, stop):
                nc.tensor.matmul_mx(
                    out=o_ps,
                    lhsT=lhs[0],
                    lhsT_scale=lhs[1],
                    rhs=v_codes[:, g, channels].bitcast(FP8X4),
                    rhs_scale=v_scales[:, g, channels],
                    start=start,
                    stop=stop,
                )

            def own_lhs(g, h):
                codes, scales = a_codes[(qi, g)]
                queries = slice(h * P, (h + 1) * P)
                return codes[:, queries].bitcast(FP8X4), scales[:, queries]

            def head(h):
                return slice(h * D, (h + 1) * D)

            own = own_passes(qi)
            if qi == ORDER[-1]:
                o_tiles[qi] = [
                    psum_turn.tile([P, D], F32, tag="turn", name="o_first"),
                    psum_turn.tile([P, D], F32, tag="turn", name="o_second"),
                ]
                for h in range(HEADS):
                    for g in above:
                        multiply(o_tiles[qi][h][:], above_lhs, g, head(h), g == above[0], False)
                for h in range(HEADS):
                    for g in own:
                        multiply(o_tiles[qi][h][:], own_lhs(g, h), g, head(h), False, g == own[-1])
                return
            if qi in OUT_IN_TURN_BANK:
                o_tiles[qi] = psum_turn.tile([P, HEADS, D], F32, tag="turn", name="o_ps")
            else:
                o_tiles[qi] = psum_out.tile([P, HEADS, D], F32, tag="o", name="o_ps")
            for g in above:
                multiply(
                    o_tiles[qi][:].rearrange("p h d -> p (h d)"), above_lhs, g, slice(0, C), g == above[0], False
                )
            for h in range(HEADS):
                for g in own:
                    start = not above and g == own[0]
                    stop = g == own[-1] and (not above or h == HEADS - 1)
                    multiply(o_tiles[qi][:, h, :], own_lhs(g, h), g, head(h), start, stop)

        def store(qi):
            o_sb = out_pool.tile([P, C], F32, tag="o_sb")
            rows = out_rows[qi * P : (qi + 1) * P, :]
            if qi == ORDER[-1]:
                for h, copy_out in enumerate((nc.vector.tensor_copy, nc.scalar.copy)):
                    cols = slice(h * D, (h + 1) * D)
                    copy_out(out=o_sb[:, cols], in_=o_tiles[qi][h][:])
                    nc.sync.dma_start(out=rows[:, cols], in_=o_sb[:, cols])
                return
            nc.scalar.copy(out=o_sb[:], in_=o_tiles[qi][:].rearrange("p h d -> p (h d)"))
            nc.sync.dma_start(out=rows, in_=o_sb[:])

        def in_work(step):
            return ORDER[step] if 0 <= step < TILES else None

        def banks_of(qi):
            if qi is None:
                return []
            if many_passes(qi):
                return [(qi, h, g) for h in range(HEADS) for g in own_passes(qi)]
            return [(qi, h, g) for g in own_passes(qi) for h in range(HEADS)]

        all_banks = [bank for qi in ORDER for bank in banks_of(qi)]
        progress = {"multiplied": 0, "drained": 0, "known": 0}

        def multiply_ahead():
            while progress["multiplied"] < min(progress["known"], progress["drained"] + SCORE_BANKS):
                multiply_scores(*all_banks[progress["multiplied"]])
                progress["multiplied"] += 1

        turns_left = []

        def turn_some(count):
            for turn in turns_left[:count]:
                turn_a(*turn)
                regroup_a(*turn)
            turns_left[:count] = []

        queries_left = ORDER[2:]

        def turn_inputs(step):
            count = 1 if step == 0 else 2
            for qi in queries_left[:count]:
                turn_q(qi)
            queries_left[:count] = []
            if step + 2 < PASSES:
                turn_keys(step + 2)

        def work_first_scores(qi):
            for bank in banks_of(qi):
                drain_scores(*bank)
                progress["drained"] += 1
            turn_keys(1)
            for h in range(HEADS):
                exponent(qi, h)

        def work_scores(qi, mid):
            banks = banks_of(qi)
            first_ready = len(banks) // 2 if qi is not None and many_passes(qi) else len(banks) - 2
            for i, bank in enumerate(banks):
                drain_scores(*bank)
                if one_pass(qi):
                    exponent(qi, i)
                progress["drained"] += 1
                multiply_ahead()
                turn_some(1)
                if not one_pass(qi) and i == first_ready:
                    row_min(qi, 0)
                    exponent(qi, 0)
            if mid is not None:
                if mid in ORDER[-LATE_ADDENDS:]:
                    diag_addend(mid)
                fill_above(mid)
            if qi is not None and not one_pass(qi):
                row_min(qi, 1)
                exponent(qi, 1)

        regroup_v(0, nc.gpsimd, P)
        regroup_v(1, nc.gpsimd, P)
        take_scalars()
        turn_q(ORDER[0])
        nc.vector.tensor_tensor(out=mc_below[:], in0=mc_above[:], in1=is_last[:], op=ALU.mult)
        for qi in ORDER[:-LATE_ADDENDS]:
            diag_addend(qi)
        nc.vector.tensor_copy(out=mc_above_bf[:], in_=mc_above[:])
        turn_keys(0)
        progress["known"] = len(banks_of(ORDER[0]))
        multiply_ahead()
        for step in range(TILES + 3):
            new = in_work(step)
            mid = in_work(step - 1)
            ripe = in_work(step - 2)
            old = in_work(step - 3)
            progress["known"] += len(banks_of(in_work(step + 1)))
            if step == 0:
                turn_q(ORDER[1])
                work_first_scores(new)

            if ripe is not None:
                turns_left.extend((ripe, g) for g in own_passes(ripe))
            turn_some(TURN_BANKS)
            if step == 2:
                make_above(0)
                make_above(TILES_PER_PASS)
                quantise_v(0)
                quantise_v(1)
            if step == 3:
                make_above(2 * TILES_PER_PASS)
                quantise_v(2)
                quantise_v(3)
            if old is not None:
                for pair in own_passes(old)[::2]:
                    quantise_a(old, pair)
                attend(old)
            multiply_ahead()
            if step != 1:
                turn_inputs(step)

            if mid is not None:
                a_tiles[mid] = a_pool.tile([P, 2 * HEADS, HALF], BF16, tag="a", name="a", align_bytes=64)
                invert_sum(mid)
                on_vector = step == 1 or mid == ORDER[-1]
                if on_vector or mid == TILES - 1:
                    gain_of(mid, nc.vector if on_vector else nc.gpsimd)
                cut = 0
                if step > 1:
                    cut = 2 * mid // 3
                    scale_low(mid, 0, nc.gpsimd, 0, mid)
                    if mid not in gains:
                        gain_of(mid, nc.gpsimd)
                    scale_low(mid, 1, nc.gpsimd, 0, cut)
            store_early = new is not None and not one_pass(new)
            if old is not None and store_early:
                store(old)
            if step > 0:
                work_scores(new, mid)
            if step == 1:
                turn_inputs(step)
            if old is not None and not store_early:
                store(old)
            turn_some(PASSES)
            if mid is not None:
                if step == 1:
                    scale_low(mid, 0, nc.vector, 0, mid)
                scale_low(mid, 1, nc.vector, cut, mid)
                for h in range(HEADS):
                    scale_diag(mid, h)
            if step == 1:
                regroup_v(2, nc.vector, C)
                regroup_v(3, nc.vector, C)
            if 2 <= step < 2 + PASSES - 1:
                quantise_above((step - 2) * TILES_PER_PASS)
